import numpy as np
import ml_dtypes


def mxq(x, axis, fmt="e4m3"):
    dtype, down = {"e4m3": (ml_dtypes.float8_e4m3fn, 7), "e5m2": (ml_dtypes.float8_e5m2, 14)}[fmt]
    v = np.moveaxis(np.asarray(x, np.float32).astype(ml_dtypes.bfloat16).astype(np.float64), axis, -1)
    blocks = v.reshape(v.shape[:-1] + (-1, 32))
    amax = np.abs(blocks).max(-1, keepdims=True)
    byte = np.maximum(np.where(amax > 0, np.frexp(amax)[1] - 1 + 127, 0) - down, 1)
    scale = np.exp2(byte - 127.0)
    codes = (blocks / scale).astype(np.float32).astype(dtype).astype(np.float64)
    return np.moveaxis((codes * scale).reshape(v.shape), -1, axis)


WIDE = False


def mx_kscale(k):
    if not WIDE:
        return np.ones(k)
    levels = np.array([10, -10, 5, -5, 0])
    a = np.random.permutation(np.resize(levels, k // 512 * 4)).reshape(k // 512, 4)
    idx = np.arange(k)
    return np.exp2(a[idx // 512, idx % 128 // 32])


BF16 = ml_dtypes.bfloat16


def bf(x):
    return np.asarray(x, np.float32).astype(BF16)


def f64(x):
    return np.asarray(x).astype(np.float64)


B, N, D, H, Z = 8, 512, 1024, 1, 512
NEG_INF = -1.0e9
CW = 1.3 / Z ** 0.25


def setup_inputs():
    s, t = mx_kscale(D), mx_kscale(Z)
    g1 = np.random.standard_normal((H, Z, D))
    g2 = np.random.standard_normal((H, Z, D))
    return {"x": bf(np.random.standard_normal((B, N, D)) * s),
            "wk": bf((0.25 * g1 + g2) * CW / np.sqrt(D) / s / t[None, :, None]),
            "wq": bf(g1 * CW / np.sqrt(D) / s * t[None, :, None]),
            "betas": bf(1.5 + 0.15 * np.random.standard_normal(H))}


def reference(x, wk, wq, betas):
    beta = f64(betas)
    xq = mxq(f64(x).reshape(B * N, D), 1, "e4m3")
    k = (xq @ mxq(f64(wk).reshape(H * Z, D), 1, "e4m3").T).reshape(B, N, H, Z).transpose(0, 2, 1, 3)
    q = (xq @ mxq(f64(wq).reshape(H * Z, D), 1, "e4m3").T).reshape(B, N, H, Z).transpose(0, 2, 1, 3)
    a = beta[None, :, None, None] * (mxq(q, 3, "e4m3") @ mxq(k, 3, "e4m3").transpose(0, 1, 3, 2))
    a = np.where(np.eye(N, dtype=bool)[None, None], NEG_INF, a)
    top = a.max(-1, keepdims=True)
    lse = top[..., 0] + np.log(np.exp(a - top).sum(-1))
    return -(lse / beta[None, :, None])

@@ -1,0 +1,296 @@
+from contextlib import ExitStack
+
+import concourse.mybir as mybir
+from concourse.masks import make_identity
+
+F32 = mybir.dt.float32
+BF16 = mybir.dt.bfloat16
+U32 = mybir.dt.uint32
+U8 = mybir.dt.uint8
+FP8X4 = mybir.dt.float8_e4m3fn_x4
+ALU = mybir.AluOpType
+ACT = mybir.ActivationFunctionType
+
+NB = 8
+N = 512
+D = 1024
+Z = 512
+P = 128
+NT = N // P
+FLOPS = 2 * NB * N * D * 2 * Z + 2 * NB * N * N * Z
+MASKED = 1.0e9
+LOWEST = 3.0e38
+
+OTHERS = (
+    ((128, 256), (384, 128)),
+    ((256, 256), (0, 128)),
+    ((0, 256), (384, 128)),
+    ((0, 256), (256, 128)),
+)
+
+
+def tile_multiheadenergyattention_pa_t_kernel(tc, x, wk, wq, betas, out):
+    nc = tc.nc
+    with ExitStack() as ctx:
+        keep = ctx.enter_context(tc.tile_pool(name="keep", bufs=1))
+        ring2 = ctx.enter_context(tc.tile_pool(name="ring2", bufs=2))
+        ring3 = ctx.enter_context(tc.tile_pool(name="ring3", bufs=3))
+        ring6 = ctx.enter_context(tc.tile_pool(name="ring6", bufs=6))
+        psum = ctx.enter_context(tc.psum_pool(name="psum", bufs=8))
+        ctx.enter_context(tc.manual_schedule())
+
+        w_dram = {"k": wk, "q": wq}
+        w_raw = {}
+        for w in ("k", "q"):
+            w_raw[w] = keep.tile([P, NT, D], BF16, name="w_raw_" + w)
+        x_raw = []
+        for b in range(NB):
+            x_raw.append(keep.tile([P, NT, D], BF16, name="x_raw_%d" % b))
+
+        def load_w(w):
+            rows = w_dram[w][0, :, :].rearrange("(p t) d -> p t d", t=NT)
+            for t in range(NT):
+                nc.sync.dma_start(out=w_raw[w][:, t, :], in_=rows[:, t, :])
+
+        load_w("k")
+        for j in range(NT):
+            nc.sync.dma_start(out=x_raw[0][:, j, :], in_=x[0, j * P : (j + 1) * P, :])
+        load_w("q")
+        for b in range(1, NB):
+            nc.sync.dma_start(out=x_raw[b][:], in_=x[b, :, :].rearrange("(j p) d -> p j d", p=P))
+        beta_bf = keep.tile([P, 1], BF16, name="beta_bf")
+        nc.scalar.dma_start(out=beta_bf[:], in_=betas.partition_broadcast(P))
+
+        ident = keep.tile([P, P], F32, name="ident")
+        make_identity(nc, ident[:])
+        off_diag = keep.tile([P, P], F32, name="off_diag")
+        nc.vector.tensor_scalar(out=off_diag[:], in0=ident[:], scalar1=1.0, scalar2=LOWEST, op0=ALU.subtract, op1=ALU.mult)
+        neg_mask = keep.tile([P, P], F32, name="neg_mask")
+        nc.vector.scalar_tensor_tensor(out=neg_mask[:], in0=ident[:], scalar=MASKED, in1=off_diag[:], op0=ALU.mult, op1=ALU.add)
+        res = keep.tile([P, P], F32, name="res")
+        nc.vector.memset(res[:], 0.0)
+        neg_beta = keep.tile([P, 1], F32, name="neg_beta")
+        inv_beta = keep.tile([P, 1], F32, name="inv_beta")
+        neg_inv_beta = keep.tile([P, 1], F32, name="neg_inv_beta")
+        beta_f = keep.tile([P, 1], F32, name="beta_f")
+
+        def BETA():
+            nc.vector.tensor_copy(out=beta_f[:], in_=beta_bf[:])
+            nc.vector.tensor_scalar(out=neg_beta[:], in0=beta_bf[:], scalar1=-1.0, scalar2=None, op0=ALU.mult)
+            nc.vector.reciprocal(out=inv_beta[:], in_=beta_f[:])
+            nc.vector.tensor_scalar(out=neg_inv_beta[:], in0=inv_beta[:], scalar1=-1.0, scalar2=None, op0=ALU.mult)
+
+        part_top = keep.tile([P, NB * NT], F32, name="part_top")
+        neg_top = keep.tile([P, NB * NT], F32, name="neg_top")
+        sums = keep.tile([P, NB * NT], F32, name="sums")
+        scrap_v = keep.tile([P, P], F32, name="scrap_v")
+        scrap_s = keep.tile([P, N], BF16, name="scrap_s")
+
+        w_grp = {}
+        w_code = {}
+        w_scale = {}
+        for w in ("k", "q"):
+            w_grp[w] = keep.tile([P, NT, D], BF16, name="w_grp_" + w, align_bytes=64)
+            w_code[w] = keep.tile([P, NT, D // 4], U32, name="w_code_" + w, align_bytes=64)
+            w_scale[w] = keep.tile([P, NT, D // 4], U8, name="w_scale_" + w, align_bytes=64)
+        x_grp = {}
+        x_code = {}
+        x_scale = {}
+        z_grp = {}
+        z_code = {}
+        z_scale = {}
+        banks = {}
+        shifted = {}
+
+        def bank(key):
+            banks[key] = psum.tile([P, 512], F32, name="bank", tag="bank")
+            return banks[key]
+
+        def flip(key, raw_rows):
+            ps = bank(key)
+            words = raw_rows.bitcast(F32)
+            for c in range(4):
+                nc.tensor.transpose(ps[:, c * P : (c + 1) * P], words[:, c * P : (c + 1) * P], ident[:])
+
+        def regroup(key, grp_rows, eng):
+            dst = grp_rows.bitcast(F32).rearrange("p (g r u) -> p g r u", g=2, u=2)
+            src = banks[key][:].rearrange("p (g u r) -> p g r u", g=2, u=2)
+            if eng == "V":
+                nc.vector.tensor_copy(out=dst, in_=src)
+            else:
+                nc.scalar.copy(out=dst, in_=src)
+
+        def TW(w, t):
+            flip(("w", w, t), w_raw[w][:, t, :])
+
+        def EW(w, t, eng):
+            regroup(("w", w, t), w_grp[w][:, t, :], eng)
+
+        def QW(w, t):
+            nc.vector.quantize_mx(out=w_code[w][:, t, :].bitcast(FP8X4), scales=w_scale[w][:, t, :], in_=w_grp[w][:, t, :])
+
+        def TX(b, j):
+            flip(("x", b, j), x_raw[b][:, j, :])
+
+        def EX(b, j, eng):
+            if b not in x_grp:
+                x_grp[b] = ring2.tile([P, NT, D], BF16, name="x_grp", tag="x_grp", align_bytes=64)
+                x_code[b] = ring3.tile([P, NT, D // 4], U32, name="x_code", tag="x_code", align_bytes=64)
+                x_scale[b] = ring3.tile([P, NT, D // 4], U8, name="x_scale", tag="x_scale", align_bytes=64)
+            regroup(("x", b, j), x_grp[b][:, j, :], eng)
+
+        def QX(b, j):
+            nc.vector.quantize_mx(out=x_code[b][:, j, :].bitcast(FP8X4), scales=x_scale[b][:, j, :], in_=x_grp[b][:, j, :])
+
+        def S1(b, w, j):
+            ps = bank(("z", b, w, j))
+            for t in range(NT):
+                for g in range(2):
+                    cols = slice(g * P, (g + 1) * P)
+                    nc.tensor.matmul_mx(
+                        out=ps[:, t * P : (t + 1) * P],
+                        lhsT=w_code[w][:, t, cols].bitcast(FP8X4),
+                        lhsT_scale=w_scale[w][:, t, cols],
+                        rhs=x_code[b][:, j, cols].bitcast(FP8X4),
+                        rhs_scale=x_scale[b][:, j, cols],
+                        start=(g == 0),
+                        stop=(g == 1),
+                    )
+
+        def EQ(b, w, j, eng):
+            if (b, w) not in z_grp:
+                z_grp[(b, w)] = ring2.tile([P, N, 4], BF16, name="z_grp_" + w, tag="z_grp_" + w, align_bytes=64)
+                z_code[(b, w)] = ring3.tile([P, N], U32, name="z_code_" + w, tag="z_code_" + w, align_bytes=64)
+                z_scale[(b, w)] = ring3.tile([P, N], U8, name="z_scale_" + w, tag="z_scale_" + w, align_bytes=64)
+            dst = z_grp[(b, w)][:, j * P : (j + 1) * P, :]
+            src = banks[("z", b, w, j)][:].rearrange("p (t n) -> p n t", t=4)
+            if eng == "V":
+                nc.vector.tensor_copy(out=dst, in_=src)
+            else:
+                nc.scalar.copy(out=dst, in_=src)
+
+        def QK(b):
+            nc.vector.quantize_mx(
+                out=z_code[(b, "k")][:].bitcast(FP8X4),
+                scales=z_scale[(b, "k")][:],
+                in_=z_grp[(b, "k")][:].rearrange("p n t -> p (n t)"),
+            )
+
+        def QQ(b, j):
+            cols = slice(j * P, (j + 1) * P)
+            nc.vector.quantize_mx(
+                out=z_code[(b, "q")][:, cols].bitcast(FP8X4),
+                scales=z_scale[(b, "q")][:, cols],
+                in_=z_grp[(b, "q")][:, cols, :].rearrange("p n t -> p (n t)"),
+            )
+
+        def S2(b, j):
+            ps = bank(("a", b, j))
+            rows = slice(j * P, (j + 1) * P)
+            at = 0
+            for first, width in ((j * P, P),) + OTHERS[j]:
+                keys = slice(first, first + width)
+                nc.tensor.matmul_mx(
+                    out=ps[:, at : at + width],
+                    lhsT=z_code[(b, "q")][:, rows].bitcast(FP8X4),
+                    lhsT_scale=z_scale[(b, "q")][:, rows],
+                    rhs=z_code[(b, "k")][:, keys].bitcast(FP8X4),
+                    rhs_scale=z_scale[(b, "k")][:, keys],
+                    start=True,
+                    stop=True,
+                )
+                at += width
+
+        def V1(b, j):
+            shifted[(b, j)] = ring6.tile([P, N], F32, name="shifted", tag="shifted")
+            nc.vector.scalar_tensor_tensor(
+                out=shifted[(b, j)][:, 0:P], in0=banks[("a", b, j)][:, 0:P], scalar=neg_beta[:, 0:1], in1=neg_mask[:],
+                op0=ALU.mult, op1=ALU.max,
+            )
+
+        def V3(b, j):
+            c = b * NT + j
+            nc.vector.tensor_scalar(
+                out=shifted[(b, j)][:, P:N], in0=banks[("a", b, j)][:, P:N], scalar1=neg_beta[:, 0:1], scalar2=None,
+                op0=ALU.mult, op1=ALU.min, accum_out=part_top[:, c : c + 1],
+            )
+
+        def V2(b, j):
+            c = b * NT + j
+            nc.vector.tensor_scalar(
+                out=scrap_v[:], in0=shifted[(b, j)][:, 0:P], scalar1=1.0, scalar2=part_top[:, c : c + 1],
+                op0=ALU.mult, op1=ALU.min, accum_out=neg_top[:, c : c + 1],
+            )
+
+        def XO(b, j):
+            c = b * NT + j
+            nc.scalar.activation(
+                out=scrap_s[:], in_=shifted[(b, j)][:], func=ACT.Exp, bias=neg_top[:, c : c + 1], scale=-1.0,
+                accum_out=sums[:, c : c + 1],
+            )
+
+        def FIN():
+            cols = NB * NT
+            scaled_top = keep.tile([P, cols], F32, name="scaled_top")
+            nc.vector.tensor_scalar(out=scaled_top[:], in0=neg_top[:], scalar1=inv_beta[:, 0:1], scalar2=None, op0=ALU.mult)
+            log_sum = keep.tile([P, cols], F32, name="log_sum")
+            nc.scalar.activation(out=log_sum[:], in_=sums[:], func=ACT.Ln)
+            nc.vector.scalar_tensor_tensor(
+                out=res[:, 0:cols], in0=log_sum[:], scalar=neg_inv_beta[:, 0:1], in1=scaled_top[:], op0=ALU.mult, op1=ALU.add
+            )
+            ps = bank("out")
+            nc.tensor.transpose(ps[:, 0:P], res[:], ident[:])
+            flat = keep.tile([P, P], F32, name="flat")
+            nc.vector.tensor_copy(out=flat[:], in_=ps[:, 0:P])
+            nc.sync.dma_start(out=out.rearrange("b o (j p) -> (b o j) p", p=P), in_=flat[0:cols, :])
+
+        for t in range(4): TW('k',t)
+        EW('k',0,'S'); EW('k',1,'V'); QW('k',0); EW('k',2,'S'); EW('k',3,'V')
+        QW('k',1); QW('k',2); QW('k',3)
+        for j in range(4): TX(0,j)
+        for j in range(4): EX(0,j,'S'); QX(0,j)
+        S1(0,'k',0); S1(0,'k',1)
+        EQ(0,'k',0,'S'); EQ(0,'k',1,'S')
+        for t in range(4): TW('q',t)
+        EW('q',0,'V'); EW('q',1,'S'); EW('q',2,'V'); EW('q',3,'S')
+        for t in range(4): QW('q',t)
+        S1(0,'k',2); S1(0,'k',3)
+        EQ(0,'k',2,'S'); EQ(0,'k',3,'S'); QK(0); BETA()
+        S1(0,'q',0); S1(0,'q',1)
+        EQ(0,'q',0,'S'); EQ(0,'q',1,'S')
+        for j in range(4): TX(1,j)
+        S1(0,'q',2); S1(0,'q',3)
+        EX(1,0,'V'); EX(1,1,'V'); QQ(0,0); EX(1,2,'V'); EX(1,3,'S'); QX(1,0); QQ(0,1); QX(1,1)
+        EQ(0,'q',2,'S'); EQ(0,'q',3,'S')
+        QX(1,2); QQ(0,2); QX(1,3)
+        for i in range(1,NB):
+            p=i-1; n=i+1; more = n<NB; last = i==NB-1
+            if more:
+                for j in range(4): TX(n,j)
+                for j in range(3): EX(n,j,'V')
+                EX(n,3,'S')
+            QQ(p,3)
+            if more: QX(n,0)
+            for j in (0,1): S1(i,'k',j); S2(p,j)
+            EQ(i,'k',0,'S'); EQ(i,'k',1,'S')
+            V1(p,0); V3(p,0); V1(p,1); V3(p,1); V2(p,0); V2(p,1)
+            for j in (2,3): S1(i,'k',j); S2(p,j)
+            EQ(i,'k',2,'S'); XO(p,0); EQ(i,'k',3,'S'); XO(p,1)
+            V1(p,2); V3(p,2)
+            if more: QX(n,1)
+            V1(p,3); V3(p,3); QK(i); V2(p,2); V2(p,3)
+            if not last:
+                for j in range(4): S1(i,'q',j)
+                EQ(i,'q',0,'S'); EQ(i,'q',1,'S'); EQ(i,'q',2,'S'); XO(p,2); EQ(i,'q',3,'S'); XO(p,3)
+                QQ(i,0); QX(n,2); QQ(i,1); QX(n,3); QQ(i,2)
+            else:
+                S1(i,'q',0); S1(i,'q',1)
+                EQ(i,'q',0,'V'); EQ(i,'q',1,'S'); XO(p,2);
+                QQ(i,0);
+                S1(i,'q',2); S2(i,0); S1(i,'q',3)
+                EQ(i,'q',2,'V'); QQ(i,1); XO(p,3); EQ(i,'q',3,'S')
+                S2(i,1)
+                V1(i,0); V3(i,0); QQ(i,2); V2(i,0); S2(i,2)
+                QQ(i,3); S2(i,3)
+                V1(i,1); V3(i,1); XO(i,0); V1(i,2); V2(i,1); V3(i,2); XO(i,1); V1(i,3); V2(i,2); V3(i,3); XO(i,2); V2(i,3); XO(i,3)
+        FIN()

@@ -244,53 +244,453 @@ def tile_multiheadenergyattention_pa_t_kernel(tc, x, wk, wq, betas, out):
             nc.vector.tensor_copy(out=flat[:], in_=ps[:, 0:P])
             nc.sync.dma_start(out=out.rearrange("b o (j p) -> (b o j) p", p=P), in_=flat[0:cols, :])
 
-        for t in range(4): TW('k',t)
-        EW('k',0,'S'); EW('k',1,'V'); QW('k',0); EW('k',2,'S'); EW('k',3,'V')
-        QW('k',1); QW('k',2); QW('k',3)
-        for j in range(4): TX(0,j)
-        for j in range(4): EX(0,j,'S'); QX(0,j)
-        S1(0,'k',0); S1(0,'k',1)
-        EQ(0,'k',0,'S'); EQ(0,'k',1,'S')
-        for t in range(4): TW('q',t)
-        EW('q',0,'V'); EW('q',1,'S'); EW('q',2,'V'); EW('q',3,'S')
-        for t in range(4): QW('q',t)
-        S1(0,'k',2); S1(0,'k',3)
-        EQ(0,'k',2,'S'); EQ(0,'k',3,'S'); QK(0); BETA()
-        S1(0,'q',0); S1(0,'q',1)
-        EQ(0,'q',0,'S'); EQ(0,'q',1,'S')
-        for j in range(4): TX(1,j)
-        S1(0,'q',2); S1(0,'q',3)
-        EX(1,0,'V'); EX(1,1,'V'); QQ(0,0); EX(1,2,'V'); EX(1,3,'S'); QX(1,0); QQ(0,1); QX(1,1)
-        EQ(0,'q',2,'S'); EQ(0,'q',3,'S')
-        QX(1,2); QQ(0,2); QX(1,3)
-        for i in range(1,NB):
-            p=i-1; n=i+1; more = n<NB; last = i==NB-1
-            if more:
-                for j in range(4): TX(n,j)
-                for j in range(3): EX(n,j,'V')
-                EX(n,3,'S')
-            QQ(p,3)
-            if more: QX(n,0)
-            for j in (0,1): S1(i,'k',j); S2(p,j)
-            EQ(i,'k',0,'S'); EQ(i,'k',1,'S')
-            V1(p,0); V3(p,0); V1(p,1); V3(p,1); V2(p,0); V2(p,1)
-            for j in (2,3): S1(i,'k',j); S2(p,j)
-            EQ(i,'k',2,'S'); XO(p,0); EQ(i,'k',3,'S'); XO(p,1)
-            V1(p,2); V3(p,2)
-            if more: QX(n,1)
-            V1(p,3); V3(p,3); QK(i); V2(p,2); V2(p,3)
-            if not last:
-                for j in range(4): S1(i,'q',j)
-                EQ(i,'q',0,'S'); EQ(i,'q',1,'S'); EQ(i,'q',2,'S'); XO(p,2); EQ(i,'q',3,'S'); XO(p,3)
-                QQ(i,0); QX(n,2); QQ(i,1); QX(n,3); QQ(i,2)
-            else:
-                S1(i,'q',0); S1(i,'q',1)
-                EQ(i,'q',0,'V'); EQ(i,'q',1,'S'); XO(p,2);
-                QQ(i,0);
-                S1(i,'q',2); S2(i,0); S1(i,'q',3)
-                EQ(i,'q',2,'V'); QQ(i,1); XO(p,3); EQ(i,'q',3,'S')
-                S2(i,1)
-                V1(i,0); V3(i,0); QQ(i,2); V2(i,0); S2(i,2)
-                QQ(i,3); S2(i,3)
-                V1(i,1); V3(i,1); XO(i,0); V1(i,2); V2(i,1); V3(i,2); XO(i,1); V1(i,3); V2(i,2); V3(i,3); XO(i,2); V2(i,3); XO(i,3)
+        TW('k', 0)
+        TW('k', 1)
+        EW('k', 0, 'V')
+        TW('k', 2)
+        EW('k', 1, 'V')
+        TW('k', 3)
+        EW('k', 2, 'V')
+        TX(0, 0)
+        EW('k', 3, 'V')
+        TX(0, 1)
+        EX(0, 0, 'V')
+        TX(0, 2)
+        QW('k', 0)
+        EX(0, 1, 'S')
+        TX(0, 3)
+        QW('k', 1)
+        EX(0, 2, 'S')
+        QW('k', 2)
+        TW('q', 0)
+        QW('k', 3)
+        EX(0, 3, 'S')
+        QX(0, 0)
+        TW('q', 1)
+        QX(0, 1)
+        EW('q', 0, 'S')
+        QX(0, 2)
+        S1(0, 'k', 0)
+        QX(0, 3)
+        EW('q', 1, 'S')
+        S1(0, 'k', 1)
+        QW('q', 0)
+        EQ(0, 'k', 0, 'S')
+        QW('q', 1)
+        TW('q', 2)
+        TW('q', 3)
+        EQ(0, 'k', 1, 'S')
+        S1(0, 'k', 2)
+        EW('q', 2, 'V')
+        EW('q', 3, 'S')
+        S1(0, 'k', 3)
+        QW('q', 2)
+        EQ(0, 'k', 2, 'S')
+        TX(1, 0)
+        QW('q', 3)
+        TX(1, 1)
+        EQ(0, 'k', 3, 'S')
+        TX(1, 2)
+        EX(1, 0, 'V')
+        TX(1, 3)
+        EX(1, 1, 'V')
+        S1(0, 'q', 0)
+        EX(1, 3, 'S')
+        EX(1, 2, 'V')
+        S1(0, 'q', 1)
+        QX(1, 0)
+        EQ(0, 'q', 0, 'S')
+        S1(0, 'q', 2)
+        QX(1, 1)
+        QX(1, 2)
+        EQ(0, 'q', 1, 'S')
+        S1(0, 'q', 3)
+        QK(0)
+        BETA()
+        EQ(0, 'q', 2, 'S')
+        QQ(0, 0)
+        TX(2, 0)
+        QX(1, 3)
+        TX(2, 1)
+        EQ(0, 'q', 3, 'S')
+        QQ(0, 1)
+        TX(2, 2)
+        EX(2, 0, 'V')
+        TX(2, 3)
+        EX(2, 1, 'V')
+        S1(1, 'k', 0)
+        EX(2, 3, 'S')
+        EX(2, 2, 'V')
+        S1(1, 'k', 1)
+        QQ(0, 2)
+        EQ(1, 'k', 0, 'S')
+        S1(1, 'k', 2)
+        QQ(0, 3)
+        QX(2, 0)
+        QX(2, 1)
+        EQ(1, 'k', 1, 'S')
+        S2(0, 0)
+        QX(2, 2)
+        S1(1, 'k', 3)
+        QX(2, 3)
+        EQ(1, 'k', 2, 'S')
+        V1(0, 0)
+        S2(0, 1)
+        V3(0, 0)
+        S1(1, 'q', 0)
+        EQ(1, 'k', 3, 'S')
+        V1(0, 1)
+        S2(0, 2)
+        V3(0, 1)
+        S1(1, 'q', 1)
+        EQ(1, 'q', 0, 'S')
+        V2(0, 0)
+        QK(1)
+        S2(0, 3)
+        S1(1, 'q', 2)
+        XO(0, 0)
+        V1(0, 2)
+        V3(0, 2)
+        EQ(1, 'q', 1, 'S')
+        S1(1, 'q', 3)
+        V1(0, 3)
+        V3(0, 3)
+        EQ(1, 'q', 2, 'S')
+        TX(3, 0)
+        V2(0, 1)
+        V2(0, 2)
+        TX(3, 1)
+        EQ(1, 'q', 3, 'S')
+        QQ(1, 0)
+        V2(0, 3)
+        TX(3, 2)
+        EX(3, 0, 'V')
+        XO(0, 1)
+        TX(3, 3)
+        QQ(1, 1)
+        S1(2, 'k', 0)
+        XO(0, 2)
+        EX(3, 1, 'V')
+        S1(2, 'k', 1)
+        EX(3, 2, 'V')
+        XO(0, 3)
+        S1(2, 'k', 2)
+        QQ(1, 2)
+        EX(3, 3, 'S')
+        QQ(1, 3)
+        QX(3, 0)
+        EQ(2, 'k', 0, 'S')
+        S2(1, 0)
+        QX(3, 1)
+        S1(2, 'k', 3)
+        QX(3, 2)
+        EQ(2, 'k', 1, 'S')
+        QX(3, 3)
+        V1(1, 0)
+        S2(1, 1)
+        V3(1, 0)
+        EQ(2, 'k', 2, 'S')
+        S1(2, 'q', 0)
+        EQ(2, 'k', 3, 'S')
+        V1(1, 1)
+        S2(1, 2)
+        V3(1, 1)
+        S1(2, 'q', 1)
+        EQ(2, 'q', 0, 'S')
+        V2(1, 0)
+        V1(1, 2)
+        S2(1, 3)
+        V3(1, 2)
+        S1(2, 'q', 2)
+        XO(1, 0)
+        V2(1, 1)
+        QK(2)
+        EQ(2, 'q', 1, 'S')
+        S1(2, 'q', 3)
+        V1(1, 3)
+        EQ(2, 'q', 2, 'S')
+        V3(1, 3)
+        TX(4, 0)
+        V2(1, 2)
+        TX(4, 1)
+        XO(1, 1)
+        QQ(2, 0)
+        TX(4, 2)
+        V2(1, 3)
+        EX(4, 0, 'V')
+        EQ(2, 'q', 3, 'S')
+        TX(4, 3)
+        S1(3, 'k', 0)
+        QQ(2, 1)
+        XO(1, 2)
+        EX(4, 1, 'V')
+        S1(3, 'k', 1)
+        XO(1, 3)
+        EX(4, 2, 'V')
+        S1(3, 'k', 2)
+        EX(4, 3, 'S')
+        QQ(2, 2)
+        QQ(2, 3)
+        QX(4, 0)
+        EQ(3, 'k', 0, 'S')
+        S2(2, 0)
+        QX(4, 1)
+        S1(3, 'k', 3)
+        QX(4, 2)
+        EQ(3, 'k', 1, 'S')
+        QX(4, 3)
+        S2(2, 1)
+        V1(2, 0)
+        EQ(3, 'k', 2, 'S')
+        V3(2, 0)
+        S1(3, 'q', 0)
+        EQ(3, 'k', 3, 'S')
+        V1(2, 1)
+        S2(2, 2)
+        V3(2, 1)
+        S1(3, 'q', 1)
+        EQ(3, 'q', 0, 'S')
+        V2(2, 0)
+        V1(2, 2)
+        S2(2, 3)
+        V3(2, 2)
+        S1(3, 'q', 2)
+        XO(2, 0)
+        V2(2, 1)
+        QK(3)
+        EQ(3, 'q', 1, 'S')
+        S1(3, 'q', 3)
+        V1(2, 3)
+        EQ(3, 'q', 2, 'S')
+        V3(2, 3)
+        TX(5, 0)
+        V2(2, 2)
+        TX(5, 1)
+        XO(2, 1)
+        QQ(3, 0)
+        TX(5, 2)
+        V2(2, 3)
+        EX(5, 0, 'V')
+        EQ(3, 'q', 3, 'S')
+        TX(5, 3)
+        S1(4, 'k', 0)
+        QQ(3, 1)
+        XO(2, 2)
+        EX(5, 1, 'V')
+        S1(4, 'k', 1)
+        XO(2, 3)
+        EX(5, 2, 'V')
+        S1(4, 'k', 2)
+        EX(5, 3, 'S')
+        QQ(3, 2)
+        QQ(3, 3)
+        QX(5, 0)
+        EQ(4, 'k', 0, 'S')
+        S2(3, 0)
+        QX(5, 1)
+        S1(4, 'k', 3)
+        QX(5, 2)
+        EQ(4, 'k', 1, 'S')
+        QX(5, 3)
+        S2(3, 1)
+        V1(3, 0)
+        EQ(4, 'k', 2, 'S')
+        V3(3, 0)
+        S1(4, 'q', 0)
+        EQ(4, 'k', 3, 'S')
+        V1(3, 1)
+        S2(3, 2)
+        V3(3, 1)
+        S1(4, 'q', 1)
+        EQ(4, 'q', 0, 'S')
+        V2(3, 0)
+        V1(3, 2)
+        S2(3, 3)
+        V3(3, 2)
+        S1(4, 'q', 2)
+        XO(3, 0)
+        V2(3, 1)
+        QK(4)
+        EQ(4, 'q', 1, 'S')
+        S1(4, 'q', 3)
+        V1(3, 3)
+        EQ(4, 'q', 2, 'S')
+        V3(3, 3)
+        TX(6, 0)
+        V2(3, 2)
+        TX(6, 1)
+        XO(3, 1)
+        QQ(4, 0)
+        TX(6, 2)
+        V2(3, 3)
+        EX(6, 0, 'V')
+        EQ(4, 'q', 3, 'S')
+        TX(6, 3)
+        S1(5, 'k', 0)
+        QQ(4, 1)
+        XO(3, 2)
+        EX(6, 1, 'V')
+        S1(5, 'k', 1)
+        XO(3, 3)
+        EX(6, 2, 'V')
+        S1(5, 'k', 2)
+        EX(6, 3, 'S')
+        QQ(4, 2)
+        QQ(4, 3)
+        QX(6, 0)
+        EQ(5, 'k', 0, 'S')
+        S2(4, 0)
+        QX(6, 1)
+        S1(5, 'k', 3)
+        QX(6, 2)
+        EQ(5, 'k', 1, 'S')
+        QX(6, 3)
+        S2(4, 1)
+        V1(4, 0)
+        EQ(5, 'k', 2, 'S')
+        V3(4, 0)
+        S1(5, 'q', 0)
+        EQ(5, 'k', 3, 'S')
+        V1(4, 1)
+        S2(4, 2)
+        V3(4, 1)
+        S1(5, 'q', 1)
+        EQ(5, 'q', 0, 'S')
+        V2(4, 0)
+        V1(4, 2)
+        S2(4, 3)
+        V3(4, 2)
+        S1(5, 'q', 2)
+        XO(4, 0)
+        V2(4, 1)
+        QK(5)
+        EQ(5, 'q', 1, 'S')
+        S1(5, 'q', 3)
+        V1(4, 3)
+        EQ(5, 'q', 2, 'S')
+        V3(4, 3)
+        TX(7, 0)
+        V2(4, 2)
+        TX(7, 1)
+        XO(4, 1)
+        QQ(5, 0)
+        TX(7, 2)
+        V2(4, 3)
+        EX(7, 0, 'V')
+        EQ(5, 'q', 3, 'S')
+        TX(7, 3)
+        S1(6, 'k', 0)
+        QQ(5, 1)
+        XO(4, 2)
+        EX(7, 1, 'V')
+        S1(6, 'k', 1)
+        XO(4, 3)
+        EX(7, 2, 'V')
+        S1(6, 'k', 2)
+        EX(7, 3, 'S')
+        QQ(5, 2)
+        QQ(5, 3)
+        QX(7, 0)
+        EQ(6, 'k', 0, 'S')
+        S2(5, 0)
+        QX(7, 1)
+        S1(6, 'k', 3)
+        QX(7, 2)
+        EQ(6, 'k', 1, 'S')
+        QX(7, 3)
+        S2(5, 1)
+        V1(5, 0)
+        EQ(6, 'k', 2, 'S')
+        V3(5, 0)
+        S1(6, 'q', 0)
+        EQ(6, 'k', 3, 'S')
+        V1(5, 1)
+        S2(5, 2)
+        V3(5, 1)
+        S1(6, 'q', 1)
+        EQ(6, 'q', 0, 'S')
+        V2(5, 0)
+        V1(5, 2)
+        S2(5, 3)
+        QK(6)
+        S1(6, 'q', 2)
+        XO(5, 0)
+        QQ(6, 0)
+        V3(5, 2)
+        EQ(6, 'q', 1, 'S')
+        S1(6, 'q', 3)
+        V2(5, 1)
+        EQ(6, 'q', 2, 'S')
+        V1(5, 3)
+        S1(7, 'k', 0)
+        V3(5, 3)
+        EQ(6, 'q', 3, 'S')
+        QQ(6, 1)
+        S2(6, 0)
+        V2(5, 2)
+        S1(7, 'k', 1)
+        QQ(6, 2)
+        XO(5, 1)
+        EQ(7, 'k', 0, 'V')
+        S2(6, 1)
+        XO(5, 2)
+        QQ(6, 3)
+        S1(7, 'k', 2)
+        V2(5, 3)
+        V1(6, 0)
+        V3(6, 0)
+        EQ(7, 'k', 1, 'S')
+        S2(6, 2)
+        V1(6, 1)
+        S1(7, 'k', 3)
+        XO(5, 3)
+        V3(6, 1)
+        EQ(7, 'k', 2, 'V')
+        S2(6, 3)
+        S1(7, 'q', 0)
+        EQ(7, 'k', 3, 'S')
+        V2(6, 0)
+        V1(6, 2)
+        V3(6, 2)
+        S1(7, 'q', 1)
+        XO(6, 0)
+        EQ(7, 'q', 0, 'V')
+        S1(7, 'q', 2)
+        QK(7)
+        EQ(7, 'q', 1, 'S')
+        S1(7, 'q', 3)
+        QQ(7, 0)
+        EQ(7, 'q', 2, 'S')
+        V1(6, 3)
+        V3(6, 3)
+        S2(7, 0)
+        EQ(7, 'q', 3, 'S')
+        QQ(7, 1)
+        V2(6, 1)
+        QQ(7, 2)
+        V2(6, 2)
+        S2(7, 1)
+        V1(7, 0)
+        XO(6, 1)
+        V3(7, 0)
+        S2(7, 2)
+        QQ(7, 3)
+        XO(6, 2)
+        V2(6, 3)
+        V1(7, 1)
+        V3(7, 1)
+        S2(7, 3)
+        XO(6, 3)
+        V1(7, 2)
+        V3(7, 2)
+        V1(7, 3)
+        V3(7, 3)
+        V2(7, 0)
+        V2(7, 1)
+        V2(7, 2)
+        V2(7, 3)
+        XO(7, 0)
+        XO(7, 1)
+        XO(7, 2)
+        XO(7, 3)
         FIN()

@@ -67,8 +67,6 @@ def tile_multiheadenergyattention_pa_t_kernel(tc, x, wk, wq, betas, out):
         nc.vector.tensor_scalar(out=off_diag[:], in0=ident[:], scalar1=1.0, scalar2=LOWEST, op0=ALU.subtract, op1=ALU.mult)
         neg_mask = keep.tile([P, P], F32, name="neg_mask")
         nc.vector.scalar_tensor_tensor(out=neg_mask[:], in0=ident[:], scalar=MASKED, in1=off_diag[:], op0=ALU.mult, op1=ALU.add)
-        res = keep.tile([P, P], F32, name="res")
-        nc.vector.memset(res[:], 0.0)
         neg_beta = keep.tile([P, 1], F32, name="neg_beta")
         inv_beta = keep.tile([P, 1], F32, name="inv_beta")
         neg_inv_beta = keep.tile([P, 1], F32, name="neg_inv_beta")
@@ -81,8 +79,10 @@ def tile_multiheadenergyattention_pa_t_kernel(tc, x, wk, wq, betas, out):
             nc.vector.tensor_scalar(out=neg_inv_beta[:], in0=inv_beta[:], scalar1=-1.0, scalar2=None, op0=ALU.mult)
 
         part_top = keep.tile([P, NB * NT], F32, name="part_top")
-        neg_top = keep.tile([P, NB * NT], F32, name="neg_top")
-        sums = keep.tile([P, NB * NT], F32, name="sums")
+        neg_top = keep.tile([P, P], F32, name="neg_top")
+        nc.vector.memset(neg_top[:], 0.0)
+        sums = keep.tile([P, P], F32, name="sums")
+        nc.vector.memset(sums[:], 1.0)
         scrap_v = keep.tile([P, P], F32, name="scrap_v")
         scrap_s = keep.tile([P, N], BF16, name="scrap_s")
 
@@ -230,19 +230,19 @@ def tile_multiheadenergyattention_pa_t_kernel(tc, x, wk, wq, betas, out):
             )
 
         def FIN():
-            cols = NB * NT
-            scaled_top = keep.tile([P, cols], F32, name="scaled_top")
-            nc.vector.tensor_scalar(out=scaled_top[:], in0=neg_top[:], scalar1=inv_beta[:, 0:1], scalar2=None, op0=ALU.mult)
-            log_sum = keep.tile([P, cols], F32, name="log_sum")
-            nc.scalar.activation(out=log_sum[:], in_=sums[:], func=ACT.Ln)
-            nc.vector.scalar_tensor_tensor(
-                out=res[:, 0:cols], in0=log_sum[:], scalar=neg_inv_beta[:, 0:1], in1=scaled_top[:], op0=ALU.mult, op1=ALU.add
-            )
-            ps = bank("out")
-            nc.tensor.transpose(ps[:, 0:P], res[:], ident[:])
+            top_bank = bank("top")
+            nc.tensor.transpose(top_bank[:, 0:P], neg_top[:], ident[:])
+            top_t = keep.tile([P, P], F32, name="top_t")
+            nc.vector.tensor_scalar(out=top_t[:], in0=top_bank[:, 0:P], scalar1=inv_beta[:, 0:1], scalar2=None, op0=ALU.mult)
+            sum_bank = bank("sum")
+            nc.tensor.transpose(sum_bank[:, 0:P], sums[:], ident[:])
+            log_t = keep.tile([P, P], F32, name="log_t")
+            nc.scalar.activation(out=log_t[:], in_=sum_bank[:, 0:P], func=ACT.Ln)
             flat = keep.tile([P, P], F32, name="flat")
-            nc.vector.tensor_copy(out=flat[:], in_=ps[:, 0:P])
-            nc.sync.dma_start(out=out.rearrange("b o (j p) -> (b o j) p", p=P), in_=flat[0:cols, :])
+            nc.vector.scalar_tensor_tensor(
+                out=flat[:], in0=log_t[:], scalar=neg_inv_beta[:, 0:1], in1=top_t[:], op0=ALU.mult, op1=ALU.add
+            )
+            nc.sync.dma_start(out=out.rearrange("b o (j p) -> (b o j) p", p=P), in_=flat[0 : NB * NT, :])
 
         TW('k', 0)
         TW('k', 1)
@@ -677,20 +677,20 @@ def tile_multiheadenergyattention_pa_t_kernel(tc, x, wk, wq, betas, out):
         QQ(7, 3)
         XO(6, 2)
         V2(6, 3)
+        V2(7, 0)
         V1(7, 1)
-        V3(7, 1)
         S2(7, 3)
+        V3(7, 1)
         XO(6, 3)
         V1(7, 2)
         V3(7, 2)
-        V1(7, 3)
-        V3(7, 3)
-        V2(7, 0)
-        V2(7, 1)
-        V2(7, 2)
-        V2(7, 3)
         XO(7, 0)
+        V2(7, 1)
+        V1(7, 3)
+        V2(7, 2)
+        V3(7, 3)
         XO(7, 1)
         XO(7, 2)
+        V2(7, 3)
         XO(7, 3)
         FIN()

@@ -61,6 +61,8 @@ def tile_multiheadenergyattention_pa_t_kernel(tc, x, wk, wq, betas, out):
         beta_bf = keep.tile([P, 1], BF16, name="beta_bf")
         nc.scalar.dma_start(out=beta_bf[:], in_=betas.partition_broadcast(P))
 
+        warm = keep.tile([P, 512], BF16, name="warm")
+        nc.vector.memset(warm[:], 0.0)
         ident = keep.tile([P, P], F32, name="ident")
         make_identity(nc, ident[:])
         off_diag = keep.tile([P, P], F32, name="off_diag")
@@ -105,6 +107,11 @@ def tile_multiheadenergyattention_pa_t_kernel(tc, x, wk, wq, betas, out):
         def bank(key):
             banks[key] = psum.tile([P, 512], F32, name="bank", tag="bank")
             return banks[key]
+
+        def WARM(width):
+            if "warm" not in banks:
+                bank("warm")
+            nc.tensor.matmul(out=banks["warm"][:, 0:width], lhsT=warm[:, 0:P], rhs=warm[:, 0:width], start=True, stop=True)
 
         def flip(key, raw_rows):
             ps = bank(key)
@@ -244,29 +251,44 @@ def tile_multiheadenergyattention_pa_t_kernel(tc, x, wk, wq, betas, out):
             )
             nc.sync.dma_start(out=out.rearrange("b o (j p) -> (b o j) p", p=P), in_=flat[0 : NB * NT, :])
 
+        WARM(512)
+        WARM(512)
+        WARM(512)
+        WARM(512)
+        WARM(512)
         TW('k', 0)
+        WARM(256)
         TW('k', 1)
+        WARM(256)
         EW('k', 0, 'V')
         TW('k', 2)
+        WARM(256)
         EW('k', 1, 'V')
         TW('k', 3)
+        WARM(256)
         EW('k', 2, 'V')
         TX(0, 0)
+        WARM(256)
         EW('k', 3, 'V')
         TX(0, 1)
+        WARM(256)
         EX(0, 0, 'V')
         TX(0, 2)
+        WARM(256)
         QW('k', 0)
         EX(0, 1, 'S')
         TX(0, 3)
+        WARM(256)
         QW('k', 1)
         EX(0, 2, 'S')
         QW('k', 2)
         TW('q', 0)
+        WARM(256)
         QW('k', 3)
         EX(0, 3, 'S')
         QX(0, 0)
         TW('q', 1)
+        WARM(256)
         QX(0, 1)
         EW('q', 0, 'S')
         QX(0, 2)

@@ -17,11 +17,17 @@ D = 1024
 Z = 512
 P = 128
 NT = N // P
+BANK = 512
+ROW_TILES = NB * NT
 FLOPS = 2 * NB * N * D * 2 * Z + 2 * NB * N * N * Z
+
 MASKED = 1.0e9
 LOWEST = 3.0e38
+VECTOR = "vector"
+SCALAR = "scalar"
+WARM_UP = 5
 
-OTHERS = (
+OTHER_KEYS = (
     ((128, 256), (384, 128)),
     ((256, 256), (0, 128)),
     ((0, 256), (384, 128)),
@@ -33,9 +39,9 @@ def tile_multiheadenergyattention_pa_t_kernel(tc, x, wk, wq, betas, out):
     nc = tc.nc
     with ExitStack() as ctx:
         keep = ctx.enter_context(tc.tile_pool(name="keep", bufs=1))
-        ring2 = ctx.enter_context(tc.tile_pool(name="ring2", bufs=2))
-        ring3 = ctx.enter_context(tc.tile_pool(name="ring3", bufs=3))
-        ring6 = ctx.enter_context(tc.tile_pool(name="ring6", bufs=6))
+        pairs = ctx.enter_context(tc.tile_pool(name="pairs", bufs=2))
+        triples = ctx.enter_context(tc.tile_pool(name="triples", bufs=3))
+        rows = ctx.enter_context(tc.tile_pool(name="rows", bufs=6))
         psum = ctx.enter_context(tc.psum_pool(name="psum", bufs=8))
         ctx.enter_context(tc.manual_schedule())
 
@@ -47,46 +53,49 @@ def tile_multiheadenergyattention_pa_t_kernel(tc, x, wk, wq, betas, out):
         for b in range(NB):
             x_raw.append(keep.tile([P, NT, D], BF16, name="x_raw_%d" % b))
 
-        def load_w(w):
-            rows = w_dram[w][0, :, :].rearrange("(p t) d -> p t d", t=NT)
+        def load_weights(w):
+            tiles = w_dram[w][0, :, :].rearrange("(p t) d -> p t d", t=NT)
             for t in range(NT):
-                nc.sync.dma_start(out=w_raw[w][:, t, :], in_=rows[:, t, :])
+                nc.sync.dma_start(out=w_raw[w][:, t, :], in_=tiles[:, t, :])
 
-        load_w("k")
+        load_weights("k")
         for j in range(NT):
             nc.sync.dma_start(out=x_raw[0][:, j, :], in_=x[0, j * P : (j + 1) * P, :])
-        load_w("q")
+        load_weights("q")
         for b in range(1, NB):
             nc.sync.dma_start(out=x_raw[b][:], in_=x[b, :, :].rearrange("(j p) d -> p j d", p=P))
         beta_bf = keep.tile([P, 1], BF16, name="beta_bf")
         nc.scalar.dma_start(out=beta_bf[:], in_=betas.partition_broadcast(P))
 
-        warm = keep.tile([P, 512], BF16, name="warm")
-        nc.vector.memset(warm[:], 0.0)
+        zeros = keep.tile([P, BANK], BF16, name="zeros")
+        nc.vector.memset(zeros[:], 0.0)
         ident = keep.tile([P, P], F32, name="ident")
         make_identity(nc, ident[:])
         off_diag = keep.tile([P, P], F32, name="off_diag")
-        nc.vector.tensor_scalar(out=off_diag[:], in0=ident[:], scalar1=1.0, scalar2=LOWEST, op0=ALU.subtract, op1=ALU.mult)
-        neg_mask = keep.tile([P, P], F32, name="neg_mask")
-        nc.vector.scalar_tensor_tensor(out=neg_mask[:], in0=ident[:], scalar=MASKED, in1=off_diag[:], op0=ALU.mult, op1=ALU.add)
-        neg_beta = keep.tile([P, 1], F32, name="neg_beta")
-        inv_beta = keep.tile([P, 1], F32, name="inv_beta")
-        neg_inv_beta = keep.tile([P, 1], F32, name="neg_inv_beta")
-        beta_f = keep.tile([P, 1], F32, name="beta_f")
-
-        def BETA():
-            nc.vector.tensor_copy(out=beta_f[:], in_=beta_bf[:])
-            nc.vector.tensor_scalar(out=neg_beta[:], in0=beta_bf[:], scalar1=-1.0, scalar2=None, op0=ALU.mult)
-            nc.vector.reciprocal(out=inv_beta[:], in_=beta_f[:])
-            nc.vector.tensor_scalar(out=neg_inv_beta[:], in0=inv_beta[:], scalar1=-1.0, scalar2=None, op0=ALU.mult)
-
-        part_top = keep.tile([P, NB * NT], F32, name="part_top")
+        nc.vector.tensor_scalar(
+            out=off_diag[:], in0=ident[:], scalar1=1.0, scalar2=LOWEST, op0=ALU.subtract, op1=ALU.mult
+        )
+        mask = keep.tile([P, P], F32, name="mask")
+        nc.vector.scalar_tensor_tensor(
+            out=mask[:], in0=ident[:], scalar=MASKED, in1=off_diag[:], op0=ALU.mult, op1=ALU.add
+        )
         neg_top = keep.tile([P, P], F32, name="neg_top")
         nc.vector.memset(neg_top[:], 0.0)
         sums = keep.tile([P, P], F32, name="sums")
         nc.vector.memset(sums[:], 1.0)
-        scrap_v = keep.tile([P, P], F32, name="scrap_v")
-        scrap_s = keep.tile([P, N], BF16, name="scrap_s")
+        others_min = keep.tile([P, ROW_TILES], F32, name="others_min")
+        unread_v = keep.tile([P, P], F32, name="unread_v")
+        unread_s = keep.tile([P, N], BF16, name="unread_s")
+        beta_f = keep.tile([P, 1], F32, name="beta_f")
+        neg_beta = keep.tile([P, 1], F32, name="neg_beta")
+        inv_beta = keep.tile([P, 1], F32, name="inv_beta")
+        neg_inv_beta = keep.tile([P, 1], F32, name="neg_inv_beta")
+
+        def beta_columns():
+            nc.vector.tensor_copy(out=beta_f[:], in_=beta_bf[:])
+            nc.vector.tensor_scalar(out=neg_beta[:], in0=beta_bf[:], scalar1=-1.0, scalar2=None, op0=ALU.mult)
+            nc.vector.reciprocal(out=inv_beta[:], in_=beta_f[:])
+            nc.vector.tensor_scalar(out=neg_inv_beta[:], in0=inv_beta[:], scalar1=-1.0, scalar2=None, op0=ALU.mult)
 
         w_grp = {}
         w_code = {}
@@ -98,64 +107,75 @@ def tile_multiheadenergyattention_pa_t_kernel(tc, x, wk, wq, betas, out):
         x_grp = {}
         x_code = {}
         x_scale = {}
-        z_grp = {}
-        z_code = {}
-        z_scale = {}
+        h_grp = {}
+        h_code = {}
+        h_scale = {}
         banks = {}
         shifted = {}
 
-        def bank(key):
-            banks[key] = psum.tile([P, 512], F32, name="bank", tag="bank")
+        def new_bank(key):
+            banks[key] = psum.tile([P, BANK], F32, name="bank", tag="bank")
             return banks[key]
 
-        def WARM(width):
-            if "warm" not in banks:
-                bank("warm")
-            nc.tensor.matmul(out=banks["warm"][:, 0:width], lhsT=warm[:, 0:P], rhs=warm[:, 0:width], start=True, stop=True)
-
-        def flip(key, raw_rows):
-            ps = bank(key)
-            words = raw_rows.bitcast(F32)
-            for c in range(4):
-                nc.tensor.transpose(ps[:, c * P : (c + 1) * P], words[:, c * P : (c + 1) * P], ident[:])
-
-        def regroup(key, grp_rows, eng):
-            dst = grp_rows.bitcast(F32).rearrange("p (g r u) -> p g r u", g=2, u=2)
-            src = banks[key][:].rearrange("p (g u r) -> p g r u", g=2, u=2)
-            if eng == "V":
+        def copy_out(engine, dst, src):
+            if engine == VECTOR:
                 nc.vector.tensor_copy(out=dst, in_=src)
             else:
                 nc.scalar.copy(out=dst, in_=src)
 
-        def TW(w, t):
+        def idle_matmul(width):
+            if "idle" not in banks:
+                new_bank("idle")
+            nc.tensor.matmul(
+                out=banks["idle"][:, 0:width], lhsT=zeros[:, 0:P], rhs=zeros[:, 0:width], start=True, stop=True
+            )
+
+        def flip(key, raw_rows):
+            bank = new_bank(key)
+            words = raw_rows.bitcast(F32)
+            for c in range(4):
+                nc.tensor.transpose(bank[:, c * P : (c + 1) * P], words[:, c * P : (c + 1) * P], ident[:])
+
+        def regroup(engine, key, grp_rows):
+            copy_out(
+                engine,
+                grp_rows.bitcast(F32).rearrange("p (g r u) -> p g r u", g=2, u=2),
+                banks[key][:].rearrange("p (g u r) -> p g r u", g=2, u=2),
+            )
+
+        def flip_weights(w, t):
             flip(("w", w, t), w_raw[w][:, t, :])
 
-        def EW(w, t, eng):
-            regroup(("w", w, t), w_grp[w][:, t, :], eng)
+        def regroup_weights(w, t, engine):
+            regroup(engine, ("w", w, t), w_grp[w][:, t, :])
 
-        def QW(w, t):
-            nc.vector.quantize_mx(out=w_code[w][:, t, :].bitcast(FP8X4), scales=w_scale[w][:, t, :], in_=w_grp[w][:, t, :])
+        def quantise_weights(w, t):
+            nc.vector.quantize_mx(
+                out=w_code[w][:, t, :].bitcast(FP8X4), scales=w_scale[w][:, t, :], in_=w_grp[w][:, t, :]
+            )
 
-        def TX(b, j):
+        def flip_tokens(b, j):
             flip(("x", b, j), x_raw[b][:, j, :])
 
-        def EX(b, j, eng):
-            if b not in x_grp:
-                x_grp[b] = ring2.tile([P, NT, D], BF16, name="x_grp", tag="x_grp", align_bytes=64)
-                x_code[b] = ring3.tile([P, NT, D // 4], U32, name="x_code", tag="x_code", align_bytes=64)
-                x_scale[b] = ring3.tile([P, NT, D // 4], U8, name="x_scale", tag="x_scale", align_bytes=64)
-            regroup(("x", b, j), x_grp[b][:, j, :], eng)
+        def regroup_tokens(b, j, engine):
+            if j == 0:
+                x_grp[b] = pairs.tile([P, NT, D], BF16, name="x_grp", tag="x_grp", align_bytes=64)
+                x_code[b] = triples.tile([P, NT, D // 4], U32, name="x_code", tag="x_code", align_bytes=64)
+                x_scale[b] = triples.tile([P, NT, D // 4], U8, name="x_scale", tag="x_scale", align_bytes=64)
+            regroup(engine, ("x", b, j), x_grp[b][:, j, :])
 
-        def QX(b, j):
-            nc.vector.quantize_mx(out=x_code[b][:, j, :].bitcast(FP8X4), scales=x_scale[b][:, j, :], in_=x_grp[b][:, j, :])
+        def quantise_tokens(b, j):
+            nc.vector.quantize_mx(
+                out=x_code[b][:, j, :].bitcast(FP8X4), scales=x_scale[b][:, j, :], in_=x_grp[b][:, j, :]
+            )
 
-        def S1(b, w, j):
-            ps = bank(("z", b, w, j))
+        def project(b, w, j):
+            bank = new_bank(("h", b, w, j))
             for t in range(NT):
                 for g in range(2):
                     cols = slice(g * P, (g + 1) * P)
                     nc.tensor.matmul_mx(
-                        out=ps[:, t * P : (t + 1) * P],
+                        out=bank[:, t * P : (t + 1) * P],
                         lhsT=w_code[w][:, t, cols].bitcast(FP8X4),
                         lhsT_scale=w_scale[w][:, t, cols],
                         rhs=x_code[b][:, j, cols].bitcast(FP8X4),
@@ -164,555 +184,283 @@ def tile_multiheadenergyattention_pa_t_kernel(tc, x, wk, wq, betas, out):
                         stop=(g == 1),
                     )
 
-        def EQ(b, w, j, eng):
-            if (b, w) not in z_grp:
-                z_grp[(b, w)] = ring2.tile([P, N, 4], BF16, name="z_grp_" + w, tag="z_grp_" + w, align_bytes=64)
-                z_code[(b, w)] = ring3.tile([P, N], U32, name="z_code_" + w, tag="z_code_" + w, align_bytes=64)
-                z_scale[(b, w)] = ring3.tile([P, N], U8, name="z_scale_" + w, tag="z_scale_" + w, align_bytes=64)
-            dst = z_grp[(b, w)][:, j * P : (j + 1) * P, :]
-            src = banks[("z", b, w, j)][:].rearrange("p (t n) -> p n t", t=4)
-            if eng == "V":
-                nc.vector.tensor_copy(out=dst, in_=src)
-            else:
-                nc.scalar.copy(out=dst, in_=src)
-
-        def QK(b):
-            nc.vector.quantize_mx(
-                out=z_code[(b, "k")][:].bitcast(FP8X4),
-                scales=z_scale[(b, "k")][:],
-                in_=z_grp[(b, "k")][:].rearrange("p n t -> p (n t)"),
+        def regroup_heads(b, w, j, engine):
+            if j == 0:
+                h_grp[(b, w)] = pairs.tile([P, N, 4], BF16, name="h_grp_" + w, tag="h_grp_" + w, align_bytes=64)
+                h_code[(b, w)] = triples.tile([P, N], U32, name="h_code_" + w, tag="h_code_" + w, align_bytes=64)
+                h_scale[(b, w)] = triples.tile([P, N], U8, name="h_scale_" + w, tag="h_scale_" + w, align_bytes=64)
+            copy_out(
+                engine,
+                h_grp[(b, w)][:, j * P : (j + 1) * P, :],
+                banks[("h", b, w, j)][:].rearrange("p (t n) -> p n t", t=NT),
             )
 
-        def QQ(b, j):
+        def quantise_keys(b):
+            nc.vector.quantize_mx(
+                out=h_code[(b, "k")][:].bitcast(FP8X4),
+                scales=h_scale[(b, "k")][:],
+                in_=h_grp[(b, "k")][:].rearrange("p n t -> p (n t)"),
+            )
+
+        def quantise_queries(b, j):
             cols = slice(j * P, (j + 1) * P)
             nc.vector.quantize_mx(
-                out=z_code[(b, "q")][:, cols].bitcast(FP8X4),
-                scales=z_scale[(b, "q")][:, cols],
-                in_=z_grp[(b, "q")][:, cols, :].rearrange("p n t -> p (n t)"),
+                out=h_code[(b, "q")][:, cols].bitcast(FP8X4),
+                scales=h_scale[(b, "q")][:, cols],
+                in_=h_grp[(b, "q")][:, cols, :].rearrange("p n t -> p (n t)"),
             )
 
-        def S2(b, j):
-            ps = bank(("a", b, j))
-            rows = slice(j * P, (j + 1) * P)
+        def scores(b, j):
+            bank = new_bank(("a", b, j))
+            queries = slice(j * P, (j + 1) * P)
             at = 0
-            for first, width in ((j * P, P),) + OTHERS[j]:
+            for first, width in ((j * P, P),) + OTHER_KEYS[j]:
                 keys = slice(first, first + width)
                 nc.tensor.matmul_mx(
-                    out=ps[:, at : at + width],
-                    lhsT=z_code[(b, "q")][:, rows].bitcast(FP8X4),
-                    lhsT_scale=z_scale[(b, "q")][:, rows],
-                    rhs=z_code[(b, "k")][:, keys].bitcast(FP8X4),
-                    rhs_scale=z_scale[(b, "k")][:, keys],
+                    out=bank[:, at : at + width],
+                    lhsT=h_code[(b, "q")][:, queries].bitcast(FP8X4),
+                    lhsT_scale=h_scale[(b, "q")][:, queries],
+                    rhs=h_code[(b, "k")][:, keys].bitcast(FP8X4),
+                    rhs_scale=h_scale[(b, "k")][:, keys],
                     start=True,
                     stop=True,
                 )
                 at += width
 
-        def V1(b, j):
-            shifted[(b, j)] = ring6.tile([P, N], F32, name="shifted", tag="shifted")
+        def shift_own(b, j):
+            shifted[(b, j)] = rows.tile([P, N], F32, name="shifted", tag="shifted")
             nc.vector.scalar_tensor_tensor(
-                out=shifted[(b, j)][:, 0:P], in0=banks[("a", b, j)][:, 0:P], scalar=neg_beta[:, 0:1], in1=neg_mask[:],
-                op0=ALU.mult, op1=ALU.max,
+                out=shifted[(b, j)][:, 0:P],
+                in0=banks[("a", b, j)][:, 0:P],
+                scalar=neg_beta[:, 0:1],
+                in1=mask[:],
+                op0=ALU.mult,
+                op1=ALU.max,
             )
 
-        def V3(b, j):
+        def shift_others(b, j):
             c = b * NT + j
             nc.vector.tensor_scalar(
-                out=shifted[(b, j)][:, P:N], in0=banks[("a", b, j)][:, P:N], scalar1=neg_beta[:, 0:1], scalar2=None,
-                op0=ALU.mult, op1=ALU.min, accum_out=part_top[:, c : c + 1],
+                out=shifted[(b, j)][:, P:N],
+                in0=banks[("a", b, j)][:, P:N],
+                scalar1=neg_beta[:, 0:1],
+                scalar2=None,
+                op0=ALU.mult,
+                op1=ALU.min,
+                accum_out=others_min[:, c : c + 1],
             )
 
-        def V2(b, j):
+        def fold_min(b, j):
             c = b * NT + j
             nc.vector.tensor_scalar(
-                out=scrap_v[:], in0=shifted[(b, j)][:, 0:P], scalar1=1.0, scalar2=part_top[:, c : c + 1],
-                op0=ALU.mult, op1=ALU.min, accum_out=neg_top[:, c : c + 1],
+                out=unread_v[:],
+                in0=shifted[(b, j)][:, 0:P],
+                scalar1=1.0,
+                scalar2=others_min[:, c : c + 1],
+                op0=ALU.mult,
+                op1=ALU.min,
+                accum_out=neg_top[:, c : c + 1],
             )
 
-        def XO(b, j):
+        def exp_sum(b, j):
             c = b * NT + j
             nc.scalar.activation(
-                out=scrap_s[:], in_=shifted[(b, j)][:], func=ACT.Exp, bias=neg_top[:, c : c + 1], scale=-1.0,
+                out=unread_s[:],
+                in_=shifted[(b, j)][:],
+                func=ACT.Exp,
+                bias=neg_top[:, c : c + 1],
+                scale=-1.0,
                 accum_out=sums[:, c : c + 1],
             )
 
-        def FIN():
-            top_bank = bank("top")
+        def finish():
+            top_bank = new_bank("top")
             nc.tensor.transpose(top_bank[:, 0:P], neg_top[:], ident[:])
             top_t = keep.tile([P, P], F32, name="top_t")
-            nc.vector.tensor_scalar(out=top_t[:], in0=top_bank[:, 0:P], scalar1=inv_beta[:, 0:1], scalar2=None, op0=ALU.mult)
-            sum_bank = bank("sum")
+            nc.vector.tensor_scalar(
+                out=top_t[:], in0=top_bank[:, 0:P], scalar1=inv_beta[:, 0:1], scalar2=None, op0=ALU.mult
+            )
+            sum_bank = new_bank("sum")
             nc.tensor.transpose(sum_bank[:, 0:P], sums[:], ident[:])
             log_t = keep.tile([P, P], F32, name="log_t")
             nc.scalar.activation(out=log_t[:], in_=sum_bank[:, 0:P], func=ACT.Ln)
-            flat = keep.tile([P, P], F32, name="flat")
+            energy = keep.tile([P, P], F32, name="energy")
             nc.vector.scalar_tensor_tensor(
-                out=flat[:], in0=log_t[:], scalar=neg_inv_beta[:, 0:1], in1=top_t[:], op0=ALU.mult, op1=ALU.add
+                out=energy[:], in0=log_t[:], scalar=neg_inv_beta[:, 0:1], in1=top_t[:], op0=ALU.mult, op1=ALU.add
             )
-            nc.sync.dma_start(out=out.rearrange("b o (j p) -> (b o j) p", p=P), in_=flat[0 : NB * NT, :])
+            nc.sync.dma_start(out=out.rearrange("b o (j p) -> (b o j) p", p=P), in_=energy[0:ROW_TILES, :])
 
-        WARM(512)
-        WARM(512)
-        WARM(512)
-        WARM(512)
-        WARM(512)
-        TW('k', 0)
-        WARM(256)
-        TW('k', 1)
-        WARM(256)
-        EW('k', 0, 'V')
-        TW('k', 2)
-        WARM(256)
-        EW('k', 1, 'V')
-        TW('k', 3)
-        WARM(256)
-        EW('k', 2, 'V')
-        TX(0, 0)
-        WARM(256)
-        EW('k', 3, 'V')
-        TX(0, 1)
-        WARM(256)
-        EX(0, 0, 'V')
-        TX(0, 2)
-        WARM(256)
-        QW('k', 0)
-        EX(0, 1, 'S')
-        TX(0, 3)
-        WARM(256)
-        QW('k', 1)
-        EX(0, 2, 'S')
-        QW('k', 2)
-        TW('q', 0)
-        WARM(256)
-        QW('k', 3)
-        EX(0, 3, 'S')
-        QX(0, 0)
-        TW('q', 1)
-        WARM(256)
-        QX(0, 1)
-        EW('q', 0, 'S')
-        QX(0, 2)
-        S1(0, 'k', 0)
-        QX(0, 3)
-        EW('q', 1, 'S')
-        S1(0, 'k', 1)
-        QW('q', 0)
-        EQ(0, 'k', 0, 'S')
-        QW('q', 1)
-        TW('q', 2)
-        TW('q', 3)
-        EQ(0, 'k', 1, 'S')
-        S1(0, 'k', 2)
-        EW('q', 2, 'V')
-        EW('q', 3, 'S')
-        S1(0, 'k', 3)
-        QW('q', 2)
-        EQ(0, 'k', 2, 'S')
-        TX(1, 0)
-        QW('q', 3)
-        TX(1, 1)
-        EQ(0, 'k', 3, 'S')
-        TX(1, 2)
-        EX(1, 0, 'V')
-        TX(1, 3)
-        EX(1, 1, 'V')
-        S1(0, 'q', 0)
-        EX(1, 3, 'S')
-        EX(1, 2, 'V')
-        S1(0, 'q', 1)
-        QX(1, 0)
-        EQ(0, 'q', 0, 'S')
-        S1(0, 'q', 2)
-        QX(1, 1)
-        QX(1, 2)
-        EQ(0, 'q', 1, 'S')
-        S1(0, 'q', 3)
-        QK(0)
-        BETA()
-        EQ(0, 'q', 2, 'S')
-        QQ(0, 0)
-        TX(2, 0)
-        QX(1, 3)
-        TX(2, 1)
-        EQ(0, 'q', 3, 'S')
-        QQ(0, 1)
-        TX(2, 2)
-        EX(2, 0, 'V')
-        TX(2, 3)
-        EX(2, 1, 'V')
-        S1(1, 'k', 0)
-        EX(2, 3, 'S')
-        EX(2, 2, 'V')
-        S1(1, 'k', 1)
-        QQ(0, 2)
-        EQ(1, 'k', 0, 'S')
-        S1(1, 'k', 2)
-        QQ(0, 3)
-        QX(2, 0)
-        QX(2, 1)
-        EQ(1, 'k', 1, 'S')
-        S2(0, 0)
-        QX(2, 2)
-        S1(1, 'k', 3)
-        QX(2, 3)
-        EQ(1, 'k', 2, 'S')
-        V1(0, 0)
-        S2(0, 1)
-        V3(0, 0)
-        S1(1, 'q', 0)
-        EQ(1, 'k', 3, 'S')
-        V1(0, 1)
-        S2(0, 2)
-        V3(0, 1)
-        S1(1, 'q', 1)
-        EQ(1, 'q', 0, 'S')
-        V2(0, 0)
-        QK(1)
-        S2(0, 3)
-        S1(1, 'q', 2)
-        XO(0, 0)
-        V1(0, 2)
-        V3(0, 2)
-        EQ(1, 'q', 1, 'S')
-        S1(1, 'q', 3)
-        V1(0, 3)
-        V3(0, 3)
-        EQ(1, 'q', 2, 'S')
-        TX(3, 0)
-        V2(0, 1)
-        V2(0, 2)
-        TX(3, 1)
-        EQ(1, 'q', 3, 'S')
-        QQ(1, 0)
-        V2(0, 3)
-        TX(3, 2)
-        EX(3, 0, 'V')
-        XO(0, 1)
-        TX(3, 3)
-        QQ(1, 1)
-        S1(2, 'k', 0)
-        XO(0, 2)
-        EX(3, 1, 'V')
-        S1(2, 'k', 1)
-        EX(3, 2, 'V')
-        XO(0, 3)
-        S1(2, 'k', 2)
-        QQ(1, 2)
-        EX(3, 3, 'S')
-        QQ(1, 3)
-        QX(3, 0)
-        EQ(2, 'k', 0, 'S')
-        S2(1, 0)
-        QX(3, 1)
-        S1(2, 'k', 3)
-        QX(3, 2)
-        EQ(2, 'k', 1, 'S')
-        QX(3, 3)
-        V1(1, 0)
-        S2(1, 1)
-        V3(1, 0)
-        EQ(2, 'k', 2, 'S')
-        S1(2, 'q', 0)
-        EQ(2, 'k', 3, 'S')
-        V1(1, 1)
-        S2(1, 2)
-        V3(1, 1)
-        S1(2, 'q', 1)
-        EQ(2, 'q', 0, 'S')
-        V2(1, 0)
-        V1(1, 2)
-        S2(1, 3)
-        V3(1, 2)
-        S1(2, 'q', 2)
-        XO(1, 0)
-        V2(1, 1)
-        QK(2)
-        EQ(2, 'q', 1, 'S')
-        S1(2, 'q', 3)
-        V1(1, 3)
-        EQ(2, 'q', 2, 'S')
-        V3(1, 3)
-        TX(4, 0)
-        V2(1, 2)
-        TX(4, 1)
-        XO(1, 1)
-        QQ(2, 0)
-        TX(4, 2)
-        V2(1, 3)
-        EX(4, 0, 'V')
-        EQ(2, 'q', 3, 'S')
-        TX(4, 3)
-        S1(3, 'k', 0)
-        QQ(2, 1)
-        XO(1, 2)
-        EX(4, 1, 'V')
-        S1(3, 'k', 1)
-        XO(1, 3)
-        EX(4, 2, 'V')
-        S1(3, 'k', 2)
-        EX(4, 3, 'S')
-        QQ(2, 2)
-        QQ(2, 3)
-        QX(4, 0)
-        EQ(3, 'k', 0, 'S')
-        S2(2, 0)
-        QX(4, 1)
-        S1(3, 'k', 3)
-        QX(4, 2)
-        EQ(3, 'k', 1, 'S')
-        QX(4, 3)
-        S2(2, 1)
-        V1(2, 0)
-        EQ(3, 'k', 2, 'S')
-        V3(2, 0)
-        S1(3, 'q', 0)
-        EQ(3, 'k', 3, 'S')
-        V1(2, 1)
-        S2(2, 2)
-        V3(2, 1)
-        S1(3, 'q', 1)
-        EQ(3, 'q', 0, 'S')
-        V2(2, 0)
-        V1(2, 2)
-        S2(2, 3)
-        V3(2, 2)
-        S1(3, 'q', 2)
-        XO(2, 0)
-        V2(2, 1)
-        QK(3)
-        EQ(3, 'q', 1, 'S')
-        S1(3, 'q', 3)
-        V1(2, 3)
-        EQ(3, 'q', 2, 'S')
-        V3(2, 3)
-        TX(5, 0)
-        V2(2, 2)
-        TX(5, 1)
-        XO(2, 1)
-        QQ(3, 0)
-        TX(5, 2)
-        V2(2, 3)
-        EX(5, 0, 'V')
-        EQ(3, 'q', 3, 'S')
-        TX(5, 3)
-        S1(4, 'k', 0)
-        QQ(3, 1)
-        XO(2, 2)
-        EX(5, 1, 'V')
-        S1(4, 'k', 1)
-        XO(2, 3)
-        EX(5, 2, 'V')
-        S1(4, 'k', 2)
-        EX(5, 3, 'S')
-        QQ(3, 2)
-        QQ(3, 3)
-        QX(5, 0)
-        EQ(4, 'k', 0, 'S')
-        S2(3, 0)
-        QX(5, 1)
-        S1(4, 'k', 3)
-        QX(5, 2)
-        EQ(4, 'k', 1, 'S')
-        QX(5, 3)
-        S2(3, 1)
-        V1(3, 0)
-        EQ(4, 'k', 2, 'S')
-        V3(3, 0)
-        S1(4, 'q', 0)
-        EQ(4, 'k', 3, 'S')
-        V1(3, 1)
-        S2(3, 2)
-        V3(3, 1)
-        S1(4, 'q', 1)
-        EQ(4, 'q', 0, 'S')
-        V2(3, 0)
-        V1(3, 2)
-        S2(3, 3)
-        V3(3, 2)
-        S1(4, 'q', 2)
-        XO(3, 0)
-        V2(3, 1)
-        QK(4)
-        EQ(4, 'q', 1, 'S')
-        S1(4, 'q', 3)
-        V1(3, 3)
-        EQ(4, 'q', 2, 'S')
-        V3(3, 3)
-        TX(6, 0)
-        V2(3, 2)
-        TX(6, 1)
-        XO(3, 1)
-        QQ(4, 0)
-        TX(6, 2)
-        V2(3, 3)
-        EX(6, 0, 'V')
-        EQ(4, 'q', 3, 'S')
-        TX(6, 3)
-        S1(5, 'k', 0)
-        QQ(4, 1)
-        XO(3, 2)
-        EX(6, 1, 'V')
-        S1(5, 'k', 1)
-        XO(3, 3)
-        EX(6, 2, 'V')
-        S1(5, 'k', 2)
-        EX(6, 3, 'S')
-        QQ(4, 2)
-        QQ(4, 3)
-        QX(6, 0)
-        EQ(5, 'k', 0, 'S')
-        S2(4, 0)
-        QX(6, 1)
-        S1(5, 'k', 3)
-        QX(6, 2)
-        EQ(5, 'k', 1, 'S')
-        QX(6, 3)
-        S2(4, 1)
-        V1(4, 0)
-        EQ(5, 'k', 2, 'S')
-        V3(4, 0)
-        S1(5, 'q', 0)
-        EQ(5, 'k', 3, 'S')
-        V1(4, 1)
-        S2(4, 2)
-        V3(4, 1)
-        S1(5, 'q', 1)
-        EQ(5, 'q', 0, 'S')
-        V2(4, 0)
-        V1(4, 2)
-        S2(4, 3)
-        V3(4, 2)
-        S1(5, 'q', 2)
-        XO(4, 0)
-        V2(4, 1)
-        QK(5)
-        EQ(5, 'q', 1, 'S')
-        S1(5, 'q', 3)
-        V1(4, 3)
-        EQ(5, 'q', 2, 'S')
-        V3(4, 3)
-        TX(7, 0)
-        V2(4, 2)
-        TX(7, 1)
-        XO(4, 1)
-        QQ(5, 0)
-        TX(7, 2)
-        V2(4, 3)
-        EX(7, 0, 'V')
-        EQ(5, 'q', 3, 'S')
-        TX(7, 3)
-        S1(6, 'k', 0)
-        QQ(5, 1)
-        XO(4, 2)
-        EX(7, 1, 'V')
-        S1(6, 'k', 1)
-        XO(4, 3)
-        EX(7, 2, 'V')
-        S1(6, 'k', 2)
-        EX(7, 3, 'S')
-        QQ(5, 2)
-        QQ(5, 3)
-        QX(7, 0)
-        EQ(6, 'k', 0, 'S')
-        S2(5, 0)
-        QX(7, 1)
-        S1(6, 'k', 3)
-        QX(7, 2)
-        EQ(6, 'k', 1, 'S')
-        QX(7, 3)
-        S2(5, 1)
-        V1(5, 0)
-        EQ(6, 'k', 2, 'S')
-        V3(5, 0)
-        S1(6, 'q', 0)
-        EQ(6, 'k', 3, 'S')
-        V1(5, 1)
-        S2(5, 2)
-        V3(5, 1)
-        S1(6, 'q', 1)
-        EQ(6, 'q', 0, 'S')
-        V2(5, 0)
-        V1(5, 2)
-        S2(5, 3)
-        QK(6)
-        S1(6, 'q', 2)
-        XO(5, 0)
-        QQ(6, 0)
-        V3(5, 2)
-        EQ(6, 'q', 1, 'S')
-        S1(6, 'q', 3)
-        V2(5, 1)
-        EQ(6, 'q', 2, 'S')
-        V1(5, 3)
-        S1(7, 'k', 0)
-        V3(5, 3)
-        EQ(6, 'q', 3, 'S')
-        QQ(6, 1)
-        S2(6, 0)
-        V2(5, 2)
-        S1(7, 'k', 1)
-        QQ(6, 2)
-        XO(5, 1)
-        EQ(7, 'k', 0, 'V')
-        S2(6, 1)
-        XO(5, 2)
-        QQ(6, 3)
-        S1(7, 'k', 2)
-        V2(5, 3)
-        V1(6, 0)
-        V3(6, 0)
-        EQ(7, 'k', 1, 'S')
-        S2(6, 2)
-        V1(6, 1)
-        S1(7, 'k', 3)
-        XO(5, 3)
-        V3(6, 1)
-        EQ(7, 'k', 2, 'V')
-        S2(6, 3)
-        S1(7, 'q', 0)
-        EQ(7, 'k', 3, 'S')
-        V2(6, 0)
-        V1(6, 2)
-        V3(6, 2)
-        S1(7, 'q', 1)
-        XO(6, 0)
-        EQ(7, 'q', 0, 'V')
-        S1(7, 'q', 2)
-        QK(7)
-        EQ(7, 'q', 1, 'S')
-        S1(7, 'q', 3)
-        QQ(7, 0)
-        EQ(7, 'q', 2, 'S')
-        V1(6, 3)
-        V3(6, 3)
-        S2(7, 0)
-        EQ(7, 'q', 3, 'S')
-        QQ(7, 1)
-        V2(6, 1)
-        QQ(7, 2)
-        V2(6, 2)
-        S2(7, 1)
-        V1(7, 0)
-        XO(6, 1)
-        V3(7, 0)
-        S2(7, 2)
-        QQ(7, 3)
-        XO(6, 2)
-        V2(6, 3)
-        V2(7, 0)
-        V1(7, 1)
-        S2(7, 3)
-        V3(7, 1)
-        XO(6, 3)
-        V1(7, 2)
-        V3(7, 2)
-        XO(7, 0)
-        V2(7, 1)
-        V1(7, 3)
-        V2(7, 2)
-        V3(7, 3)
-        XO(7, 1)
-        XO(7, 2)
-        V2(7, 3)
-        XO(7, 3)
-        FIN()
+
+        for r in range(WARM_UP):
+            idle_matmul(BANK)
+        for t in range(NT):
+            flip_weights("k", t)
+            idle_matmul(BANK // 2)
+        for t in range(NT):
+            regroup_weights("k", t, VECTOR)
+        for j in range(NT):
+            flip_tokens(0, j)
+            idle_matmul(BANK // 2)
+        regroup_tokens(0, 0, VECTOR)
+        for j in (1, 2, 3):
+            regroup_tokens(0, j, SCALAR)
+        for t in range(NT):
+            quantise_weights("k", t)
+        for j in range(NT):
+            quantise_tokens(0, j)
+        for t in (0, 1):
+            flip_weights("q", t)
+            idle_matmul(BANK // 2)
+        project(0, "k", 0)
+        project(0, "k", 1)
+        for t in (2, 3):
+            flip_weights("q", t)
+        project(0, "k", 2)
+        project(0, "k", 3)
+        for t in (0, 1):
+            regroup_weights("q", t, SCALAR)
+        for t in (0, 1):
+            quantise_weights("q", t)
+        for j in (0, 1):
+            regroup_heads(0, "k", j, SCALAR)
+        regroup_weights("q", 2, VECTOR)
+        regroup_weights("q", 3, SCALAR)
+        for t in (2, 3):
+            quantise_weights("q", t)
+        for j in (2, 3):
+            regroup_heads(0, "k", j, SCALAR)
+        for j in range(NT):
+            flip_tokens(1, j)
+        for j in (0, 1, 2):
+            regroup_tokens(1, j, VECTOR)
+        regroup_tokens(1, 3, SCALAR)
+        for j in range(NT):
+            project(0, "q", j)
+        for j in range(NT):
+            quantise_tokens(1, j)
+        quantise_keys(0)
+        beta_columns()
+        for j in (0, 1, 2):
+            regroup_heads(0, "q", j, SCALAR)
+
+        for n in range(2, NB):
+            i = n - 1
+            p = n - 2
+            for j in range(NT):
+                flip_tokens(n, j)
+            if p > 0:
+                fold_min(p - 1, 2)
+                exp_sum(p - 1, 1)
+            quantise_queries(p, 0)
+            if p > 0:
+                fold_min(p - 1, 3)
+            regroup_tokens(n, 0, VECTOR)
+            regroup_heads(p, "q", 3, SCALAR)
+            quantise_queries(p, 1)
+            if p > 0:
+                exp_sum(p - 1, 2)
+            regroup_tokens(n, 1, VECTOR)
+            if p > 0:
+                exp_sum(p - 1, 3)
+            regroup_tokens(n, 2, VECTOR)
+            regroup_tokens(n, 3, SCALAR)
+            quantise_queries(p, 2)
+            quantise_queries(p, 3)
+            for j in (0, 1, 2):
+                project(i, "k", j)
+            for j in range(NT):
+                quantise_tokens(n, j)
+            regroup_heads(i, "k", 0, SCALAR)
+            regroup_heads(i, "k", 1, SCALAR)
+            scores(p, 0)
+            project(i, "k", 3)
+            scores(p, 1)
+            regroup_heads(i, "k", 2, SCALAR)
+            shift_own(p, 0)
+            shift_others(p, 0)
+            project(i, "q", 0)
+            regroup_heads(i, "k", 3, SCALAR)
+            scores(p, 2)
+            shift_own(p, 1)
+            shift_others(p, 1)
+            project(i, "q", 1)
+            regroup_heads(i, "q", 0, SCALAR)
+            fold_min(p, 0)
+            scores(p, 3)
+            shift_own(p, 2)
+            shift_others(p, 2)
+            project(i, "q", 2)
+            exp_sum(p, 0)
+            fold_min(p, 1)
+            quantise_keys(i)
+            regroup_heads(i, "q", 1, SCALAR)
+            project(i, "q", 3)
+            shift_own(p, 3)
+            regroup_heads(i, "q", 2, SCALAR)
+            shift_others(p, 3)
+
+        i = NB - 1
+        p = NB - 2
+        fold_min(p - 1, 2)
+        exp_sum(p - 1, 1)
+        quantise_queries(p, 0)
+        fold_min(p - 1, 3)
+        regroup_heads(p, "q", 3, SCALAR)
+        quantise_queries(p, 1)
+        exp_sum(p - 1, 2)
+        quantise_queries(p, 2)
+        for j in (0, 1, 2):
+            project(i, "k", j)
+            scores(p, j)
+        regroup_heads(i, "k", 0, VECTOR)
+        quantise_queries(p, 3)
+        regroup_heads(i, "k", 1, SCALAR)
+        exp_sum(p - 1, 3)
+        project(i, "k", 3)
+        scores(p, 3)
+        for j in (0, 1):
+            shift_own(p, j)
+            shift_others(p, j)
+        regroup_heads(i, "k", 2, VECTOR)
+        regroup_heads(i, "k", 3, SCALAR)
+        fold_min(p, 0)
+        shift_own(p, 2)
+        shift_others(p, 2)
+        for j in range(NT):
+            project(i, "q", j)
+        exp_sum(p, 0)
+        regroup_heads(i, "q", 0, VECTOR)
+        quantise_keys(i)
+        quantise_queries(i, 0)
+        for j in (1, 2, 3):
+            regroup_heads(i, "q", j, SCALAR)
+        shift_own(p, 3)
+        shift_others(p, 3)
+        quantise_queries(i, 1)
+        fold_min(p, 1)
+        quantise_queries(i, 2)
+        fold_min(p, 2)
+        for j in (0, 1, 2):
+            scores(i, j)
+        shift_own(i, 0)
+        shift_others(i, 0)
+        quantise_queries(i, 3)
+        scores(i, 3)
+        fold_min(p, 3)
+        for j in (1, 2, 3):
+            exp_sum(p, j)
+        fold_min(i, 0)
+        shift_own(i, 1)
+        shift_others(i, 1)
+        exp_sum(i, 0)
+        shift_own(i, 2)
+        shift_others(i, 2)
+        fold_min(i, 1)
+        exp_sum(i, 1)
+        shift_own(i, 3)
+        fold_min(i, 2)
+        shift_others(i, 3)
+        exp_sum(i, 2)
+        fold_min(i, 3)
+        exp_sum(i, 3)
+        finish()

@@ -343,7 +343,7 @@ def tile_multiheadenergyattention_pa_t_kernel(tc, x, wk, wq, betas, out):
         for j in (0, 1, 2):
             regroup_heads(0, "q", j, SCALAR)
 
-        for n in range(2, NB):
+        def period_start(n):
             i = n - 1
             p = n - 2
             for j in range(NT):
@@ -388,6 +388,11 @@ def tile_multiheadenergyattention_pa_t_kernel(tc, x, wk, wq, betas, out):
             fold_min(p, 0)
             scores(p, 3)
             shift_own(p, 2)
+
+        for n in range(2, NB - 1):
+            i = n - 1
+            p = n - 2
+            period_start(n)
             shift_others(p, 2)
             project(i, "q", 2)
             exp_sum(p, 0)
@@ -399,67 +404,90 @@ def tile_multiheadenergyattention_pa_t_kernel(tc, x, wk, wq, betas, out):
             regroup_heads(i, "q", 2, SCALAR)
             shift_others(p, 3)
 
+        i = NB - 2
+        p = NB - 3
+        period_start(NB - 1)
+        quantise_keys(i)
+        project(i, "q", 2)
+        exp_sum(p, 0)
+        quantise_queries(i, 0)
+        shift_others(p, 2)
+        regroup_heads(i, "q", 1, SCALAR)
+        project(i, "q", 3)
+        fold_min(p, 1)
+        regroup_heads(i, "q", 2, SCALAR)
+        shift_own(p, 3)
+        shift_others(p, 3)
+
         i = NB - 1
         p = NB - 2
-        fold_min(p - 1, 2)
-        exp_sum(p - 1, 1)
-        quantise_queries(p, 0)
-        fold_min(p - 1, 3)
+        project(i, "k", 0)
         regroup_heads(p, "q", 3, SCALAR)
         quantise_queries(p, 1)
-        exp_sum(p - 1, 2)
+        scores(p, 0)
+        fold_min(p - 1, 2)
+        project(i, "k", 1)
         quantise_queries(p, 2)
-        for j in (0, 1, 2):
-            project(i, "k", j)
-            scores(p, j)
+        exp_sum(p - 1, 1)
         regroup_heads(i, "k", 0, VECTOR)
+        scores(p, 1)
+        exp_sum(p - 1, 2)
         quantise_queries(p, 3)
+        project(i, "k", 2)
+        fold_min(p - 1, 3)
+        shift_own(p, 0)
+        shift_others(p, 0)
         regroup_heads(i, "k", 1, SCALAR)
-        exp_sum(p - 1, 3)
+        scores(p, 2)
+        shift_own(p, 1)
         project(i, "k", 3)
-        scores(p, 3)
-        for j in (0, 1):
-            shift_own(p, j)
-            shift_others(p, j)
+        exp_sum(p - 1, 3)
+        shift_others(p, 1)
         regroup_heads(i, "k", 2, VECTOR)
+        scores(p, 3)
+        project(i, "q", 0)
         regroup_heads(i, "k", 3, SCALAR)
         fold_min(p, 0)
         shift_own(p, 2)
         shift_others(p, 2)
-        for j in range(NT):
-            project(i, "q", j)
+        project(i, "q", 1)
         exp_sum(p, 0)
         regroup_heads(i, "q", 0, VECTOR)
+        project(i, "q", 2)
         quantise_keys(i)
+        regroup_heads(i, "q", 1, SCALAR)
+        project(i, "q", 3)
         quantise_queries(i, 0)
-        for j in (1, 2, 3):
-            regroup_heads(i, "q", j, SCALAR)
+        regroup_heads(i, "q", 2, SCALAR)
         shift_own(p, 3)
         shift_others(p, 3)
+        scores(i, 0)
+        regroup_heads(i, "q", 3, SCALAR)
         quantise_queries(i, 1)
         fold_min(p, 1)
         quantise_queries(i, 2)
         fold_min(p, 2)
-        for j in (0, 1, 2):
-            scores(i, j)
+        scores(i, 1)
         shift_own(i, 0)
+        exp_sum(p, 1)
         shift_others(i, 0)
+        scores(i, 2)
         quantise_queries(i, 3)
-        scores(i, 3)
+        exp_sum(p, 2)
         fold_min(p, 3)
-        for j in (1, 2, 3):
-            exp_sum(p, j)
         fold_min(i, 0)
         shift_own(i, 1)
+        scores(i, 3)
         shift_others(i, 1)
-        exp_sum(i, 0)
+        exp_sum(p, 3)
         shift_own(i, 2)
         shift_others(i, 2)
+        exp_sum(i, 0)
         fold_min(i, 1)
-        exp_sum(i, 1)
         shift_own(i, 3)
         fold_min(i, 2)
         shift_others(i, 3)
+        exp_sum(i, 1)
         exp_sum(i, 2)
         fold_min(i, 3)
         exp_sum(i, 3)

@@ -23,16 +23,12 @@ FLOPS = 2 * NB * N * D * 2 * Z + 2 * NB * N * N * Z
 
 MASKED = 1.0e9
 LOWEST = 3.0e38
+ROW_SLOTS = 6
+TENSOR = "tensor"
 VECTOR = "vector"
 SCALAR = "scalar"
 WARM_UP = 5
-
-OTHER_KEYS = (
-    ((128, 256), (384, 128)),
-    ((256, 256), (0, 128)),
-    ((0, 256), (384, 128)),
-    ((0, 256), (256, 128)),
-)
+BANKS = 8
 
 
 def tile_multiheadenergyattention_pa_t_kernel(tc, x, wk, wq, betas, out):
@@ -41,7 +37,7 @@ def tile_multiheadenergyattention_pa_t_kernel(tc, x, wk, wq, betas, out):
         keep = ctx.enter_context(tc.tile_pool(name="keep", bufs=1))
         pairs = ctx.enter_context(tc.tile_pool(name="pairs", bufs=2))
         triples = ctx.enter_context(tc.tile_pool(name="triples", bufs=3))
-        rows = ctx.enter_context(tc.tile_pool(name="rows", bufs=6))
+        rows = ctx.enter_context(tc.tile_pool(name="rows", bufs=ROW_SLOTS))
         psum = ctx.enter_context(tc.psum_pool(name="psum", bufs=8))
         ctx.enter_context(tc.manual_schedule())
 
@@ -62,7 +58,9 @@ def tile_multiheadenergyattention_pa_t_kernel(tc, x, wk, wq, betas, out):
         for j in range(NT):
             nc.sync.dma_start(out=x_raw[0][:, j, :], in_=x[0, j * P : (j + 1) * P, :])
         load_weights("q")
-        for b in range(1, NB):
+        for j in range(NT):
+            nc.sync.dma_start(out=x_raw[1][:, j, :], in_=x[1, j * P : (j + 1) * P, :])
+        for b in range(2, NB):
             nc.sync.dma_start(out=x_raw[b][:], in_=x[b, :, :].rearrange("(j p) d -> p j d", p=P))
         beta_bf = keep.tile([P, 1], BF16, name="beta_bf")
         nc.scalar.dma_start(out=beta_bf[:], in_=betas.partition_broadcast(P))
@@ -97,6 +95,8 @@ def tile_multiheadenergyattention_pa_t_kernel(tc, x, wk, wq, betas, out):
             nc.vector.reciprocal(out=inv_beta[:], in_=beta_f[:])
             nc.vector.tensor_scalar(out=neg_inv_beta[:], in0=inv_beta[:], scalar1=-1.0, scalar2=None, op0=ALU.mult)
 
+        beta_columns()
+
         w_grp = {}
         w_code = {}
         w_scale = {}
@@ -123,15 +123,13 @@ def tile_multiheadenergyattention_pa_t_kernel(tc, x, wk, wq, betas, out):
             else:
                 nc.scalar.copy(out=dst, in_=src)
 
-        def idle_matmul(width):
-            if "idle" not in banks:
-                new_bank("idle")
-            nc.tensor.matmul(
-                out=banks["idle"][:, 0:width], lhsT=zeros[:, 0:P], rhs=zeros[:, 0:width], start=True, stop=True
-            )
+        def idle_matmul(bank, width):
+            nc.tensor.matmul(out=bank[:, 0:width], lhsT=zeros[:, 0:P], rhs=zeros[:, 0:width], start=True, stop=True)
 
-        def flip(key, raw_rows):
+        def flip(key, raw_rows, idle=()):
             bank = new_bank(key)
+            for width in idle:
+                idle_matmul(bank, width)
             words = raw_rows.bitcast(F32)
             for c in range(4):
                 nc.tensor.transpose(bank[:, c * P : (c + 1) * P], words[:, c * P : (c + 1) * P], ident[:])
@@ -143,8 +141,8 @@ def tile_multiheadenergyattention_pa_t_kernel(tc, x, wk, wq, betas, out):
                 banks[key][:].rearrange("p (g u r) -> p g r u", g=2, u=2),
             )
 
-        def flip_weights(w, t):
-            flip(("w", w, t), w_raw[w][:, t, :])
+        def flip_weights(w, t, *idle):
+            flip(("w", w, t), w_raw[w][:, t, :], idle)
 
         def regroup_weights(w, t, engine):
             regroup(engine, ("w", w, t), w_grp[w][:, t, :])
@@ -154,11 +152,11 @@ def tile_multiheadenergyattention_pa_t_kernel(tc, x, wk, wq, betas, out):
                 out=w_code[w][:, t, :].bitcast(FP8X4), scales=w_scale[w][:, t, :], in_=w_grp[w][:, t, :]
             )
 
-        def flip_tokens(b, j):
-            flip(("x", b, j), x_raw[b][:, j, :])
+        def flip_tokens(b, j, *idle):
+            flip(("x", b, j), x_raw[b][:, j, :], idle)
 
         def regroup_tokens(b, j, engine):
-            if j == 0:
+            if b not in x_grp:
                 x_grp[b] = pairs.tile([P, NT, D], BF16, name="x_grp", tag="x_grp", align_bytes=64)
                 x_code[b] = triples.tile([P, NT, D // 4], U32, name="x_code", tag="x_code", align_bytes=64)
                 x_scale[b] = triples.tile([P, NT, D // 4], U8, name="x_scale", tag="x_scale", align_bytes=64)
@@ -185,7 +183,7 @@ def tile_multiheadenergyattention_pa_t_kernel(tc, x, wk, wq, betas, out):
                     )
 
         def regroup_heads(b, w, j, engine):
-            if j == 0:
+            if (b, w) not in h_grp:
                 h_grp[(b, w)] = pairs.tile([P, N, 4], BF16, name="h_grp_" + w, tag="h_grp_" + w, align_bytes=64)
                 h_code[(b, w)] = triples.tile([P, N], U32, name="h_code_" + w, tag="h_code_" + w, align_bytes=64)
                 h_scale[(b, w)] = triples.tile([P, N], U8, name="h_scale_" + w, tag="h_scale_" + w, align_bytes=64)
@@ -210,14 +208,21 @@ def tile_multiheadenergyattention_pa_t_kernel(tc, x, wk, wq, betas, out):
                 in_=h_grp[(b, "q")][:, cols, :].rearrange("p n t -> p (n t)"),
             )
 
+        def own_keys(j):
+            return slice(N - P, N) if j % 2 else slice(0, P)
+
+        def other_keys(j):
+            return slice(0, N - P) if j % 2 else slice(P, N)
+
         def scores(b, j):
             bank = new_bank(("a", b, j))
             queries = slice(j * P, (j + 1) * P)
-            at = 0
-            for first, width in ((j * P, P),) + OTHER_KEYS[j]:
-                keys = slice(first, first + width)
+            half = N // 2
+            own = (j // 2) * half
+            for at, first in ((0, half - own if j % 2 else own), (half, own if j % 2 else half - own)):
+                keys = slice(first, first + half)
                 nc.tensor.matmul_mx(
-                    out=bank[:, at : at + width],
+                    out=bank[:, at : at + half],
                     lhsT=h_code[(b, "q")][:, queries].bitcast(FP8X4),
                     lhsT_scale=h_scale[(b, "q")][:, queries],
                     rhs=h_code[(b, "k")][:, keys].bitcast(FP8X4),
@@ -225,13 +230,12 @@ def tile_multiheadenergyattention_pa_t_kernel(tc, x, wk, wq, betas, out):
                     start=True,
                     stop=True,
                 )
-                at += width
 
         def shift_own(b, j):
             shifted[(b, j)] = rows.tile([P, N], F32, name="shifted", tag="shifted")
             nc.vector.scalar_tensor_tensor(
-                out=shifted[(b, j)][:, 0:P],
-                in0=banks[("a", b, j)][:, 0:P],
+                out=shifted[(b, j)][:, own_keys(j)],
+                in0=banks[("a", b, j)][:, own_keys(j)],
                 scalar=neg_beta[:, 0:1],
                 in1=mask[:],
                 op0=ALU.mult,
@@ -241,8 +245,8 @@ def tile_multiheadenergyattention_pa_t_kernel(tc, x, wk, wq, betas, out):
         def shift_others(b, j):
             c = b * NT + j
             nc.vector.tensor_scalar(
-                out=shifted[(b, j)][:, P:N],
-                in0=banks[("a", b, j)][:, P:N],
+                out=shifted[(b, j)][:, other_keys(j)],
+                in0=banks[("a", b, j)][:, other_keys(j)],
                 scalar1=neg_beta[:, 0:1],
                 scalar2=None,
                 op0=ALU.mult,
@@ -254,7 +258,7 @@ def tile_multiheadenergyattention_pa_t_kernel(tc, x, wk, wq, betas, out):
             c = b * NT + j
             nc.vector.tensor_scalar(
                 out=unread_v[:],
-                in0=shifted[(b, j)][:, 0:P],
+                in0=shifted[(b, j)][:, own_keys(j)],
                 scalar1=1.0,
                 scalar2=others_min[:, c : c + 1],
                 op0=ALU.mult,
@@ -290,205 +294,148 @@ def tile_multiheadenergyattention_pa_t_kernel(tc, x, wk, wq, betas, out):
             )
             nc.sync.dma_start(out=out.rearrange("b o (j p) -> (b o j) p", p=P), in_=energy[0:ROW_TILES, :])
 
+        run = {
+            "flip_w": flip_weights,
+            "flip_x": flip_tokens,
+            "project": project,
+            "scores": scores,
+            "lay_w": regroup_weights,
+            "lay_x": regroup_tokens,
+            "lay_h": regroup_heads,
+            "quant_w": quantise_weights,
+            "quant_x": quantise_tokens,
+            "quant_k": quantise_keys,
+            "quant_q": quantise_queries,
+            "own": shift_own,
+            "others": shift_others,
+            "fold": fold_min,
+            "exp": exp_sum,
+        }
 
-        for r in range(WARM_UP):
-            idle_matmul(BANK)
-        for t in range(NT):
-            flip_weights("k", t)
-            idle_matmul(BANK // 2)
-        for t in range(NT):
-            regroup_weights("k", t, VECTOR)
-        for j in range(NT):
-            flip_tokens(0, j)
-            idle_matmul(BANK // 2)
-        regroup_tokens(0, 0, VECTOR)
-        for j in (1, 2, 3):
-            regroup_tokens(0, j, SCALAR)
-        for t in range(NT):
-            quantise_weights("k", t)
-        for j in range(NT):
-            quantise_tokens(0, j)
-        for t in (0, 1):
-            flip_weights("q", t)
-            idle_matmul(BANK // 2)
-        project(0, "k", 0)
-        project(0, "k", 1)
-        for t in (2, 3):
-            flip_weights("q", t)
-        project(0, "k", 2)
-        project(0, "k", 3)
-        for t in (0, 1):
-            regroup_weights("q", t, SCALAR)
-        for t in (0, 1):
-            quantise_weights("q", t)
-        for j in (0, 1):
-            regroup_heads(0, "k", j, SCALAR)
-        regroup_weights("q", 2, VECTOR)
-        regroup_weights("q", 3, SCALAR)
-        for t in (2, 3):
-            quantise_weights("q", t)
-        for j in (2, 3):
-            regroup_heads(0, "k", j, SCALAR)
-        for j in range(NT):
-            flip_tokens(1, j)
-        for j in (0, 1, 2):
-            regroup_tokens(1, j, VECTOR)
-        regroup_tokens(1, 3, SCALAR)
-        for j in range(NT):
-            project(0, "q", j)
-        for j in range(NT):
-            quantise_tokens(1, j)
-        quantise_keys(0)
-        beta_columns()
-        for j in (0, 1, 2):
-            regroup_heads(0, "q", j, SCALAR)
+        def bank_readers(step):
+            kind = step[0]
+            if kind in ("flip_w", "flip_x"):
+                return [("lay" + kind[4:],) + step[1:3]]
+            if kind == "project":
+                return [("lay_h",) + step[1:]]
+            return [("own",) + step[1:], ("others",) + step[1:]]
 
-        def period_start(n):
+        def needs(step):
+            kind = step[0]
+            if kind in ("lay_w", "lay_x"):
+                return [("flip" + kind[3:],) + step[1:3]]
+            if kind in ("quant_w", "quant_x"):
+                return [("lay" + kind[5:],) + step[1:3]]
+            if kind == "project":
+                b, w, j = step[1:]
+                return [("quant_w", w, t) for t in range(NT)] + [("quant_x", b, j)]
+            if kind == "lay_h":
+                return [("project",) + step[1:]]
+            if kind == "quant_k":
+                return [("lay_h", step[1], "k", j) for j in range(NT)]
+            if kind == "quant_q":
+                return [("lay_h", step[1], "q", step[2])]
+            if kind == "scores":
+                return [("quant_k", step[1]), ("quant_q",) + step[1:]]
+            if kind == "own":
+                c = step[1] * NT + step[2]
+                late = [("exp", (c - ROW_SLOTS) // NT, (c - ROW_SLOTS) % NT)] if c >= ROW_SLOTS else []
+                return [("scores",) + step[1:]] + late
+            if kind == "others":
+                return [("own",) + step[1:]]
+            if kind == "fold":
+                return [("own",) + step[1:], ("others",) + step[1:]]
+            if kind == "exp":
+                return [("fold",) + step[1:]]
+            return []
+
+        def weave(queues):
+            done = set()
+            filled = []
+            at = {engine: 0 for engine in queues}
+            for turn in range(sum(len(queues[engine]) for engine in queues)):
+                for engine in queues:
+                    if at[engine] == len(queues[engine]):
+                        continue
+                    step = queues[engine][at[engine]]
+                    name = step[:3] if step[0] in ("flip_w", "flip_x") else step
+                    wanted = needs(step)
+                    if engine == TENSOR and len(filled) >= BANKS:
+                        wanted = wanted + bank_readers(filled[len(filled) - BANKS])
+                    if not all(n in done for n in wanted):
+                        continue
+                    if step[0] in ("lay_w", "lay_x", "lay_h"):
+                        run[step[0]](*step[1:], engine)
+                    else:
+                        run[step[0]](*step[1:])
+                    if engine == TENSOR:
+                        filled.append(step)
+                    done.add(name)
+                    at[engine] += 1
+            assert all(at[engine] == len(queues[engine]) for engine in queues)
+
+        t_list, v_list, s_list = [], [], []
+        last = NB - 1
+
+        t_list += [("flip_w", "k", 0) + (BANK,) * WARM_UP, ("flip_w", "k", 1), ("flip_w", "k", 2, BANK), ("flip_w", "k", 3)]
+        t_list += [("flip_x", 0, 0, BANK), ("flip_x", 0, 1), ("flip_x", 0, 2, BANK), ("flip_x", 0, 3)]
+        t_list += [("project", 0, "k", 0), ("project", 0, "k", 1)]
+        t_list += [("flip_w", "q", 0), ("flip_w", "q", 1), ("flip_w", "q", 2)]
+        t_list += [("project", 0, "k", 2), ("project", 0, "k", 3)]
+        t_list += [("flip_w", "q", 3)]
+        s_list += [("lay_w", "k", 0), ("lay_w", "k", 2), ("lay_x", 0, 0), ("lay_x", 0, 1), ("lay_x", 0, 2)]
+        v_list += [("lay_w", "k", 1), ("quant_w", "k", 0), ("lay_w", "k", 3), ("quant_w", "k", 1)]
+        v_list += [("quant_w", "k", 2), ("quant_w", "k", 3), ("quant_x", 0, 0), ("quant_x", 0, 1), ("lay_x", 0, 3)]
+        v_list += [("quant_x", 0, 2), ("quant_x", 0, 3)]
+        s_list += [("lay_h", 0, "k", 0), ("lay_w", "q", 0), ("lay_h", 0, "k", 1), ("lay_w", "q", 2)]
+        v_list += [("lay_w", "q", 1), ("quant_w", "q", 0), ("quant_w", "q", 1), ("quant_w", "q", 2), ("lay_w", "q", 3)]
+        s_list += [("lay_h", 0, "k", 2), ("lay_x", 1, 0), ("lay_h", 0, "k", 3)]
+        v_list += [("quant_w", "q", 3)]
+        t_list += [("flip_x", 1, j) for j in range(NT)]
+        t_list += [("project", 0, "q", j) for j in range(NT)]
+        v_list += [("lay_x", 1, j) for j in (1, 2, 3)] + [("quant_x", 1, j) for j in range(NT)] + [("quant_k", 0)]
+        s_list += [("lay_h", 0, "q", j) for j in (0, 1, 2)]
+
+        for n in range(2, NB):
             i = n - 1
             p = n - 2
-            for j in range(NT):
-                flip_tokens(n, j)
+            t_list += [("flip_x", n, j) for j in range(NT)]
+            t_list += [("project", i, "k", 0), ("project", i, "k", 1), ("project", i, "k", 2), ("scores", p, 0)]
+            t_list += [("project", i, "k", 3), ("scores", p, 1), ("project", i, "q", 0), ("scores", p, 2)]
+            t_list += [("project", i, "q", 1), ("scores", p, 3), ("project", i, "q", 2), ("project", i, "q", 3)]
             if p > 0:
-                fold_min(p - 1, 2)
-                exp_sum(p - 1, 1)
-            quantise_queries(p, 0)
+                v_list += [("fold", p - 1, 2)]
+                s_list += [("exp", p - 1, 1)]
+            v_list += [("quant_q", p, 0)]
             if p > 0:
-                fold_min(p - 1, 3)
-            regroup_tokens(n, 0, VECTOR)
-            regroup_heads(p, "q", 3, SCALAR)
-            quantise_queries(p, 1)
+                v_list += [("fold", p - 1, 3)]
+            v_list += [("lay_x", n, 0), ("quant_q", p, 1), ("lay_x", n, 1), ("lay_x", n, 2), ("quant_q", p, 2), ("quant_q", p, 3)]
+            s_list += [("lay_h", p, "q", 3)]
             if p > 0:
-                exp_sum(p - 1, 2)
-            regroup_tokens(n, 1, VECTOR)
-            if p > 0:
-                exp_sum(p - 1, 3)
-            regroup_tokens(n, 2, VECTOR)
-            regroup_tokens(n, 3, SCALAR)
-            quantise_queries(p, 2)
-            quantise_queries(p, 3)
-            for j in (0, 1, 2):
-                project(i, "k", j)
-            for j in range(NT):
-                quantise_tokens(n, j)
-            regroup_heads(i, "k", 0, SCALAR)
-            regroup_heads(i, "k", 1, SCALAR)
-            scores(p, 0)
-            project(i, "k", 3)
-            scores(p, 1)
-            regroup_heads(i, "k", 2, SCALAR)
-            shift_own(p, 0)
-            shift_others(p, 0)
-            project(i, "q", 0)
-            regroup_heads(i, "k", 3, SCALAR)
-            scores(p, 2)
-            shift_own(p, 1)
-            shift_others(p, 1)
-            project(i, "q", 1)
-            regroup_heads(i, "q", 0, SCALAR)
-            fold_min(p, 0)
-            scores(p, 3)
-            shift_own(p, 2)
+                s_list += [("exp", p - 1, 2), ("exp", p - 1, 3)]
+            s_list += [("lay_x", n, 3)]
+            v_list += [("quant_x", n, j) for j in range(NT)]
+            s_list += [("lay_h", i, "k", j) for j in range(NT)]
+            s_list += [("lay_h", i, "q", 0)]
+            v_list += [("own", p, 0), ("others", p, 0), ("own", p, 1), ("others", p, 1), ("fold", p, 0), ("own", p, 2), ("others", p, 2)]
+            s_list += [("exp", p, 0)]
+            v_list += [("fold", p, 1), ("quant_k", i), ("own", p, 3), ("others", p, 3)]
+            s_list += [("lay_h", i, "q", 1), ("lay_h", i, "q", 2)]
 
-        for n in range(2, NB - 1):
-            i = n - 1
-            p = n - 2
-            period_start(n)
-            shift_others(p, 2)
-            project(i, "q", 2)
-            exp_sum(p, 0)
-            fold_min(p, 1)
-            quantise_keys(i)
-            regroup_heads(i, "q", 1, SCALAR)
-            project(i, "q", 3)
-            shift_own(p, 3)
-            regroup_heads(i, "q", 2, SCALAR)
-            shift_others(p, 3)
+        i = last
+        p = last - 1
+        t_list += [("project", i, "k", 0), ("scores", p, 0), ("project", i, "k", 1), ("scores", p, 1)]
+        t_list += [("project", i, "k", 2), ("scores", p, 2), ("project", i, "k", 3), ("scores", p, 3)]
+        t_list += [("project", i, "q", j) for j in range(NT)]
+        t_list += [("scores", i, j) for j in range(NT)]
+        s_list += [("lay_h", p, "q", 3), ("exp", p - 1, 1), ("exp", p - 1, 2), ("lay_h", i, "k", 1), ("exp", p - 1, 3), ("lay_h", i, "k", 3)]
+        v_list += [("quant_q", p, 0), ("quant_q", p, 1), ("fold", p - 1, 2), ("quant_q", p, 2), ("lay_h", i, "k", 0), ("quant_q", p, 3), ("fold", p - 1, 3)]
+        v_list += [("own", p, 0), ("others", p, 0), ("own", p, 1), ("others", p, 1), ("lay_h", i, "k", 2), ("fold", p, 0), ("own", p, 2), ("others", p, 2)]
+        v_list += [("lay_h", i, "q", 0), ("quant_k", i), ("quant_q", i, 0), ("own", p, 3), ("others", p, 3)]
+        s_list += [("exp", p, 0), ("lay_h", i, "q", 1), ("lay_h", i, "q", 2), ("lay_h", i, "q", 3)]
+        v_list += [("quant_q", i, 1), ("fold", p, 1), ("quant_q", i, 2), ("fold", p, 2), ("own", i, 0), ("others", i, 0), ("quant_q", i, 3), ("fold", p, 3), ("fold", i, 0)]
+        v_list += [("own", i, 1), ("others", i, 1), ("own", i, 2), ("others", i, 2), ("fold", i, 1), ("own", i, 3), ("fold", i, 2), ("others", i, 3), ("fold", i, 3)]
+        s_list += [("exp", p, j) for j in (1, 2, 3)] + [("exp", i, j) for j in range(NT)]
 
-        i = NB - 2
-        p = NB - 3
-        period_start(NB - 1)
-        quantise_keys(i)
-        project(i, "q", 2)
-        exp_sum(p, 0)
-        quantise_queries(i, 0)
-        shift_others(p, 2)
-        regroup_heads(i, "q", 1, SCALAR)
-        project(i, "q", 3)
-        fold_min(p, 1)
-        regroup_heads(i, "q", 2, SCALAR)
-        shift_own(p, 3)
-        shift_others(p, 3)
-
-        i = NB - 1
-        p = NB - 2
-        project(i, "k", 0)
-        regroup_heads(p, "q", 3, SCALAR)
-        quantise_queries(p, 1)
-        scores(p, 0)
-        fold_min(p - 1, 2)
-        project(i, "k", 1)
-        quantise_queries(p, 2)
-        exp_sum(p - 1, 1)
-        regroup_heads(i, "k", 0, VECTOR)
-        scores(p, 1)
-        exp_sum(p - 1, 2)
-        quantise_queries(p, 3)
-        project(i, "k", 2)
-        fold_min(p - 1, 3)
-        shift_own(p, 0)
-        shift_others(p, 0)
-        regroup_heads(i, "k", 1, SCALAR)
-        scores(p, 2)
-        shift_own(p, 1)
-        project(i, "k", 3)
-        exp_sum(p - 1, 3)
-        shift_others(p, 1)
-        regroup_heads(i, "k", 2, VECTOR)
-        scores(p, 3)
-        project(i, "q", 0)
-        regroup_heads(i, "k", 3, SCALAR)
-        fold_min(p, 0)
-        shift_own(p, 2)
-        shift_others(p, 2)
-        project(i, "q", 1)
-        exp_sum(p, 0)
-        regroup_heads(i, "q", 0, VECTOR)
-        project(i, "q", 2)
-        quantise_keys(i)
-        regroup_heads(i, "q", 1, SCALAR)
-        project(i, "q", 3)
-        quantise_queries(i, 0)
-        regroup_heads(i, "q", 2, SCALAR)
-        shift_own(p, 3)
-        shift_others(p, 3)
-        scores(i, 0)
-        regroup_heads(i, "q", 3, SCALAR)
-        quantise_queries(i, 1)
-        fold_min(p, 1)
-        quantise_queries(i, 2)
-        fold_min(p, 2)
-        scores(i, 1)
-        shift_own(i, 0)
-        exp_sum(p, 1)
-        shift_others(i, 0)
-        scores(i, 2)
-        quantise_queries(i, 3)
-        exp_sum(p, 2)
-        fold_min(p, 3)
-        fold_min(i, 0)
-        shift_own(i, 1)
-        scores(i, 3)
-        shift_others(i, 1)
-        exp_sum(p, 3)
-        shift_own(i, 2)
-        shift_others(i, 2)
-        exp_sum(i, 0)
-        fold_min(i, 1)
-        shift_own(i, 3)
-        fold_min(i, 2)
-        shift_others(i, 3)
-        exp_sum(i, 1)
-        exp_sum(i, 2)
-        fold_min(i, 3)
-        exp_sum(i, 3)
+        weave({TENSOR: t_list, VECTOR: v_list, SCALAR: s_list})
         finish()

@@ -24,7 +24,9 @@ FLOPS = 2 * NB * N * D * 2 * Z + 2 * NB * N * N * Z
 MASKED = 1.0e9
 LOWEST = 3.0e38
 ROW_SLOTS = 6
+TURNS = 4
 TENSOR = "tensor"
+MASK_ROOT = 2.0**50
 VECTOR = "vector"
 SCALAR = "scalar"
 WARM_UP = 5
@@ -60,10 +62,11 @@ def tile_multiheadenergyattention_pa_t_kernel(tc, x, wk, wq, betas, out):
         load_weights("q")
         for j in range(NT):
             nc.sync.dma_start(out=x_raw[1][:, j, :], in_=x[1, j * P : (j + 1) * P, :])
+        beta_bf = keep.tile([P, 1], BF16, name="beta_bf")
         for b in range(2, NB):
             nc.sync.dma_start(out=x_raw[b][:], in_=x[b, :, :].rearrange("(j p) d -> p j d", p=P))
-        beta_bf = keep.tile([P, 1], BF16, name="beta_bf")
-        nc.scalar.dma_start(out=beta_bf[:], in_=betas.partition_broadcast(P))
+            if b == 2:
+                nc.sync.dma_start(out=beta_bf[:], in_=betas.partition_broadcast(P))
 
         zeros = keep.tile([P, BANK], BF16, name="zeros")
         nc.vector.memset(zeros[:], 0.0)
@@ -77,13 +80,35 @@ def tile_multiheadenergyattention_pa_t_kernel(tc, x, wk, wq, betas, out):
         nc.vector.scalar_tensor_tensor(
             out=mask[:], in0=ident[:], scalar=MASKED, in1=off_diag[:], op0=ALU.mult, op1=ALU.add
         )
+        m_grp = {}
+        m_code = {}
+        m_scale = {}
+        for side, root in (("q", MASK_ROOT), ("k", -MASK_ROOT)):
+            m_grp[side] = keep.tile([P, P, 4], BF16, name="m_grp_" + side, align_bytes=64)
+            m_code[side] = keep.tile([P, P], U32, name="m_code_" + side, align_bytes=64)
+            m_scale[side] = keep.tile([P, P], U8, name="m_scale_" + side, align_bytes=64)
+            nc.gpsimd.memset(m_grp[side][:], 0.0)
+            nc.vector.tensor_scalar(
+                out=m_grp[side][:, :, 0], in0=ident[:], scalar1=root, scalar2=None, op0=ALU.mult
+            )
+        for side in ("q", "k"):
+            nc.vector.quantize_mx(
+                out=m_code[side][:].bitcast(FP8X4),
+                scales=m_scale[side][:],
+                in_=m_grp[side][:].rearrange("p n t -> p (n t)"),
+            )
         neg_top = keep.tile([P, P], F32, name="neg_top")
         nc.vector.memset(neg_top[:], 0.0)
         sums = keep.tile([P, P], F32, name="sums")
         nc.vector.memset(sums[:], 1.0)
         others_min = keep.tile([P, ROW_TILES], F32, name="others_min")
-        unread_v = keep.tile([P, P], F32, name="unread_v")
-        unread_s = keep.tile([P, N], BF16, name="unread_s")
+        unread_v = []
+        unread_s = []
+        unread_w = []
+        for r in range(TURNS):
+            unread_v.append(keep.tile([P, P], F32, name="unread_v_%d" % r))
+            unread_s.append(keep.tile([P, N], BF16, name="unread_s_%d" % r))
+            unread_w.append(keep.tile([P, N], BF16, name="unread_w_%d" % r))
         beta_f = keep.tile([P, 1], F32, name="beta_f")
         neg_beta = keep.tile([P, 1], F32, name="neg_beta")
         inv_beta = keep.tile([P, 1], F32, name="inv_beta")
@@ -94,8 +119,6 @@ def tile_multiheadenergyattention_pa_t_kernel(tc, x, wk, wq, betas, out):
             nc.vector.tensor_scalar(out=neg_beta[:], in0=beta_bf[:], scalar1=-1.0, scalar2=None, op0=ALU.mult)
             nc.vector.reciprocal(out=inv_beta[:], in_=beta_f[:])
             nc.vector.tensor_scalar(out=neg_inv_beta[:], in0=inv_beta[:], scalar1=-1.0, scalar2=None, op0=ALU.mult)
-
-        beta_columns()
 
         w_grp = {}
         w_code = {}
@@ -257,7 +280,7 @@ def tile_multiheadenergyattention_pa_t_kernel(tc, x, wk, wq, betas, out):
         def fold_min(b, j):
             c = b * NT + j
             nc.vector.tensor_scalar(
-                out=unread_v[:],
+                out=unread_v[c % TURNS][:],
                 in0=shifted[(b, j)][:, own_keys(j)],
                 scalar1=1.0,
                 scalar2=others_min[:, c : c + 1],
@@ -266,10 +289,55 @@ def tile_multiheadenergyattention_pa_t_kernel(tc, x, wk, wq, betas, out):
                 accum_out=neg_top[:, c : c + 1],
             )
 
+        def masked_scores(b, j):
+            bank = new_bank(("a", b, j))
+            own = slice(j * P, (j + 1) * P)
+            nc.tensor.matmul_mx(
+                out=bank[:],
+                lhsT=h_code[(b, "q")][:, own].bitcast(FP8X4),
+                lhsT_scale=h_scale[(b, "q")][:, own],
+                rhs=h_code[(b, "k")][:].bitcast(FP8X4),
+                rhs_scale=h_scale[(b, "k")][:],
+                start=True,
+                stop=False,
+            )
+            nc.tensor.matmul_mx(
+                out=bank[:, own],
+                lhsT=m_code["q"][:].bitcast(FP8X4),
+                lhsT_scale=m_scale["q"][:],
+                rhs=m_code["k"][:].bitcast(FP8X4),
+                rhs_scale=m_scale["k"][:],
+                start=False,
+                stop=True,
+            )
+
+        def masked_top(b, j):
+            c = b * NT + j
+            nc.vector.tensor_scalar(
+                out=unread_w[c % TURNS][:],
+                in0=banks[("a", b, j)][:],
+                scalar1=neg_beta[:, 0:1],
+                scalar2=None,
+                op0=ALU.mult,
+                op1=ALU.min,
+                accum_out=neg_top[:, c : c + 1],
+            )
+
+        def masked_exp(b, j):
+            c = b * NT + j
+            nc.scalar.activation(
+                out=unread_s[c % TURNS][:],
+                in_=banks[("a", b, j)][:],
+                func=ACT.Exp,
+                bias=neg_top[:, c : c + 1],
+                scale=beta_f[:, 0:1],
+                accum_out=sums[:, c : c + 1],
+            )
+
         def exp_sum(b, j):
             c = b * NT + j
             nc.scalar.activation(
-                out=unread_s[:],
+                out=unread_s[c % TURNS][:],
                 in_=shifted[(b, j)][:],
                 func=ACT.Exp,
                 bias=neg_top[:, c : c + 1],
@@ -309,6 +377,10 @@ def tile_multiheadenergyattention_pa_t_kernel(tc, x, wk, wq, betas, out):
             "own": shift_own,
             "others": shift_others,
             "fold": fold_min,
+            "m_scores": masked_scores,
+            "m_top": masked_top,
+            "m_exp": masked_exp,
+            "beta": beta_columns,
             "exp": exp_sum,
         }
 
@@ -318,6 +390,8 @@ def tile_multiheadenergyattention_pa_t_kernel(tc, x, wk, wq, betas, out):
                 return [("lay" + kind[4:],) + step[1:3]]
             if kind == "project":
                 return [("lay_h",) + step[1:]]
+            if kind == "m_scores":
+                return [("m_exp",) + step[1:]]
             return [("own",) + step[1:], ("others",) + step[1:]]
 
         def needs(step):
@@ -335,7 +409,11 @@ def tile_multiheadenergyattention_pa_t_kernel(tc, x, wk, wq, betas, out):
                 return [("lay_h", step[1], "k", j) for j in range(NT)]
             if kind == "quant_q":
                 return [("lay_h", step[1], "q", step[2])]
-            if kind == "scores":
+            if kind == "m_top":
+                return [("m_scores",) + step[1:]]
+            if kind == "m_exp":
+                return [("m_top",) + step[1:]]
+            if kind in ("scores", "m_scores"):
                 return [("quant_k", step[1]), ("quant_q",) + step[1:]]
             if kind == "own":
                 c = step[1] * NT + step[2]
@@ -393,7 +471,7 @@ def tile_multiheadenergyattention_pa_t_kernel(tc, x, wk, wq, betas, out):
         v_list += [("quant_w", "q", 3)]
         t_list += [("flip_x", 1, j) for j in range(NT)]
         t_list += [("project", 0, "q", j) for j in range(NT)]
-        v_list += [("lay_x", 1, j) for j in (1, 2, 3)] + [("quant_x", 1, j) for j in range(NT)] + [("quant_k", 0)]
+        v_list += [("lay_x", 1, j) for j in (1, 2, 3)] + [("quant_x", 1, j) for j in range(NT)] + [("quant_k", 0), ("beta",)]
         s_list += [("lay_h", 0, "q", j) for j in (0, 1, 2)]
 
         for n in range(2, NB):
@@ -424,18 +502,21 @@ def tile_multiheadenergyattention_pa_t_kernel(tc, x, wk, wq, betas, out):
 
         i = last
         p = last - 1
-        t_list += [("project", i, "k", 0), ("scores", p, 0), ("project", i, "k", 1), ("scores", p, 1)]
-        t_list += [("project", i, "k", 2), ("scores", p, 2), ("project", i, "k", 3), ("scores", p, 3)]
-        t_list += [("project", i, "q", j) for j in range(NT)]
-        t_list += [("scores", i, j) for j in range(NT)]
-        s_list += [("lay_h", p, "q", 3), ("exp", p - 1, 1), ("exp", p - 1, 2), ("lay_h", i, "k", 1), ("exp", p - 1, 3), ("lay_h", i, "k", 3)]
-        v_list += [("quant_q", p, 0), ("quant_q", p, 1), ("fold", p - 1, 2), ("quant_q", p, 2), ("lay_h", i, "k", 0), ("quant_q", p, 3), ("fold", p - 1, 3)]
-        v_list += [("own", p, 0), ("others", p, 0), ("own", p, 1), ("others", p, 1), ("lay_h", i, "k", 2), ("fold", p, 0), ("own", p, 2), ("others", p, 2)]
-        v_list += [("lay_h", i, "q", 0), ("quant_k", i), ("quant_q", i, 0), ("own", p, 3), ("others", p, 3)]
-        s_list += [("exp", p, 0), ("lay_h", i, "q", 1), ("lay_h", i, "q", 2), ("lay_h", i, "q", 3)]
-        v_list += [("quant_q", i, 1), ("fold", p, 1), ("quant_q", i, 2), ("fold", p, 2), ("own", i, 0), ("others", i, 0), ("quant_q", i, 3), ("fold", p, 3), ("fold", i, 0)]
-        v_list += [("own", i, 1), ("others", i, 1), ("own", i, 2), ("others", i, 2), ("fold", i, 1), ("own", i, 3), ("fold", i, 2), ("others", i, 3), ("fold", i, 3)]
-        s_list += [("exp", p, j) for j in (1, 2, 3)] + [("exp", i, j) for j in range(NT)]
+        t_list += [("project", i, "k", 0), ("project", i, "k", 1), ("m_scores", p, 0), ("project", i, "k", 2)]
+        t_list += [("m_scores", p, 1), ("project", i, "k", 3), ("m_scores", p, 2), ("project", i, "q", 0)]
+        t_list += [("m_scores", p, 3), ("project", i, "q", 1), ("project", i, "q", 2), ("project", i, "q", 3)]
+        t_list += [("m_scores", i, 0), ("m_scores", i, 1), ("m_scores", i, 2), ("m_scores", i, 3)]
+        v_list += [("quant_q", p, 0), ("quant_q", p, 1), ("fold", p - 1, 2), ("quant_q", p, 2)]
+        v_list += [("lay_h", i, "k", 0), ("quant_q", p, 3), ("fold", p - 1, 3), ("m_top", p, 0)]
+        v_list += [("lay_h", i, "k", 2), ("m_top", p, 1), ("m_top", p, 2), ("quant_k", i)]
+        v_list += [("lay_h", i, "q", 1), ("quant_q", i, 0), ("m_top", p, 3), ("quant_q", i, 1)]
+        v_list += [("m_top", i, 0), ("quant_q", i, 2), ("m_top", i, 1), ("quant_q", i, 3)]
+        v_list += [("m_top", i, 2), ("m_top", i, 3)]
+        s_list += [("lay_h", p, "q", 3), ("exp", p - 1, 1), ("lay_h", i, "k", 1), ("exp", p - 1, 2)]
+        s_list += [("exp", p - 1, 3), ("lay_h", i, "k", 3), ("m_exp", p, 0), ("lay_h", i, "q", 0)]
+        s_list += [("m_exp", p, 1), ("lay_h", i, "q", 2), ("m_exp", p, 2), ("lay_h", i, "q", 3)]
+        s_list += [("m_exp", p, 3), ("m_exp", i, 0), ("m_exp", i, 1), ("m_exp", i, 2)]
+        s_list += [("m_exp", i, 3)]
 
         weave({TENSOR: t_list, VECTOR: v_list, SCALAR: s_list})
         finish()

@@ -29,7 +29,8 @@ TENSOR = "tensor"
 MASK_ROOT = 2.0**50
 VECTOR = "vector"
 SCALAR = "scalar"
-WARM_UP = 5
+WARM_UP = 4
+IDLE = 320
 BANKS = 8
 
 
@@ -428,6 +429,8 @@ def tile_multiheadenergyattention_pa_t_kernel(tc, x, wk, wq, betas, out):
             return []
 
         def weave(queues):
+            for engine in queues:
+                queues[engine] = [step for step in queues[engine] if len(step) < 2 or step[1] not in (-1,)]
             done = set()
             filled = []
             at = {engine: 0 for engine in queues}
@@ -455,8 +458,8 @@ def tile_multiheadenergyattention_pa_t_kernel(tc, x, wk, wq, betas, out):
         t_list, v_list, s_list = [], [], []
         last = NB - 1
 
-        t_list += [("flip_w", "k", 0) + (BANK,) * WARM_UP, ("flip_w", "k", 1), ("flip_w", "k", 2, BANK), ("flip_w", "k", 3)]
-        t_list += [("flip_x", 0, 0, BANK), ("flip_x", 0, 1), ("flip_x", 0, 2, BANK), ("flip_x", 0, 3)]
+        t_list += [("flip_w", "k", 0) + (BANK,) * WARM_UP] + [("flip_w", "k", t, IDLE) for t in (1, 2, 3)]
+        t_list += [("flip_x", 0, j, IDLE) for j in range(NT)]
         t_list += [("project", 0, "k", 0), ("project", 0, "k", 1)]
         t_list += [("flip_w", "q", 0), ("flip_w", "q", 1), ("flip_w", "q", 2)]
         t_list += [("project", 0, "k", 2), ("project", 0, "k", 3)]
@@ -474,31 +477,90 @@ def tile_multiheadenergyattention_pa_t_kernel(tc, x, wk, wq, betas, out):
         v_list += [("lay_x", 1, j) for j in (1, 2, 3)] + [("quant_x", 1, j) for j in range(NT)] + [("quant_k", 0), ("beta",)]
         s_list += [("lay_h", 0, "q", j) for j in (0, 1, 2)]
 
-        for n in range(2, NB):
-            i = n - 1
-            p = n - 2
-            t_list += [("flip_x", n, j) for j in range(NT)]
-            t_list += [("project", i, "k", 0), ("project", i, "k", 1), ("project", i, "k", 2), ("scores", p, 0)]
-            t_list += [("project", i, "k", 3), ("scores", p, 1), ("project", i, "q", 0), ("scores", p, 2)]
-            t_list += [("project", i, "q", 1), ("scores", p, 3), ("project", i, "q", 2), ("project", i, "q", 3)]
-            if p > 0:
-                v_list += [("fold", p - 1, 2)]
-                s_list += [("exp", p - 1, 1)]
-            v_list += [("quant_q", p, 0)]
-            if p > 0:
-                v_list += [("fold", p - 1, 3)]
-            v_list += [("lay_x", n, 0), ("quant_q", p, 1), ("lay_x", n, 1), ("lay_x", n, 2), ("quant_q", p, 2), ("quant_q", p, 3)]
-            s_list += [("lay_h", p, "q", 3)]
-            if p > 0:
-                s_list += [("exp", p - 1, 2), ("exp", p - 1, 3)]
-            s_list += [("lay_x", n, 3)]
-            v_list += [("quant_x", n, j) for j in range(NT)]
-            s_list += [("lay_h", i, "k", j) for j in range(NT)]
-            s_list += [("lay_h", i, "q", 0)]
-            v_list += [("own", p, 0), ("others", p, 0), ("own", p, 1), ("others", p, 1), ("fold", p, 0), ("own", p, 2), ("others", p, 2)]
-            s_list += [("exp", p, 0)]
-            v_list += [("fold", p, 1), ("quant_k", i), ("own", p, 3), ("others", p, 3)]
-            s_list += [("lay_h", i, "q", 1), ("lay_h", i, "q", 2)]
+        t_list += [("flip_x", 2, 0), ("flip_x", 2, 1), ("flip_x", 2, 2), ("flip_x", 2, 3)]
+        t_list += [("project", 1, "k", 0), ("project", 1, "k", 1), ("project", 1, "k", 2), ("scores", 0, 0)]
+        t_list += [("project", 1, "k", 3), ("scores", 0, 1), ("project", 1, "q", 0), ("scores", 0, 2)]
+        t_list += [("project", 1, "q", 1), ("scores", 0, 3), ("project", 1, "q", 2), ("project", 1, "q", 3)]
+        v_list += [("quant_q", 0, 0), ("fold", -1, 2), ("lay_x", 2, 0), ("quant_q", 0, 1)]
+        v_list += [("fold", -1, 3), ("lay_x", 2, 1), ("lay_x", 2, 2), ("quant_q", 0, 2)]
+        v_list += [("quant_q", 0, 3), ("quant_x", 2, 0), ("quant_x", 2, 1), ("quant_x", 2, 2)]
+        v_list += [("quant_x", 2, 3), ("own", 0, 0), ("others", 0, 0), ("own", 0, 1)]
+        v_list += [("others", 0, 1), ("fold", 0, 0), ("own", 0, 2), ("others", 0, 2)]
+        v_list += [("fold", 0, 1), ("quant_k", 1), ("own", 0, 3), ("others", 0, 3)]
+        s_list += [("lay_h", 0, "q", 3), ("exp", -1, 1), ("exp", -1, 2), ("exp", -1, 3)]
+        s_list += [("lay_x", 2, 3), ("lay_h", 1, "k", 0), ("lay_h", 1, "k", 1), ("lay_h", 1, "k", 2)]
+        s_list += [("lay_h", 1, "k", 3), ("lay_h", 1, "q", 0), ("exp", 0, 0), ("lay_h", 1, "q", 1)]
+        s_list += [("lay_h", 1, "q", 2)]
+        t_list += [("flip_x", 3, 0), ("flip_x", 3, 1), ("flip_x", 3, 2), ("flip_x", 3, 3)]
+        t_list += [("project", 2, "k", 0), ("project", 2, "k", 1), ("project", 2, "k", 2), ("scores", 1, 0)]
+        t_list += [("project", 2, "k", 3), ("scores", 1, 1), ("project", 2, "q", 0), ("scores", 1, 2)]
+        t_list += [("project", 2, "q", 1), ("scores", 1, 3), ("project", 2, "q", 2), ("project", 2, "q", 3)]
+        v_list += [("quant_q", 1, 0), ("fold", 0, 2), ("lay_x", 3, 0), ("quant_q", 1, 1)]
+        v_list += [("fold", 0, 3), ("lay_x", 3, 1), ("lay_x", 3, 2), ("quant_q", 1, 2)]
+        v_list += [("quant_q", 1, 3), ("quant_x", 3, 0), ("quant_x", 3, 1), ("quant_x", 3, 2)]
+        v_list += [("quant_x", 3, 3), ("own", 1, 0), ("others", 1, 0), ("own", 1, 1)]
+        v_list += [("others", 1, 1), ("fold", 1, 0), ("own", 1, 2), ("others", 1, 2)]
+        v_list += [("fold", 1, 1), ("quant_k", 2), ("own", 1, 3), ("others", 1, 3)]
+        s_list += [("lay_h", 1, "q", 3), ("exp", 0, 1), ("exp", 0, 2), ("exp", 0, 3)]
+        s_list += [("lay_x", 3, 3), ("lay_h", 2, "k", 0), ("lay_h", 2, "k", 1), ("lay_h", 2, "k", 2)]
+        s_list += [("lay_h", 2, "k", 3), ("lay_h", 2, "q", 0), ("exp", 1, 0), ("lay_h", 2, "q", 1)]
+        s_list += [("lay_h", 2, "q", 2)]
+        t_list += [("flip_x", 4, 0), ("flip_x", 4, 1), ("flip_x", 4, 2), ("flip_x", 4, 3)]
+        t_list += [("project", 3, "k", 0), ("project", 3, "k", 1), ("project", 3, "k", 2), ("scores", 2, 0)]
+        t_list += [("project", 3, "k", 3), ("scores", 2, 1), ("project", 3, "q", 0), ("scores", 2, 2)]
+        t_list += [("project", 3, "q", 1), ("scores", 2, 3), ("project", 3, "q", 2), ("project", 3, "q", 3)]
+        v_list += [("quant_q", 2, 0), ("fold", 1, 2), ("lay_x", 4, 0), ("quant_q", 2, 1)]
+        v_list += [("fold", 1, 3), ("lay_x", 4, 1), ("lay_x", 4, 2), ("quant_q", 2, 2)]
+        v_list += [("quant_q", 2, 3), ("quant_x", 4, 0), ("quant_x", 4, 1), ("quant_x", 4, 2)]
+        v_list += [("quant_x", 4, 3), ("own", 2, 0), ("others", 2, 0), ("own", 2, 1)]
+        v_list += [("others", 2, 1), ("fold", 2, 0), ("own", 2, 2), ("others", 2, 2)]
+        v_list += [("fold", 2, 1), ("quant_k", 3), ("own", 2, 3), ("others", 2, 3)]
+        s_list += [("lay_h", 2, "q", 3), ("exp", 1, 1), ("exp", 1, 2), ("exp", 1, 3)]
+        s_list += [("lay_x", 4, 3), ("lay_h", 3, "k", 0), ("lay_h", 3, "k", 1), ("lay_h", 3, "k", 2)]
+        s_list += [("lay_h", 3, "k", 3), ("lay_h", 3, "q", 0), ("exp", 2, 0), ("lay_h", 3, "q", 1)]
+        s_list += [("lay_h", 3, "q", 2)]
+        t_list += [("flip_x", 5, 0), ("flip_x", 5, 1), ("flip_x", 5, 2), ("flip_x", 5, 3)]
+        t_list += [("project", 4, "k", 0), ("project", 4, "k", 1), ("project", 4, "k", 2), ("scores", 3, 0)]
+        t_list += [("project", 4, "k", 3), ("scores", 3, 1), ("project", 4, "q", 0), ("scores", 3, 2)]
+        t_list += [("project", 4, "q", 1), ("scores", 3, 3), ("project", 4, "q", 2), ("project", 4, "q", 3)]
+        v_list += [("quant_q", 3, 0), ("fold", 2, 2), ("lay_x", 5, 0), ("quant_q", 3, 1)]
+        v_list += [("fold", 2, 3), ("lay_x", 5, 1), ("lay_x", 5, 2), ("quant_q", 3, 2)]
+        v_list += [("quant_q", 3, 3), ("quant_x", 5, 0), ("quant_x", 5, 1), ("quant_x", 5, 2)]
+        v_list += [("quant_x", 5, 3), ("own", 3, 0), ("others", 3, 0), ("own", 3, 1)]
+        v_list += [("others", 3, 1), ("fold", 3, 0), ("own", 3, 2), ("others", 3, 2)]
+        v_list += [("fold", 3, 1), ("quant_k", 4), ("own", 3, 3), ("others", 3, 3)]
+        s_list += [("lay_h", 3, "q", 3), ("exp", 2, 1), ("exp", 2, 2), ("exp", 2, 3)]
+        s_list += [("lay_x", 5, 3), ("lay_h", 4, "k", 0), ("lay_h", 4, "k", 1), ("lay_h", 4, "k", 2)]
+        s_list += [("lay_h", 4, "k", 3), ("lay_h", 4, "q", 0), ("exp", 3, 0), ("lay_h", 4, "q", 1)]
+        s_list += [("lay_h", 4, "q", 2)]
+        t_list += [("flip_x", 6, 0), ("flip_x", 6, 1), ("flip_x", 6, 2), ("flip_x", 6, 3)]
+        t_list += [("project", 5, "k", 0), ("project", 5, "k", 1), ("project", 5, "k", 2), ("scores", 4, 0)]
+        t_list += [("project", 5, "k", 3), ("scores", 4, 1), ("project", 5, "q", 0), ("scores", 4, 2)]
+        t_list += [("project", 5, "q", 1), ("scores", 4, 3), ("project", 5, "q", 2), ("project", 5, "q", 3)]
+        v_list += [("quant_q", 4, 0), ("fold", 3, 2), ("lay_x", 6, 0), ("quant_q", 4, 1)]
+        v_list += [("fold", 3, 3), ("lay_x", 6, 1), ("lay_x", 6, 2), ("quant_q", 4, 2)]
+        v_list += [("quant_q", 4, 3), ("quant_x", 6, 0), ("quant_x", 6, 1), ("quant_x", 6, 2)]
+        v_list += [("quant_x", 6, 3), ("own", 4, 0), ("others", 4, 0), ("own", 4, 1)]
+        v_list += [("others", 4, 1), ("fold", 4, 0), ("own", 4, 2), ("others", 4, 2)]
+        v_list += [("fold", 4, 1), ("quant_k", 5), ("own", 4, 3), ("others", 4, 3)]
+        s_list += [("lay_h", 4, "q", 3), ("exp", 3, 1), ("exp", 3, 2), ("exp", 3, 3)]
+        s_list += [("lay_x", 6, 3), ("lay_h", 5, "k", 0), ("lay_h", 5, "k", 1), ("lay_h", 5, "k", 2)]
+        s_list += [("lay_h", 5, "k", 3), ("lay_h", 5, "q", 0), ("exp", 4, 0), ("lay_h", 5, "q", 1)]
+        s_list += [("lay_h", 5, "q", 2)]
+        t_list += [("flip_x", 7, 0), ("flip_x", 7, 1), ("flip_x", 7, 2), ("flip_x", 7, 3)]
+        t_list += [("project", 6, "k", 0), ("project", 6, "k", 1), ("project", 6, "k", 2), ("scores", 5, 0)]
+        t_list += [("project", 6, "k", 3), ("scores", 5, 1), ("project", 6, "q", 0), ("scores", 5, 2)]
+        t_list += [("project", 6, "q", 1), ("scores", 5, 3), ("project", 6, "q", 2), ("project", 6, "q", 3)]
+        v_list += [("quant_q", 5, 0), ("fold", 4, 2), ("lay_x", 7, 0), ("quant_q", 5, 1)]
+        v_list += [("fold", 4, 3), ("lay_x", 7, 1), ("lay_x", 7, 2), ("quant_q", 5, 2)]
+        v_list += [("quant_q", 5, 3), ("quant_x", 7, 0), ("quant_x", 7, 1), ("quant_x", 7, 2)]
+        v_list += [("quant_x", 7, 3), ("own", 5, 0), ("others", 5, 0), ("own", 5, 1)]
+        v_list += [("others", 5, 1), ("fold", 5, 0), ("own", 5, 2), ("others", 5, 2)]
+        v_list += [("fold", 5, 1), ("quant_k", 6), ("own", 5, 3), ("others", 5, 3)]
+        s_list += [("lay_h", 5, "q", 3), ("exp", 4, 1), ("exp", 4, 2), ("exp", 4, 3)]
+        s_list += [("lay_x", 7, 3), ("lay_h", 6, "k", 0), ("lay_h", 6, "k", 1), ("lay_h", 6, "k", 2)]
+        s_list += [("lay_h", 6, "k", 3), ("lay_h", 6, "q", 0), ("exp", 5, 0), ("lay_h", 6, "q", 1)]
+        s_list += [("lay_h", 6, "q", 2)]
 
         i = last
         p = last - 1

@@ -102,12 +102,10 @@ def tile_multiheadenergyattention_pa_t_kernel(tc, x, wk, wq, betas, out):
         nc.vector.memset(neg_top[:], 0.0)
         sums = keep.tile([P, P], F32, name="sums")
         nc.vector.memset(sums[:], 1.0)
-        others_min = keep.tile([P, ROW_TILES], F32, name="others_min")
-        unread_v = []
+        own_min = keep.tile([P, ROW_TILES], F32, name="own_min")
         unread_s = []
         unread_w = []
         for r in range(TURNS):
-            unread_v.append(keep.tile([P, P], F32, name="unread_v_%d" % r))
             unread_s.append(keep.tile([P, N], BF16, name="unread_s_%d" % r))
             unread_w.append(keep.tile([P, N], BF16, name="unread_w_%d" % r))
         beta_f = keep.tile([P, 1], F32, name="beta_f")
@@ -266,25 +264,22 @@ def tile_multiheadenergyattention_pa_t_kernel(tc, x, wk, wq, betas, out):
                 op1=ALU.max,
             )
 
+        def least_own(b, j):
+            c = b * NT + j
+            nc.vector.tensor_reduce(
+                out=own_min[:, c : c + 1],
+                in_=shifted[(b, j)][:, own_keys(j)],
+                axis=mybir.AxisListType.X,
+                op=ALU.min,
+            )
+
         def shift_others(b, j):
             c = b * NT + j
             nc.vector.tensor_scalar(
                 out=shifted[(b, j)][:, other_keys(j)],
                 in0=banks[("a", b, j)][:, other_keys(j)],
                 scalar1=neg_beta[:, 0:1],
-                scalar2=None,
-                op0=ALU.mult,
-                op1=ALU.min,
-                accum_out=others_min[:, c : c + 1],
-            )
-
-        def fold_min(b, j):
-            c = b * NT + j
-            nc.vector.tensor_scalar(
-                out=unread_v[c % TURNS][:],
-                in0=shifted[(b, j)][:, own_keys(j)],
-                scalar1=1.0,
-                scalar2=others_min[:, c : c + 1],
+                scalar2=own_min[:, c : c + 1],
                 op0=ALU.mult,
                 op1=ALU.min,
                 accum_out=neg_top[:, c : c + 1],
@@ -377,7 +372,7 @@ def tile_multiheadenergyattention_pa_t_kernel(tc, x, wk, wq, betas, out):
             "quant_q": quantise_queries,
             "own": shift_own,
             "others": shift_others,
-            "fold": fold_min,
+            "least": least_own,
             "m_scores": masked_scores,
             "m_top": masked_top,
             "m_exp": masked_exp,
@@ -420,12 +415,12 @@ def tile_multiheadenergyattention_pa_t_kernel(tc, x, wk, wq, betas, out):
                 c = step[1] * NT + step[2]
                 late = [("exp", (c - ROW_SLOTS) // NT, (c - ROW_SLOTS) % NT)] if c >= ROW_SLOTS else []
                 return [("scores",) + step[1:]] + late
-            if kind == "others":
+            if kind == "least":
                 return [("own",) + step[1:]]
-            if kind == "fold":
-                return [("own",) + step[1:], ("others",) + step[1:]]
+            if kind == "others":
+                return [("least",) + step[1:]]
             if kind == "exp":
-                return [("fold",) + step[1:]]
+                return [("others",) + step[1:]]
             return []
 
         def weave(queues):
@@ -474,111 +469,43 @@ def tile_multiheadenergyattention_pa_t_kernel(tc, x, wk, wq, betas, out):
         v_list += [("quant_w", "q", 3)]
         t_list += [("flip_x", 1, j) for j in range(NT)]
         t_list += [("project", 0, "q", j) for j in range(NT)]
-        v_list += [("lay_x", 1, j) for j in (1, 2, 3)] + [("quant_x", 1, j) for j in range(NT)] + [("quant_k", 0), ("beta",)]
+        v_list += [("lay_x", 1, j) for j in (1, 2, 3)] + [("quant_x", 1, j) for j in range(NT)] + [("quant_k", 0), ("beta",), ("quant_q", 0, 0), ("quant_q", 0, 1)]
         s_list += [("lay_h", 0, "q", j) for j in (0, 1, 2)]
 
-        t_list += [("flip_x", 2, 0), ("flip_x", 2, 1), ("flip_x", 2, 2), ("flip_x", 2, 3)]
-        t_list += [("project", 1, "k", 0), ("project", 1, "k", 1), ("project", 1, "k", 2), ("scores", 0, 0)]
-        t_list += [("project", 1, "k", 3), ("scores", 0, 1), ("project", 1, "q", 0), ("scores", 0, 2)]
-        t_list += [("project", 1, "q", 1), ("scores", 0, 3), ("project", 1, "q", 2), ("project", 1, "q", 3)]
-        v_list += [("quant_q", 0, 0), ("fold", -1, 2), ("lay_x", 2, 0), ("quant_q", 0, 1)]
-        v_list += [("fold", -1, 3), ("lay_x", 2, 1), ("lay_x", 2, 2), ("quant_q", 0, 2)]
-        v_list += [("quant_q", 0, 3), ("quant_x", 2, 0), ("quant_x", 2, 1), ("quant_x", 2, 2)]
-        v_list += [("quant_x", 2, 3), ("own", 0, 0), ("others", 0, 0), ("own", 0, 1)]
-        v_list += [("others", 0, 1), ("fold", 0, 0), ("own", 0, 2), ("others", 0, 2)]
-        v_list += [("fold", 0, 1), ("quant_k", 1), ("own", 0, 3), ("others", 0, 3)]
-        s_list += [("lay_h", 0, "q", 3), ("exp", -1, 1), ("exp", -1, 2), ("exp", -1, 3)]
-        s_list += [("lay_x", 2, 3), ("lay_h", 1, "k", 0), ("lay_h", 1, "k", 1), ("lay_h", 1, "k", 2)]
-        s_list += [("lay_h", 1, "k", 3), ("lay_h", 1, "q", 0), ("exp", 0, 0), ("lay_h", 1, "q", 1)]
-        s_list += [("lay_h", 1, "q", 2)]
-        t_list += [("flip_x", 3, 0), ("flip_x", 3, 1), ("flip_x", 3, 2), ("flip_x", 3, 3)]
-        t_list += [("project", 2, "k", 0), ("project", 2, "k", 1), ("project", 2, "k", 2), ("scores", 1, 0)]
-        t_list += [("project", 2, "k", 3), ("scores", 1, 1), ("project", 2, "q", 0), ("scores", 1, 2)]
-        t_list += [("project", 2, "q", 1), ("scores", 1, 3), ("project", 2, "q", 2), ("project", 2, "q", 3)]
-        v_list += [("quant_q", 1, 0), ("fold", 0, 2), ("lay_x", 3, 0), ("quant_q", 1, 1)]
-        v_list += [("fold", 0, 3), ("lay_x", 3, 1), ("lay_x", 3, 2), ("quant_q", 1, 2)]
-        v_list += [("quant_q", 1, 3), ("quant_x", 3, 0), ("quant_x", 3, 1), ("quant_x", 3, 2)]
-        v_list += [("quant_x", 3, 3), ("own", 1, 0), ("others", 1, 0), ("own", 1, 1)]
-        v_list += [("others", 1, 1), ("fold", 1, 0), ("own", 1, 2), ("others", 1, 2)]
-        v_list += [("fold", 1, 1), ("quant_k", 2), ("own", 1, 3), ("others", 1, 3)]
-        s_list += [("lay_h", 1, "q", 3), ("exp", 0, 1), ("exp", 0, 2), ("exp", 0, 3)]
-        s_list += [("lay_x", 3, 3), ("lay_h", 2, "k", 0), ("lay_h", 2, "k", 1), ("lay_h", 2, "k", 2)]
-        s_list += [("lay_h", 2, "k", 3), ("lay_h", 2, "q", 0), ("exp", 1, 0), ("lay_h", 2, "q", 1)]
-        s_list += [("lay_h", 2, "q", 2)]
-        t_list += [("flip_x", 4, 0), ("flip_x", 4, 1), ("flip_x", 4, 2), ("flip_x", 4, 3)]
-        t_list += [("project", 3, "k", 0), ("project", 3, "k", 1), ("project", 3, "k", 2), ("scores", 2, 0)]
-        t_list += [("project", 3, "k", 3), ("scores", 2, 1), ("project", 3, "q", 0), ("scores", 2, 2)]
-        t_list += [("project", 3, "q", 1), ("scores", 2, 3), ("project", 3, "q", 2), ("project", 3, "q", 3)]
-        v_list += [("quant_q", 2, 0), ("fold", 1, 2), ("lay_x", 4, 0), ("quant_q", 2, 1)]
-        v_list += [("fold", 1, 3), ("lay_x", 4, 1), ("lay_x", 4, 2), ("quant_q", 2, 2)]
-        v_list += [("quant_q", 2, 3), ("quant_x", 4, 0), ("quant_x", 4, 1), ("quant_x", 4, 2)]
-        v_list += [("quant_x", 4, 3), ("own", 2, 0), ("others", 2, 0), ("own", 2, 1)]
-        v_list += [("others", 2, 1), ("fold", 2, 0), ("own", 2, 2), ("others", 2, 2)]
-        v_list += [("fold", 2, 1), ("quant_k", 3), ("own", 2, 3), ("others", 2, 3)]
-        s_list += [("lay_h", 2, "q", 3), ("exp", 1, 1), ("exp", 1, 2), ("exp", 1, 3)]
-        s_list += [("lay_x", 4, 3), ("lay_h", 3, "k", 0), ("lay_h", 3, "k", 1), ("lay_h", 3, "k", 2)]
-        s_list += [("lay_h", 3, "k", 3), ("lay_h", 3, "q", 0), ("exp", 2, 0), ("lay_h", 3, "q", 1)]
-        s_list += [("lay_h", 3, "q", 2)]
-        t_list += [("flip_x", 5, 0), ("flip_x", 5, 1), ("flip_x", 5, 2), ("flip_x", 5, 3)]
-        t_list += [("project", 4, "k", 0), ("project", 4, "k", 1), ("project", 4, "k", 2), ("scores", 3, 0)]
-        t_list += [("project", 4, "k", 3), ("scores", 3, 1), ("project", 4, "q", 0), ("scores", 3, 2)]
-        t_list += [("project", 4, "q", 1), ("scores", 3, 3), ("project", 4, "q", 2), ("project", 4, "q", 3)]
-        v_list += [("quant_q", 3, 0), ("fold", 2, 2), ("lay_x", 5, 0), ("quant_q", 3, 1)]
-        v_list += [("fold", 2, 3), ("lay_x", 5, 1), ("lay_x", 5, 2), ("quant_q", 3, 2)]
-        v_list += [("quant_q", 3, 3), ("quant_x", 5, 0), ("quant_x", 5, 1), ("quant_x", 5, 2)]
-        v_list += [("quant_x", 5, 3), ("own", 3, 0), ("others", 3, 0), ("own", 3, 1)]
-        v_list += [("others", 3, 1), ("fold", 3, 0), ("own", 3, 2), ("others", 3, 2)]
-        v_list += [("fold", 3, 1), ("quant_k", 4), ("own", 3, 3), ("others", 3, 3)]
-        s_list += [("lay_h", 3, "q", 3), ("exp", 2, 1), ("exp", 2, 2), ("exp", 2, 3)]
-        s_list += [("lay_x", 5, 3), ("lay_h", 4, "k", 0), ("lay_h", 4, "k", 1), ("lay_h", 4, "k", 2)]
-        s_list += [("lay_h", 4, "k", 3), ("lay_h", 4, "q", 0), ("exp", 3, 0), ("lay_h", 4, "q", 1)]
-        s_list += [("lay_h", 4, "q", 2)]
-        t_list += [("flip_x", 6, 0), ("flip_x", 6, 1), ("flip_x", 6, 2), ("flip_x", 6, 3)]
-        t_list += [("project", 5, "k", 0), ("project", 5, "k", 1), ("project", 5, "k", 2), ("scores", 4, 0)]
-        t_list += [("project", 5, "k", 3), ("scores", 4, 1), ("project", 5, "q", 0), ("scores", 4, 2)]
-        t_list += [("project", 5, "q", 1), ("scores", 4, 3), ("project", 5, "q", 2), ("project", 5, "q", 3)]
-        v_list += [("quant_q", 4, 0), ("fold", 3, 2), ("lay_x", 6, 0), ("quant_q", 4, 1)]
-        v_list += [("fold", 3, 3), ("lay_x", 6, 1), ("lay_x", 6, 2), ("quant_q", 4, 2)]
-        v_list += [("quant_q", 4, 3), ("quant_x", 6, 0), ("quant_x", 6, 1), ("quant_x", 6, 2)]
-        v_list += [("quant_x", 6, 3), ("own", 4, 0), ("others", 4, 0), ("own", 4, 1)]
-        v_list += [("others", 4, 1), ("fold", 4, 0), ("own", 4, 2), ("others", 4, 2)]
-        v_list += [("fold", 4, 1), ("quant_k", 5), ("own", 4, 3), ("others", 4, 3)]
-        s_list += [("lay_h", 4, "q", 3), ("exp", 3, 1), ("exp", 3, 2), ("exp", 3, 3)]
-        s_list += [("lay_x", 6, 3), ("lay_h", 5, "k", 0), ("lay_h", 5, "k", 1), ("lay_h", 5, "k", 2)]
-        s_list += [("lay_h", 5, "k", 3), ("lay_h", 5, "q", 0), ("exp", 4, 0), ("lay_h", 5, "q", 1)]
-        s_list += [("lay_h", 5, "q", 2)]
-        t_list += [("flip_x", 7, 0), ("flip_x", 7, 1), ("flip_x", 7, 2), ("flip_x", 7, 3)]
-        t_list += [("project", 6, "k", 0), ("project", 6, "k", 1), ("project", 6, "k", 2), ("scores", 5, 0)]
-        t_list += [("project", 6, "k", 3), ("scores", 5, 1), ("project", 6, "q", 0), ("scores", 5, 2)]
-        t_list += [("project", 6, "q", 1), ("scores", 5, 3), ("project", 6, "q", 2), ("project", 6, "q", 3)]
-        v_list += [("quant_q", 5, 0), ("fold", 4, 2), ("lay_x", 7, 0), ("quant_q", 5, 1)]
-        v_list += [("fold", 4, 3), ("lay_x", 7, 1), ("lay_x", 7, 2), ("quant_q", 5, 2)]
-        v_list += [("quant_q", 5, 3), ("quant_x", 7, 0), ("quant_x", 7, 1), ("quant_x", 7, 2)]
-        v_list += [("quant_x", 7, 3), ("own", 5, 0), ("others", 5, 0), ("own", 5, 1)]
-        v_list += [("others", 5, 1), ("fold", 5, 0), ("own", 5, 2), ("others", 5, 2)]
-        v_list += [("fold", 5, 1), ("quant_k", 6), ("own", 5, 3), ("others", 5, 3)]
-        s_list += [("lay_h", 5, "q", 3), ("exp", 4, 1), ("exp", 4, 2), ("exp", 4, 3)]
-        s_list += [("lay_x", 7, 3), ("lay_h", 6, "k", 0), ("lay_h", 6, "k", 1), ("lay_h", 6, "k", 2)]
-        s_list += [("lay_h", 6, "k", 3), ("lay_h", 6, "q", 0), ("exp", 5, 0), ("lay_h", 6, "q", 1)]
-        s_list += [("lay_h", 6, "q", 2)]
+        for n in range(2, NB):
+            i = n - 1
+            p = n - 2
+            t_list += [("flip_x", n, 0), ("flip_x", n, 1), ("flip_x", n, 2), ("flip_x", n, 3)]
+            t_list += [("project", i, "k", 0), ("project", i, "k", 1), ("project", i, "k", 2), ("scores", p, 0)]
+            t_list += [("project", i, "k", 3), ("scores", p, 1), ("project", i, "q", 0), ("scores", p, 2)]
+            t_list += [("project", i, "q", 1), ("scores", p, 3), ("project", i, "q", 2), ("project", i, "q", 3)]
+            v_list += [("lay_x", n, 0), ("quant_q", p, 2), ("lay_x", n, 1), ("quant_q", p, 3)]
+            v_list += [("lay_x", n, 2), ("quant_x", n, 0), ("own", p, 0), ("quant_x", n, 1)]
+            v_list += [("least", p, 0), ("quant_x", n, 2), ("others", p, 0), ("own", p, 1)]
+            v_list += [("quant_x", n, 3), ("least", p, 1), ("own", p, 2), ("others", p, 1)]
+            v_list += [("quant_k", i), ("least", p, 2), ("own", p, 3), ("others", p, 2)]
+            v_list += [("least", p, 3), ("quant_q", i, 0), ("quant_q", i, 1), ("others", p, 3)]
+            s_list += [("lay_h", p, "q", 3)]
+            if p > 0:
+                s_list += [("exp", p - 1, 1), ("exp", p - 1, 2), ("exp", p - 1, 3)]
+            s_list += [("lay_x", n, 3), ("lay_h", i, "k", 0), ("lay_h", i, "k", 1), ("lay_h", i, "k", 2)]
+            s_list += [("lay_h", i, "k", 3), ("lay_h", i, "q", 0), ("exp", p, 0), ("lay_h", i, "q", 1)]
+            s_list += [("lay_h", i, "q", 2)]
 
-        i = last
-        p = last - 1
-        t_list += [("project", i, "k", 0), ("project", i, "k", 1), ("m_scores", p, 0), ("project", i, "k", 2)]
-        t_list += [("m_scores", p, 1), ("project", i, "k", 3), ("m_scores", p, 2), ("project", i, "q", 0)]
-        t_list += [("m_scores", p, 3), ("project", i, "q", 1), ("project", i, "q", 2), ("project", i, "q", 3)]
-        t_list += [("m_scores", i, 0), ("m_scores", i, 1), ("m_scores", i, 2), ("m_scores", i, 3)]
-        v_list += [("quant_q", p, 0), ("quant_q", p, 1), ("fold", p - 1, 2), ("quant_q", p, 2)]
-        v_list += [("lay_h", i, "k", 0), ("quant_q", p, 3), ("fold", p - 1, 3), ("m_top", p, 0)]
-        v_list += [("lay_h", i, "k", 2), ("m_top", p, 1), ("m_top", p, 2), ("quant_k", i)]
-        v_list += [("lay_h", i, "q", 1), ("quant_q", i, 0), ("m_top", p, 3), ("quant_q", i, 1)]
-        v_list += [("m_top", i, 0), ("quant_q", i, 2), ("m_top", i, 1), ("quant_q", i, 3)]
-        v_list += [("m_top", i, 2), ("m_top", i, 3)]
-        s_list += [("lay_h", p, "q", 3), ("exp", p - 1, 1), ("lay_h", i, "k", 1), ("exp", p - 1, 2)]
-        s_list += [("exp", p - 1, 3), ("lay_h", i, "k", 3), ("m_exp", p, 0), ("lay_h", i, "q", 0)]
-        s_list += [("m_exp", p, 1), ("lay_h", i, "q", 2), ("m_exp", p, 2), ("lay_h", i, "q", 3)]
-        s_list += [("m_exp", p, 3), ("m_exp", i, 0), ("m_exp", i, 1), ("m_exp", i, 2)]
-        s_list += [("m_exp", i, 3)]
+        t_list += [("project", 7, "k", 0), ("project", 7, "k", 1), ("m_scores", 6, 0), ("project", 7, "k", 2)]
+        t_list += [("m_scores", 6, 1), ("project", 7, "k", 3), ("m_scores", 6, 2), ("project", 7, "q", 0)]
+        t_list += [("m_scores", 6, 3), ("project", 7, "q", 1), ("project", 7, "q", 2), ("project", 7, "q", 3)]
+        t_list += [("m_scores", 7, 0), ("m_scores", 7, 1), ("m_scores", 7, 2), ("m_scores", 7, 3)]
+        v_list += [("quant_q", 6, 2), ("lay_h", 7, "k", 0), ("quant_q", 6, 3), ("m_top", 6, 0)]
+        v_list += [("lay_h", 7, "k", 2), ("m_top", 6, 1), ("m_top", 6, 2), ("quant_k", 7)]
+        v_list += [("lay_h", 7, "q", 1), ("quant_q", 7, 0), ("m_top", 6, 3), ("quant_q", 7, 1)]
+        v_list += [("m_top", 7, 0), ("quant_q", 7, 2), ("m_top", 7, 1), ("quant_q", 7, 3)]
+        v_list += [("m_top", 7, 2), ("m_top", 7, 3)]
+        s_list += [("lay_h", 6, "q", 3), ("exp", 5, 1), ("lay_h", 7, "k", 1), ("exp", 5, 2)]
+        s_list += [("exp", 5, 3), ("lay_h", 7, "k", 3), ("m_exp", 6, 0), ("lay_h", 7, "q", 0)]
+        s_list += [("m_exp", 6, 1), ("lay_h", 7, "q", 2), ("m_exp", 6, 2), ("lay_h", 7, "q", 3)]
+        s_list += [("m_exp", 6, 3), ("m_exp", 7, 0), ("m_exp", 7, 1), ("m_exp", 7, 2)]
+        s_list += [("m_exp", 7, 3)]
 
         weave({TENSOR: t_list, VECTOR: v_list, SCALAR: s_list})
         finish()

@@ -30,6 +30,7 @@ MASK_ROOT = 2.0**50
 VECTOR = "vector"
 SCALAR = "scalar"
 WARM_UP = 4
+BRIDGE = 32
 IDLE = 320
 BANKS = 8
 
@@ -189,8 +190,10 @@ def tile_multiheadenergyattention_pa_t_kernel(tc, x, wk, wq, betas, out):
                 out=x_code[b][:, j, :].bitcast(FP8X4), scales=x_scale[b][:, j, :], in_=x_grp[b][:, j, :]
             )
 
-        def project(b, w, j):
+        def project(b, w, j, *idle):
             bank = new_bank(("h", b, w, j))
+            for width in idle:
+                idle_matmul(bank, width)
             for t in range(NT):
                 for g in range(2):
                     cols = slice(g * P, (g + 1) * P)
@@ -434,8 +437,8 @@ def tile_multiheadenergyattention_pa_t_kernel(tc, x, wk, wq, betas, out):
                     if at[engine] == len(queues[engine]):
                         continue
                     step = queues[engine][at[engine]]
-                    name = step[:3] if step[0] in ("flip_w", "flip_x") else step
-                    wanted = needs(step)
+                    name = step[:3] if step[0] in ("flip_w", "flip_x") else step[:4] if step[0] == "project" else step
+                    wanted = needs(name)
                     if engine == TENSOR and len(filled) >= BANKS:
                         wanted = wanted + bank_readers(filled[len(filled) - BANKS])
                     if not all(n in done for n in wanted):
@@ -445,7 +448,7 @@ def tile_multiheadenergyattention_pa_t_kernel(tc, x, wk, wq, betas, out):
                     else:
                         run[step[0]](*step[1:])
                     if engine == TENSOR:
-                        filled.append(step)
+                        filled.append(name)
                     done.add(name)
                     at[engine] += 1
             assert all(at[engine] == len(queues[engine]) for engine in queues)
@@ -455,10 +458,10 @@ def tile_multiheadenergyattention_pa_t_kernel(tc, x, wk, wq, betas, out):
 
         t_list += [("flip_w", "k", 0) + (BANK,) * WARM_UP] + [("flip_w", "k", t, IDLE) for t in (1, 2, 3)]
         t_list += [("flip_x", 0, j, IDLE) for j in range(NT)]
-        t_list += [("project", 0, "k", 0), ("project", 0, "k", 1)]
-        t_list += [("flip_w", "q", 0), ("flip_w", "q", 1), ("flip_w", "q", 2)]
-        t_list += [("project", 0, "k", 2), ("project", 0, "k", 3)]
-        t_list += [("flip_w", "q", 3)]
+        t_list += [("project", 0, "k", 0, BRIDGE), ("project", 0, "k", 1)]
+        t_list += [("flip_w", "q", 0, BRIDGE), ("flip_w", "q", 1), ("flip_w", "q", 2)]
+        t_list += [("project", 0, "k", 2, BRIDGE), ("project", 0, "k", 3)]
+        t_list += [("flip_w", "q", 3, BRIDGE)]
         s_list += [("lay_w", "k", 0), ("lay_w", "k", 2), ("lay_x", 0, 0), ("lay_x", 0, 1), ("lay_x", 0, 2)]
         v_list += [("lay_w", "k", 1), ("quant_w", "k", 0), ("lay_w", "k", 3), ("quant_w", "k", 1)]
         v_list += [("quant_w", "k", 2), ("quant_w", "k", 3), ("quant_x", 0, 0), ("quant_x", 0, 1), ("lay_x", 0, 3)]
@@ -468,15 +471,15 @@ def tile_multiheadenergyattention_pa_t_kernel(tc, x, wk, wq, betas, out):
         s_list += [("lay_h", 0, "k", 2), ("lay_x", 1, 0), ("lay_h", 0, "k", 3)]
         v_list += [("quant_w", "q", 3)]
         t_list += [("flip_x", 1, j) for j in range(NT)]
-        t_list += [("project", 0, "q", j) for j in range(NT)]
+        t_list += [("project", 0, "q", 0, BRIDGE)] + [("project", 0, "q", j) for j in (1, 2, 3)]
         v_list += [("lay_x", 1, j) for j in (1, 2, 3)] + [("quant_x", 1, j) for j in range(NT)] + [("quant_k", 0), ("beta",), ("quant_q", 0, 0), ("quant_q", 0, 1)]
         s_list += [("lay_h", 0, "q", j) for j in (0, 1, 2)]
 
         for n in range(2, NB):
             i = n - 1
             p = n - 2
-            t_list += [("flip_x", n, 0), ("flip_x", n, 1), ("flip_x", n, 2), ("flip_x", n, 3)]
-            t_list += [("project", i, "k", 0), ("project", i, "k", 1), ("project", i, "k", 2), ("scores", p, 0)]
+            t_list += [("flip_x", n, 0, BRIDGE), ("flip_x", n, 1), ("flip_x", n, 2), ("flip_x", n, 3)]
+            t_list += [("project", i, "k", 0, BRIDGE), ("project", i, "k", 1), ("project", i, "k", 2), ("scores", p, 0)]
             t_list += [("project", i, "k", 3), ("scores", p, 1), ("project", i, "q", 0), ("scores", p, 2)]
             t_list += [("project", i, "q", 1), ("scores", p, 3), ("project", i, "q", 2), ("project", i, "q", 3)]
             v_list += [("lay_x", n, 0), ("quant_q", p, 2), ("lay_x", n, 1), ("quant_q", p, 3)]

@@ -458,21 +458,18 @@ def tile_multiheadenergyattention_pa_t_kernel(tc, x, wk, wq, betas, out):
 
         t_list += [("flip_w", "k", 0) + (BANK,) * WARM_UP] + [("flip_w", "k", t, IDLE) for t in (1, 2, 3)]
         t_list += [("flip_x", 0, j, IDLE) for j in range(NT)]
-        t_list += [("project", 0, "k", 0, BRIDGE), ("project", 0, "k", 1)]
-        t_list += [("flip_w", "q", 0, BRIDGE), ("flip_w", "q", 1), ("flip_w", "q", 2)]
-        t_list += [("project", 0, "k", 2, BRIDGE), ("project", 0, "k", 3)]
-        t_list += [("flip_w", "q", 3, BRIDGE)]
-        s_list += [("lay_w", "k", 0), ("lay_w", "k", 2), ("lay_x", 0, 0), ("lay_x", 0, 1), ("lay_x", 0, 2)]
-        v_list += [("lay_w", "k", 1), ("quant_w", "k", 0), ("lay_w", "k", 3), ("quant_w", "k", 1)]
-        v_list += [("quant_w", "k", 2), ("quant_w", "k", 3), ("quant_x", 0, 0), ("quant_x", 0, 1), ("lay_x", 0, 3)]
-        v_list += [("quant_x", 0, 2), ("quant_x", 0, 3)]
-        s_list += [("lay_h", 0, "k", 0), ("lay_w", "q", 0), ("lay_h", 0, "k", 1), ("lay_w", "q", 2)]
-        v_list += [("lay_w", "q", 1), ("quant_w", "q", 0), ("quant_w", "q", 1), ("quant_w", "q", 2), ("lay_w", "q", 3)]
-        s_list += [("lay_h", 0, "k", 2), ("lay_x", 1, 0), ("lay_h", 0, "k", 3)]
-        v_list += [("quant_w", "q", 3)]
+        t_list += [("project", 0, "k", 0, BRIDGE)] + [("project", 0, "k", j) for j in (1, 2, 3)]
+        t_list += [("flip_w", "q", 0, BRIDGE)] + [("flip_w", "q", t) for t in (1, 2, 3)]
         t_list += [("flip_x", 1, j) for j in range(NT)]
         t_list += [("project", 0, "q", 0, BRIDGE)] + [("project", 0, "q", j) for j in (1, 2, 3)]
-        v_list += [("lay_x", 1, j) for j in (1, 2, 3)] + [("quant_x", 1, j) for j in range(NT)] + [("quant_k", 0), ("beta",), ("quant_q", 0, 0), ("quant_q", 0, 1)]
+        s_list += [("lay_w", "k", 0), ("lay_w", "k", 2), ("lay_w", "k", 3), ("lay_x", 0, 0), ("lay_x", 0, 1), ("lay_x", 0, 2)]
+        v_list += [("lay_w", "k", 1), ("quant_w", "k", 0), ("quant_w", "k", 1)]
+        v_list += [("quant_w", "k", 2), ("quant_w", "k", 3), ("quant_x", 0, 0), ("quant_x", 0, 1), ("lay_x", 0, 3)]
+        v_list += [("quant_x", 0, 2), ("quant_x", 0, 3), ("lay_h", 0, "k", 1)]
+        s_list += [("lay_h", 0, "k", 0), ("lay_h", 0, "k", 2), ("lay_h", 0, "k", 3), ("lay_w", "q", 1), ("lay_w", "q", 3)]
+        v_list += [("lay_w", "q", 0), ("lay_w", "q", 2), ("quant_w", "q", 0), ("quant_w", "q", 1), ("quant_w", "q", 2), ("quant_w", "q", 3)]
+        s_list += [("lay_x", 1, 0), ("lay_x", 1, 2)]
+        v_list += [("lay_x", 1, 1), ("lay_x", 1, 3)] + [("quant_x", 1, j) for j in range(NT)] + [("quant_k", 0), ("beta",), ("quant_q", 0, 0), ("quant_q", 0, 1)]
         s_list += [("lay_h", 0, "q", j) for j in (0, 1, 2)]
 
         for n in range(2, NB):
@@ -484,10 +481,10 @@ def tile_multiheadenergyattention_pa_t_kernel(tc, x, wk, wq, betas, out):
             t_list += [("project", i, "q", 1), ("scores", p, 3), ("project", i, "q", 2), ("project", i, "q", 3)]
             v_list += [("lay_x", n, 0), ("quant_q", p, 2), ("lay_x", n, 1), ("quant_q", p, 3)]
             v_list += [("lay_x", n, 2), ("quant_x", n, 0), ("own", p, 0), ("quant_x", n, 1)]
-            v_list += [("least", p, 0), ("quant_x", n, 2), ("others", p, 0), ("own", p, 1)]
-            v_list += [("quant_x", n, 3), ("least", p, 1), ("own", p, 2), ("others", p, 1)]
-            v_list += [("quant_k", i), ("least", p, 2), ("own", p, 3), ("others", p, 2)]
-            v_list += [("least", p, 3), ("quant_q", i, 0), ("quant_q", i, 1), ("others", p, 3)]
+            v_list += [("least", p, 0), ("quant_x", n, 2), ("own", p, 1), ("others", p, 0)]
+            v_list += [("least", p, 1), ("quant_x", n, 3), ("own", p, 2), ("others", p, 1)]
+            v_list += [("least", p, 2), ("quant_k", i), ("own", p, 3), ("others", p, 2)]
+            v_list += [("quant_q", i, 0), ("least", p, 3), ("quant_q", i, 1), ("others", p, 3)]
             s_list += [("lay_h", p, "q", 3)]
             if p > 0:
                 s_list += [("exp", p - 1, 1), ("exp", p - 1, 2), ("exp", p - 1, 3)]
@@ -502,11 +499,11 @@ def tile_multiheadenergyattention_pa_t_kernel(tc, x, wk, wq, betas, out):
         v_list += [("quant_q", 6, 2), ("lay_h", 7, "k", 0), ("quant_q", 6, 3), ("m_top", 6, 0)]
         v_list += [("lay_h", 7, "k", 2), ("m_top", 6, 1), ("m_top", 6, 2), ("quant_k", 7)]
         v_list += [("lay_h", 7, "q", 1), ("quant_q", 7, 0), ("m_top", 6, 3), ("quant_q", 7, 1)]
-        v_list += [("m_top", 7, 0), ("quant_q", 7, 2), ("m_top", 7, 1), ("quant_q", 7, 3)]
+        v_list += [("quant_q", 7, 2), ("m_top", 7, 0), ("quant_q", 7, 3), ("m_top", 7, 1)]
         v_list += [("m_top", 7, 2), ("m_top", 7, 3)]
-        s_list += [("lay_h", 6, "q", 3), ("exp", 5, 1), ("lay_h", 7, "k", 1), ("exp", 5, 2)]
-        s_list += [("exp", 5, 3), ("lay_h", 7, "k", 3), ("m_exp", 6, 0), ("lay_h", 7, "q", 0)]
-        s_list += [("m_exp", 6, 1), ("lay_h", 7, "q", 2), ("m_exp", 6, 2), ("lay_h", 7, "q", 3)]
+        s_list += [("lay_h", 6, "q", 3), ("exp", 5, 1), ("exp", 5, 2), ("lay_h", 7, "k", 1)]
+        s_list += [("exp", 5, 3), ("m_exp", 6, 0), ("lay_h", 7, "k", 3), ("m_exp", 6, 1)]
+        s_list += [("lay_h", 7, "q", 0), ("m_exp", 6, 2), ("lay_h", 7, "q", 2), ("lay_h", 7, "q", 3)]
         s_list += [("m_exp", 6, 3), ("m_exp", 7, 0), ("m_exp", 7, 1), ("m_exp", 7, 2)]
         s_list += [("m_exp", 7, 3)]
 

@@ -87,8 +87,8 @@ def tile_multiheadenergyattention_pa_t_kernel(tc, x, wk, wq, betas, out):
         m_scale = {}
         for side, root in (("q", MASK_ROOT), ("k", -MASK_ROOT)):
             m_grp[side] = keep.tile([P, P, 4], BF16, name="m_grp_" + side, align_bytes=64)
-            m_code[side] = keep.tile([P, P], U32, name="m_code_" + side, align_bytes=64)
-            m_scale[side] = keep.tile([P, P], U8, name="m_scale_" + side, align_bytes=64)
+            m_code[side] = keep.tile([P, P], U32, name="m_code_" + side, align_bytes=256)
+            m_scale[side] = keep.tile([P, P], U8, name="m_scale_" + side, align_bytes=256)
             nc.gpsimd.memset(m_grp[side][:], 0.0)
             nc.vector.tensor_scalar(
                 out=m_grp[side][:, :, 0], in0=ident[:], scalar1=root, scalar2=None, op0=ALU.mult
@@ -125,8 +125,8 @@ def tile_multiheadenergyattention_pa_t_kernel(tc, x, wk, wq, betas, out):
         w_scale = {}
         for w in ("k", "q"):
             w_grp[w] = keep.tile([P, NT, D], BF16, name="w_grp_" + w, align_bytes=64)
-            w_code[w] = keep.tile([P, NT, D // 4], U32, name="w_code_" + w, align_bytes=64)
-            w_scale[w] = keep.tile([P, NT, D // 4], U8, name="w_scale_" + w, align_bytes=64)
+            w_code[w] = keep.tile([P, NT, D // 4], U32, name="w_code_" + w, align_bytes=256)
+            w_scale[w] = keep.tile([P, NT, D // 4], U8, name="w_scale_" + w, align_bytes=256)
         x_grp = {}
         x_code = {}
         x_scale = {}
@@ -181,8 +181,8 @@ def tile_multiheadenergyattention_pa_t_kernel(tc, x, wk, wq, betas, out):
         def regroup_tokens(b, j, engine):
             if b not in x_grp:
                 x_grp[b] = pairs.tile([P, NT, D], BF16, name="x_grp", tag="x_grp", align_bytes=64)
-                x_code[b] = triples.tile([P, NT, D // 4], U32, name="x_code", tag="x_code", align_bytes=64)
-                x_scale[b] = triples.tile([P, NT, D // 4], U8, name="x_scale", tag="x_scale", align_bytes=64)
+                x_code[b] = triples.tile([P, NT, D // 4], U32, name="x_code", tag="x_code", align_bytes=256)
+                x_scale[b] = triples.tile([P, NT, D // 4], U8, name="x_scale", tag="x_scale", align_bytes=256)
             regroup(engine, ("x", b, j), x_grp[b][:, j, :])
 
         def quantise_tokens(b, j):
@@ -210,8 +210,8 @@ def tile_multiheadenergyattention_pa_t_kernel(tc, x, wk, wq, betas, out):
         def regroup_heads(b, w, j, engine):
             if (b, w) not in h_grp:
                 h_grp[(b, w)] = pairs.tile([P, N, 4], BF16, name="h_grp_" + w, tag="h_grp_" + w, align_bytes=64)
-                h_code[(b, w)] = triples.tile([P, N], U32, name="h_code_" + w, tag="h_code_" + w, align_bytes=64)
-                h_scale[(b, w)] = triples.tile([P, N], U8, name="h_scale_" + w, tag="h_scale_" + w, align_bytes=64)
+                h_code[(b, w)] = triples.tile([P, N], U32, name="h_code_" + w, tag="h_code_" + w, align_bytes=256)
+                h_scale[(b, w)] = triples.tile([P, N], U8, name="h_scale_" + w, tag="h_scale_" + w, align_bytes=256)
             copy_out(
                 engine,
                 h_grp[(b, w)][:, j * P : (j + 1) * P, :],

@@ -26,6 +26,9 @@ LOWEST = 3.0e38
 ROW_SLOTS = 6
 TURNS = 4
 TENSOR = "tensor"
+TURNED = 2
+BLOCK = 32
+BLOCKS = 2 * N // BLOCK
 MASK_ROOT = 2.0**50
 VECTOR = "vector"
 SCALAR = "scalar"
@@ -49,9 +52,14 @@ def tile_multiheadenergyattention_pa_t_kernel(tc, x, wk, wq, betas, out):
         w_raw = {}
         for w in ("k", "q"):
             w_raw[w] = keep.tile([P, NT, D], BF16, name="w_raw_" + w)
-        x_raw = []
+        x_raw = {}
+        x_blocks = {}
         for b in range(NB):
-            x_raw.append(keep.tile([P, NT, D], BF16, name="x_raw_%d" % b))
+            if b < TURNED:
+                x_raw[b] = keep.tile([P, NT, D], BF16, name="x_raw_%d" % b)
+            else:
+                x_raw[b] = keep.tile([P, NT, D // 2], BF16, name="x_raw_%d" % b)
+                x_blocks[b] = keep.tile([P, BLOCKS, 2 * BLOCK], BF16, name="x_blocks_%d" % b, align_bytes=64)
 
         def load_weights(w):
             tiles = w_dram[w][0, :, :].rearrange("(p t) d -> p t d", t=NT)
@@ -65,10 +73,17 @@ def tile_multiheadenergyattention_pa_t_kernel(tc, x, wk, wq, betas, out):
         for j in range(NT):
             nc.sync.dma_start(out=x_raw[1][:, j, :], in_=x[1, j * P : (j + 1) * P, :])
         beta_bf = keep.tile([P, 1], BF16, name="beta_bf")
-        for b in range(2, NB):
-            nc.sync.dma_start(out=x_raw[b][:], in_=x[b, :, :].rearrange("(j p) d -> p j d", p=P))
-            if b == 2:
+        for b in range(TURNED, NB):
+            nc.sync.dma_start(out=x_raw[b][:], in_=x[b, :, 0 : D // 2].rearrange("(j p) d -> p j d", p=P))
+            if b == TURNED:
                 nc.sync.dma_start(out=beta_bf[:], in_=betas.partition_broadcast(P))
+            for u in range(2):
+                for q in (0, 2, 1, 3):
+                    first = 512 + 256 * u + 2 * BLOCK * q
+                    nc.sync.dma_start(
+                        out=x_blocks[b][BLOCK * q + u : BLOCK * (q + 1) : 2, :, :],
+                        in_=x[b, :, first : first + 2 * BLOCK].rearrange("(c n) f -> n c f", c=BLOCKS),
+                    )
 
         zeros = keep.tile([P, BANK], BF16, name="zeros")
         nc.vector.memset(zeros[:], 0.0)
@@ -87,8 +102,8 @@ def tile_multiheadenergyattention_pa_t_kernel(tc, x, wk, wq, betas, out):
         m_scale = {}
         for side, root in (("q", MASK_ROOT), ("k", -MASK_ROOT)):
             m_grp[side] = keep.tile([P, P, 4], BF16, name="m_grp_" + side, align_bytes=64)
-            m_code[side] = keep.tile([P, P], U32, name="m_code_" + side, align_bytes=256)
-            m_scale[side] = keep.tile([P, P], U8, name="m_scale_" + side, align_bytes=256)
+            m_code[side] = keep.tile([P, P], U32, name="m_code_" + side, align_bytes=64)
+            m_scale[side] = keep.tile([P, P], U8, name="m_scale_" + side, align_bytes=64)
             nc.gpsimd.memset(m_grp[side][:], 0.0)
             nc.vector.tensor_scalar(
                 out=m_grp[side][:, :, 0], in0=ident[:], scalar1=root, scalar2=None, op0=ALU.mult
@@ -125,8 +140,8 @@ def tile_multiheadenergyattention_pa_t_kernel(tc, x, wk, wq, betas, out):
         w_scale = {}
         for w in ("k", "q"):
             w_grp[w] = keep.tile([P, NT, D], BF16, name="w_grp_" + w, align_bytes=64)
-            w_code[w] = keep.tile([P, NT, D // 4], U32, name="w_code_" + w, align_bytes=256)
-            w_scale[w] = keep.tile([P, NT, D // 4], U8, name="w_scale_" + w, align_bytes=256)
+            w_code[w] = keep.tile([P, NT, D // 4], U32, name="w_code_" + w, align_bytes=64)
+            w_scale[w] = keep.tile([P, NT, D // 4], U8, name="w_scale_" + w, align_bytes=64)
         x_grp = {}
         x_code = {}
         x_scale = {}
@@ -181,14 +196,54 @@ def tile_multiheadenergyattention_pa_t_kernel(tc, x, wk, wq, betas, out):
         def regroup_tokens(b, j, engine):
             if b not in x_grp:
                 x_grp[b] = pairs.tile([P, NT, D], BF16, name="x_grp", tag="x_grp", align_bytes=64)
-                x_code[b] = triples.tile([P, NT, D // 4], U32, name="x_code", tag="x_code", align_bytes=256)
-                x_scale[b] = triples.tile([P, NT, D // 4], U8, name="x_scale", tag="x_scale", align_bytes=256)
+                x_code[b] = triples.tile([P, NT, D // 4], U32, name="x_code", tag="x_code", align_bytes=64)
+                x_scale[b] = triples.tile([P, NT, D // 4], U8, name="x_scale", tag="x_scale", align_bytes=64)
             regroup(engine, ("x", b, j), x_grp[b][:, j, :])
+
+        def flip_pair(b, h, *idle):
+            bank = new_bank(("p", b, h))
+            for width in idle:
+                idle_matmul(bank, width)
+            for r in range(2):
+                words = x_raw[b][:, 2 * h + r, :].bitcast(F32)
+                for u in range(2):
+                    at = (2 * r + u) * P
+                    nc.tensor.transpose(bank[:, at : at + P], words[:, u * P : (u + 1) * P], ident[:])
+
+        def new_halves(b):
+            if b not in x_grp:
+                x_grp[b] = pairs.tile([P, 2, 4 * N], BF16, name="x_grp", tag="x_grp", align_bytes=64)
+                x_code[b] = triples.tile([P, 2, N], U32, name="x_code", tag="x_code", align_bytes=64)
+                x_scale[b] = triples.tile([P, 2, N], U8, name="x_scale", tag="x_scale", align_bytes=64)
+
+        def regroup_pair(b, h, engine):
+            new_halves(b)
+            copy_out(
+                engine,
+                x_grp[b][:, 0, h * 2 * N : (h + 1) * 2 * N].bitcast(F32).rearrange("p (j r u) -> p j r u", j=2, u=2),
+                banks[("p", b, h)][:].rearrange("p (j u r) -> p j r u", j=2, u=2),
+            )
+
+        def turn_blocks(b):
+            new_halves(b)
+            nc.vector.transpose(
+                out=x_grp[b][:, 1, :].bitcast(F32), in_=x_blocks[b][:].rearrange("p c f -> p (c f)").bitcast(F32)
+            )
+
+        def quantise_half(b, g):
+            nc.vector.quantize_mx(
+                out=x_code[b][:, g, :].bitcast(FP8X4), scales=x_scale[b][:, g, :], in_=x_grp[b][:, g, :]
+            )
 
         def quantise_tokens(b, j):
             nc.vector.quantize_mx(
                 out=x_code[b][:, j, :].bitcast(FP8X4), scales=x_scale[b][:, j, :], in_=x_grp[b][:, j, :]
             )
+
+        def moving(tiles, b, j, g):
+            if b < TURNED:
+                return tiles[b][:, j, g * P : (g + 1) * P]
+            return tiles[b][:, g, j * P : (j + 1) * P]
 
         def project(b, w, j, *idle):
             bank = new_bank(("h", b, w, j))
@@ -201,8 +256,8 @@ def tile_multiheadenergyattention_pa_t_kernel(tc, x, wk, wq, betas, out):
                         out=bank[:, t * P : (t + 1) * P],
                         lhsT=w_code[w][:, t, cols].bitcast(FP8X4),
                         lhsT_scale=w_scale[w][:, t, cols],
-                        rhs=x_code[b][:, j, cols].bitcast(FP8X4),
-                        rhs_scale=x_scale[b][:, j, cols],
+                        rhs=moving(x_code, b, j, g).bitcast(FP8X4),
+                        rhs_scale=moving(x_scale, b, j, g),
                         start=(g == 0),
                         stop=(g == 1),
                     )
@@ -210,8 +265,8 @@ def tile_multiheadenergyattention_pa_t_kernel(tc, x, wk, wq, betas, out):
         def regroup_heads(b, w, j, engine):
             if (b, w) not in h_grp:
                 h_grp[(b, w)] = pairs.tile([P, N, 4], BF16, name="h_grp_" + w, tag="h_grp_" + w, align_bytes=64)
-                h_code[(b, w)] = triples.tile([P, N], U32, name="h_code_" + w, tag="h_code_" + w, align_bytes=256)
-                h_scale[(b, w)] = triples.tile([P, N], U8, name="h_scale_" + w, tag="h_scale_" + w, align_bytes=256)
+                h_code[(b, w)] = triples.tile([P, N], U32, name="h_code_" + w, tag="h_code_" + w, align_bytes=64)
+                h_scale[(b, w)] = triples.tile([P, N], U8, name="h_scale_" + w, tag="h_scale_" + w, align_bytes=64)
             copy_out(
                 engine,
                 h_grp[(b, w)][:, j * P : (j + 1) * P, :],
@@ -371,6 +426,10 @@ def tile_multiheadenergyattention_pa_t_kernel(tc, x, wk, wq, betas, out):
             "lay_h": regroup_heads,
             "quant_w": quantise_weights,
             "quant_x": quantise_tokens,
+            "flip_p": flip_pair,
+            "lay_p": regroup_pair,
+            "turn": turn_blocks,
+            "quant_h": quantise_half,
             "quant_k": quantise_keys,
             "quant_q": quantise_queries,
             "own": shift_own,
@@ -385,7 +444,7 @@ def tile_multiheadenergyattention_pa_t_kernel(tc, x, wk, wq, betas, out):
 
         def bank_readers(step):
             kind = step[0]
-            if kind in ("flip_w", "flip_x"):
+            if kind in ("flip_w", "flip_x", "flip_p"):
                 return [("lay" + kind[4:],) + step[1:3]]
             if kind == "project":
                 return [("lay_h",) + step[1:]]
@@ -395,15 +454,19 @@ def tile_multiheadenergyattention_pa_t_kernel(tc, x, wk, wq, betas, out):
 
         def needs(step):
             kind = step[0]
-            if kind in ("lay_w", "lay_x"):
+            if kind in ("lay_w", "lay_x", "lay_p"):
                 return [("flip" + kind[3:],) + step[1:3]]
             if kind in ("quant_w", "quant_x"):
                 return [("lay" + kind[5:],) + step[1:3]]
             if kind == "project":
                 b, w, j = step[1:]
-                return [("quant_w", w, t) for t in range(NT)] + [("quant_x", b, j)]
+                return [("quant_w", w, t) for t in range(NT)] + (
+                    [("quant_x", b, j)] if b < TURNED else [("quant_h", b, 0), ("quant_h", b, 1)]
+                )
             if kind == "lay_h":
                 return [("project",) + step[1:]]
+            if kind == "quant_h":
+                return [("turn", step[1])] if step[2] else [("lay_p", step[1], 0), ("lay_p", step[1], 1)]
             if kind == "quant_k":
                 return [("lay_h", step[1], "k", j) for j in range(NT)]
             if kind == "quant_q":
@@ -437,13 +500,13 @@ def tile_multiheadenergyattention_pa_t_kernel(tc, x, wk, wq, betas, out):
                     if at[engine] == len(queues[engine]):
                         continue
                     step = queues[engine][at[engine]]
-                    name = step[:3] if step[0] in ("flip_w", "flip_x") else step[:4] if step[0] == "project" else step
+                    name = step[:3] if step[0] in ("flip_w", "flip_x", "flip_p") else step[:4] if step[0] == "project" else step
                     wanted = needs(name)
                     if engine == TENSOR and len(filled) >= BANKS:
                         wanted = wanted + bank_readers(filled[len(filled) - BANKS])
                     if not all(n in done for n in wanted):
                         continue
-                    if step[0] in ("lay_w", "lay_x", "lay_h"):
+                    if step[0] in ("lay_w", "lay_x", "lay_h", "lay_p"):
                         run[step[0]](*step[1:], engine)
                     else:
                         run[step[0]](*step[1:])
@@ -469,40 +532,79 @@ def tile_multiheadenergyattention_pa_t_kernel(tc, x, wk, wq, betas, out):
         s_list += [("lay_h", 0, "k", 0), ("lay_h", 0, "k", 2), ("lay_h", 0, "k", 3), ("lay_w", "q", 1), ("lay_w", "q", 3)]
         v_list += [("lay_w", "q", 0), ("lay_w", "q", 2), ("quant_w", "q", 0), ("quant_w", "q", 1), ("quant_w", "q", 2), ("quant_w", "q", 3)]
         s_list += [("lay_x", 1, 0), ("lay_x", 1, 2)]
-        v_list += [("lay_x", 1, 1), ("lay_x", 1, 3)] + [("quant_x", 1, j) for j in range(NT)] + [("quant_k", 0), ("beta",), ("quant_q", 0, 0), ("quant_q", 0, 1)]
-        s_list += [("lay_h", 0, "q", j) for j in (0, 1, 2)]
-
-        for n in range(2, NB):
-            i = n - 1
-            p = n - 2
-            t_list += [("flip_x", n, 0, BRIDGE), ("flip_x", n, 1), ("flip_x", n, 2), ("flip_x", n, 3)]
-            t_list += [("project", i, "k", 0, BRIDGE), ("project", i, "k", 1), ("project", i, "k", 2), ("scores", p, 0)]
-            t_list += [("project", i, "k", 3), ("scores", p, 1), ("project", i, "q", 0), ("scores", p, 2)]
-            t_list += [("project", i, "q", 1), ("scores", p, 3), ("project", i, "q", 2), ("project", i, "q", 3)]
-            v_list += [("lay_x", n, 0), ("quant_q", p, 2), ("lay_x", n, 1), ("quant_q", p, 3)]
-            v_list += [("lay_x", n, 2), ("quant_x", n, 0), ("own", p, 0), ("quant_x", n, 1)]
-            v_list += [("least", p, 0), ("quant_x", n, 2), ("own", p, 1), ("others", p, 0)]
-            v_list += [("least", p, 1), ("quant_x", n, 3), ("own", p, 2), ("others", p, 1)]
-            v_list += [("least", p, 2), ("quant_k", i), ("own", p, 3), ("others", p, 2)]
-            v_list += [("quant_q", i, 0), ("least", p, 3), ("quant_q", i, 1), ("others", p, 3)]
-            s_list += [("lay_h", p, "q", 3)]
-            if p > 0:
-                s_list += [("exp", p - 1, 1), ("exp", p - 1, 2), ("exp", p - 1, 3)]
-            s_list += [("lay_x", n, 3), ("lay_h", i, "k", 0), ("lay_h", i, "k", 1), ("lay_h", i, "k", 2)]
-            s_list += [("lay_h", i, "k", 3), ("lay_h", i, "q", 0), ("exp", p, 0), ("lay_h", i, "q", 1)]
-            s_list += [("lay_h", i, "q", 2)]
-
+        v_list += [("lay_x", 1, 1), ("lay_x", 1, 3)] + [("quant_x", 1, j) for j in range(NT)] + [("beta",)]
+        s_list += [("lay_h", 0, "q", j) for j in range(NT)]
+        t_list += [("flip_p", 2, 0, BRIDGE), ("flip_p", 2, 1), ("project", 1, "k", 0, BRIDGE), ("project", 1, "k", 1)]
+        t_list += [("project", 1, "k", 2), ("m_scores", 0, 0), ("project", 1, "k", 3), ("m_scores", 0, 1)]
+        t_list += [("project", 1, "q", 0), ("m_scores", 0, 2), ("project", 1, "q", 1), ("m_scores", 0, 3)]
+        t_list += [("project", 1, "q", 2), ("project", 1, "q", 3), ("flip_p", 3, 0, BRIDGE), ("flip_p", 3, 1)]
+        t_list += [("project", 2, "k", 0, BRIDGE), ("project", 2, "k", 1), ("project", 2, "k", 2), ("m_scores", 1, 0)]
+        t_list += [("project", 2, "k", 3), ("m_scores", 1, 1), ("project", 2, "q", 0), ("m_scores", 1, 2)]
+        t_list += [("project", 2, "q", 1), ("m_scores", 1, 3), ("project", 2, "q", 2), ("project", 2, "q", 3)]
+        t_list += [("flip_p", 4, 0, BRIDGE), ("flip_p", 4, 1), ("project", 3, "k", 0, BRIDGE), ("project", 3, "k", 1)]
+        t_list += [("project", 3, "k", 2), ("m_scores", 2, 0), ("project", 3, "k", 3), ("m_scores", 2, 1)]
+        t_list += [("project", 3, "q", 0), ("m_scores", 2, 2), ("project", 3, "q", 1), ("m_scores", 2, 3)]
+        t_list += [("project", 3, "q", 2), ("project", 3, "q", 3), ("flip_p", 5, 0, BRIDGE), ("flip_p", 5, 1)]
+        t_list += [("project", 4, "k", 0, BRIDGE), ("project", 4, "k", 1), ("project", 4, "k", 2), ("m_scores", 3, 0)]
+        t_list += [("project", 4, "k", 3), ("m_scores", 3, 1), ("project", 4, "q", 0), ("m_scores", 3, 2)]
+        t_list += [("project", 4, "q", 1), ("m_scores", 3, 3), ("project", 4, "q", 2), ("project", 4, "q", 3)]
+        t_list += [("flip_p", 6, 0, BRIDGE), ("flip_p", 6, 1), ("project", 5, "k", 0, BRIDGE), ("project", 5, "k", 1)]
+        t_list += [("project", 5, "k", 2), ("m_scores", 4, 0), ("project", 5, "k", 3), ("m_scores", 4, 1)]
+        t_list += [("project", 5, "q", 0), ("m_scores", 4, 2), ("project", 5, "q", 1), ("m_scores", 4, 3)]
+        t_list += [("project", 5, "q", 2), ("project", 5, "q", 3), ("flip_p", 7, 0, BRIDGE), ("flip_p", 7, 1)]
+        t_list += [("project", 6, "k", 0, BRIDGE), ("project", 6, "k", 1), ("project", 6, "k", 2), ("m_scores", 5, 0)]
+        t_list += [("project", 6, "k", 3), ("m_scores", 5, 1), ("project", 6, "q", 0), ("m_scores", 5, 2)]
+        t_list += [("project", 6, "q", 1), ("m_scores", 5, 3), ("project", 6, "q", 2), ("project", 6, "q", 3)]
         t_list += [("project", 7, "k", 0), ("project", 7, "k", 1), ("m_scores", 6, 0), ("project", 7, "k", 2)]
         t_list += [("m_scores", 6, 1), ("project", 7, "k", 3), ("m_scores", 6, 2), ("project", 7, "q", 0)]
         t_list += [("m_scores", 6, 3), ("project", 7, "q", 1), ("project", 7, "q", 2), ("project", 7, "q", 3)]
         t_list += [("m_scores", 7, 0), ("m_scores", 7, 1), ("m_scores", 7, 2), ("m_scores", 7, 3)]
-        v_list += [("quant_q", 6, 2), ("lay_h", 7, "k", 0), ("quant_q", 6, 3), ("m_top", 6, 0)]
-        v_list += [("lay_h", 7, "k", 2), ("m_top", 6, 1), ("m_top", 6, 2), ("quant_k", 7)]
-        v_list += [("lay_h", 7, "q", 1), ("quant_q", 7, 0), ("m_top", 6, 3), ("quant_q", 7, 1)]
-        v_list += [("quant_q", 7, 2), ("m_top", 7, 0), ("quant_q", 7, 3), ("m_top", 7, 1)]
-        v_list += [("m_top", 7, 2), ("m_top", 7, 3)]
-        s_list += [("lay_h", 6, "q", 3), ("exp", 5, 1), ("exp", 5, 2), ("lay_h", 7, "k", 1)]
-        s_list += [("exp", 5, 3), ("m_exp", 6, 0), ("lay_h", 7, "k", 3), ("m_exp", 6, 1)]
+        v_list += [("quant_k", 0), ("quant_q", 0, 0), ("quant_q", 0, 1), ("turn", 2)]
+        v_list += [("lay_p", 2, 0), ("lay_p", 2, 1), ("quant_q", 0, 2), ("quant_q", 0, 3)]
+        v_list += [("m_top", 0, 0), ("quant_h", 2, 0), ("m_top", 0, 1), ("m_top", 0, 2)]
+        v_list += [("quant_h", 2, 1), ("m_top", 0, 3), ("quant_k", 1), ("quant_q", 1, 0)]
+        v_list += [("quant_q", 1, 1), ("turn", 3), ("lay_p", 3, 0), ("lay_p", 3, 1)]
+        v_list += [("quant_q", 1, 2), ("quant_q", 1, 3), ("m_top", 1, 0), ("quant_h", 3, 0)]
+        v_list += [("m_top", 1, 1), ("m_top", 1, 2), ("quant_h", 3, 1), ("m_top", 1, 3)]
+        v_list += [("quant_k", 2), ("quant_q", 2, 0), ("quant_q", 2, 1), ("turn", 4)]
+        v_list += [("lay_p", 4, 0), ("lay_p", 4, 1), ("quant_q", 2, 2), ("quant_q", 2, 3)]
+        v_list += [("m_top", 2, 0), ("quant_h", 4, 0), ("m_top", 2, 1), ("m_top", 2, 2)]
+        v_list += [("quant_h", 4, 1), ("m_top", 2, 3), ("quant_k", 3), ("quant_q", 3, 0)]
+        v_list += [("quant_q", 3, 1), ("turn", 5), ("lay_p", 5, 0), ("lay_p", 5, 1)]
+        v_list += [("quant_q", 3, 2), ("quant_q", 3, 3), ("m_top", 3, 0), ("quant_h", 5, 0)]
+        v_list += [("m_top", 3, 1), ("m_top", 3, 2), ("quant_h", 5, 1), ("m_top", 3, 3)]
+        v_list += [("quant_k", 4), ("quant_q", 4, 0), ("quant_q", 4, 1), ("turn", 6)]
+        v_list += [("lay_p", 6, 0), ("lay_p", 6, 1), ("quant_q", 4, 2), ("quant_q", 4, 3)]
+        v_list += [("m_top", 4, 0), ("quant_h", 6, 0), ("m_top", 4, 1), ("m_top", 4, 2)]
+        v_list += [("quant_h", 6, 1), ("m_top", 4, 3), ("quant_k", 5), ("quant_q", 5, 0)]
+        v_list += [("quant_q", 5, 1), ("turn", 7), ("lay_p", 7, 0), ("lay_p", 7, 1)]
+        v_list += [("quant_q", 5, 2), ("quant_q", 5, 3), ("m_top", 5, 0), ("quant_h", 7, 0)]
+        v_list += [("m_top", 5, 1), ("m_top", 5, 2), ("quant_h", 7, 1), ("m_top", 5, 3)]
+        v_list += [("quant_k", 6), ("quant_q", 6, 0), ("lay_h", 6, "q", 1), ("quant_q", 6, 1)]
+        v_list += [("quant_q", 6, 2), ("quant_q", 6, 3), ("m_top", 6, 0), ("m_top", 6, 1)]
+        v_list += [("lay_h", 7, "k", 3), ("m_top", 6, 2), ("quant_k", 7), ("lay_h", 7, "q", 1)]
+        v_list += [("quant_q", 7, 0), ("m_top", 6, 3), ("quant_q", 7, 1), ("quant_q", 7, 2)]
+        v_list += [("m_top", 7, 0), ("quant_q", 7, 3), ("m_top", 7, 1), ("m_top", 7, 2)]
+        v_list += [("m_top", 7, 3)]
+        s_list += [("lay_h", 1, "k", 0), ("lay_h", 1, "k", 1), ("lay_h", 1, "k", 2), ("lay_h", 1, "k", 3)]
+        s_list += [("m_exp", 0, 0), ("lay_h", 1, "q", 0), ("m_exp", 0, 1), ("lay_h", 1, "q", 1)]
+        s_list += [("m_exp", 0, 2), ("lay_h", 1, "q", 2), ("m_exp", 0, 3), ("lay_h", 1, "q", 3)]
+        s_list += [("lay_h", 2, "k", 0), ("lay_h", 2, "k", 1), ("lay_h", 2, "k", 2), ("lay_h", 2, "k", 3)]
+        s_list += [("m_exp", 1, 0), ("lay_h", 2, "q", 0), ("m_exp", 1, 1), ("lay_h", 2, "q", 1)]
+        s_list += [("m_exp", 1, 2), ("lay_h", 2, "q", 2), ("m_exp", 1, 3), ("lay_h", 2, "q", 3)]
+        s_list += [("lay_h", 3, "k", 0), ("lay_h", 3, "k", 1), ("lay_h", 3, "k", 2), ("lay_h", 3, "k", 3)]
+        s_list += [("m_exp", 2, 0), ("lay_h", 3, "q", 0), ("m_exp", 2, 1), ("lay_h", 3, "q", 1)]
+        s_list += [("m_exp", 2, 2), ("lay_h", 3, "q", 2), ("m_exp", 2, 3), ("lay_h", 3, "q", 3)]
+        s_list += [("lay_h", 4, "k", 0), ("lay_h", 4, "k", 1), ("lay_h", 4, "k", 2), ("lay_h", 4, "k", 3)]
+        s_list += [("m_exp", 3, 0), ("lay_h", 4, "q", 0), ("m_exp", 3, 1), ("lay_h", 4, "q", 1)]
+        s_list += [("m_exp", 3, 2), ("lay_h", 4, "q", 2), ("m_exp", 3, 3), ("lay_h", 4, "q", 3)]
+        s_list += [("lay_h", 5, "k", 0), ("lay_h", 5, "k", 1), ("lay_h", 5, "k", 2), ("lay_h", 5, "k", 3)]
+        s_list += [("m_exp", 4, 0), ("lay_h", 5, "q", 0), ("m_exp", 4, 1), ("lay_h", 5, "q", 1)]
+        s_list += [("m_exp", 4, 2), ("lay_h", 5, "q", 2), ("m_exp", 4, 3), ("lay_h", 5, "q", 3)]
+        s_list += [("lay_h", 6, "k", 0), ("lay_h", 6, "k", 1), ("lay_h", 6, "k", 2), ("lay_h", 6, "k", 3)]
+        s_list += [("m_exp", 5, 0), ("lay_h", 6, "q", 0), ("m_exp", 5, 1), ("lay_h", 6, "q", 2)]
+        s_list += [("m_exp", 5, 2), ("lay_h", 6, "q", 3), ("m_exp", 5, 3), ("lay_h", 7, "k", 0)]
+        s_list += [("lay_h", 7, "k", 1), ("lay_h", 7, "k", 2), ("m_exp", 6, 0), ("m_exp", 6, 1)]
         s_list += [("lay_h", 7, "q", 0), ("m_exp", 6, 2), ("lay_h", 7, "q", 2), ("lay_h", 7, "q", 3)]
         s_list += [("m_exp", 6, 3), ("m_exp", 7, 0), ("m_exp", 7, 1), ("m_exp", 7, 2)]
         s_list += [("m_exp", 7, 3)]

@@ -17,25 +17,24 @@ D = 1024
 Z = 512
 P = 128
 NT = N // P
+PASSES = 2
+D_PASS = D // PASSES
 BANK = 512
+BANKS = 8
+BLOCK = 32
+GROUPS = 2 * N // BLOCK
 ROW_TILES = NB * NT
 FLOPS = 2 * NB * N * D * 2 * Z + 2 * NB * N * N * Z
 
-MASKED = 1.0e9
-LOWEST = 3.0e38
-ROW_SLOTS = 6
-TURNS = 4
-TENSOR = "tensor"
 TURNED = 2
-BLOCK = 32
-BLOCKS = 2 * N // BLOCK
 MASK_ROOT = 2.0**50
+TENSOR = "tensor"
 VECTOR = "vector"
 SCALAR = "scalar"
+TURNS = 4
 WARM_UP = 4
-BRIDGE = 32
 IDLE = 320
-BANKS = 8
+BRIDGE = 32
 
 
 def tile_multiheadenergyattention_pa_t_kernel(tc, x, wk, wq, betas, out):
@@ -44,86 +43,75 @@ def tile_multiheadenergyattention_pa_t_kernel(tc, x, wk, wq, betas, out):
         keep = ctx.enter_context(tc.tile_pool(name="keep", bufs=1))
         pairs = ctx.enter_context(tc.tile_pool(name="pairs", bufs=2))
         triples = ctx.enter_context(tc.tile_pool(name="triples", bufs=3))
-        rows = ctx.enter_context(tc.tile_pool(name="rows", bufs=ROW_SLOTS))
-        psum = ctx.enter_context(tc.psum_pool(name="psum", bufs=8))
+        psum = ctx.enter_context(tc.psum_pool(name="psum", bufs=BANKS))
         ctx.enter_context(tc.manual_schedule())
 
         w_dram = {"k": wk, "q": wq}
         w_raw = {}
         for w in ("k", "q"):
             w_raw[w] = keep.tile([P, NT, D], BF16, name="w_raw_" + w)
-        x_raw = {}
-        x_blocks = {}
+        x_raw = []
         for b in range(NB):
-            if b < TURNED:
-                x_raw[b] = keep.tile([P, NT, D], BF16, name="x_raw_%d" % b)
-            else:
-                x_raw[b] = keep.tile([P, NT, D // 2], BF16, name="x_raw_%d" % b)
-                x_blocks[b] = keep.tile([P, BLOCKS, 2 * BLOCK], BF16, name="x_blocks_%d" % b, align_bytes=64)
+            x_raw.append(keep.tile([P, NT, D if b < TURNED else D_PASS], BF16, name="x_raw_%d" % b))
+        x_blocks = {}
+        for b in range(TURNED, NB):
+            x_blocks[b] = keep.tile([P, GROUPS, 2 * BLOCK], BF16, name="x_blocks_%d" % b, align_bytes=64)
 
         def load_weights(w):
             tiles = w_dram[w][0, :, :].rearrange("(p t) d -> p t d", t=NT)
             for t in range(NT):
                 nc.sync.dma_start(out=w_raw[w][:, t, :], in_=tiles[:, t, :])
 
-        load_weights("k")
-        for j in range(NT):
-            nc.sync.dma_start(out=x_raw[0][:, j, :], in_=x[0, j * P : (j + 1) * P, :])
-        load_weights("q")
-        for j in range(NT):
-            nc.sync.dma_start(out=x_raw[1][:, j, :], in_=x[1, j * P : (j + 1) * P, :])
-        beta_bf = keep.tile([P, 1], BF16, name="beta_bf")
-        for b in range(TURNED, NB):
-            nc.sync.dma_start(out=x_raw[b][:], in_=x[b, :, 0 : D // 2].rearrange("(j p) d -> p j d", p=P))
-            if b == TURNED:
-                nc.sync.dma_start(out=beta_bf[:], in_=betas.partition_broadcast(P))
+        def load_tokens(b):
+            for j in range(NT):
+                nc.sync.dma_start(out=x_raw[b][:, j, :], in_=x[b, j * P : (j + 1) * P, :])
+
+        def load_blocks(b):
             for u in range(2):
                 for q in (0, 2, 1, 3):
-                    first = 512 + 256 * u + 2 * BLOCK * q
+                    first = D_PASS + 256 * u + 2 * BLOCK * q
                     nc.sync.dma_start(
                         out=x_blocks[b][BLOCK * q + u : BLOCK * (q + 1) : 2, :, :],
-                        in_=x[b, :, first : first + 2 * BLOCK].rearrange("(c n) f -> n c f", c=BLOCKS),
+                        in_=x[b, :, first : first + 2 * BLOCK].rearrange("(c n) f -> n c f", c=GROUPS),
                     )
+
+        load_weights("k")
+        load_tokens(0)
+        load_weights("q")
+        load_tokens(1)
+        beta_bf = keep.tile([P, 1], BF16, name="beta_bf")
+        for b in range(TURNED, NB):
+            nc.sync.dma_start(out=x_raw[b][:], in_=x[b, :, 0:D_PASS].rearrange("(j p) d -> p j d", p=P))
+            if b == TURNED:
+                nc.sync.dma_start(out=beta_bf[:], in_=betas.partition_broadcast(P))
+            load_blocks(b)
 
         zeros = keep.tile([P, BANK], BF16, name="zeros")
         nc.vector.memset(zeros[:], 0.0)
         ident = keep.tile([P, P], F32, name="ident")
         make_identity(nc, ident[:])
-        off_diag = keep.tile([P, P], F32, name="off_diag")
-        nc.vector.tensor_scalar(
-            out=off_diag[:], in0=ident[:], scalar1=1.0, scalar2=LOWEST, op0=ALU.subtract, op1=ALU.mult
-        )
-        mask = keep.tile([P, P], F32, name="mask")
-        nc.vector.scalar_tensor_tensor(
-            out=mask[:], in0=ident[:], scalar=MASKED, in1=off_diag[:], op0=ALU.mult, op1=ALU.add
-        )
-        m_grp = {}
         m_code = {}
         m_scale = {}
         for side, root in (("q", MASK_ROOT), ("k", -MASK_ROOT)):
-            m_grp[side] = keep.tile([P, P, 4], BF16, name="m_grp_" + side, align_bytes=64)
+            m_grp = keep.tile([P, P, 4], BF16, name="m_grp_" + side, align_bytes=64)
             m_code[side] = keep.tile([P, P], U32, name="m_code_" + side, align_bytes=64)
             m_scale[side] = keep.tile([P, P], U8, name="m_scale_" + side, align_bytes=64)
-            nc.gpsimd.memset(m_grp[side][:], 0.0)
-            nc.vector.tensor_scalar(
-                out=m_grp[side][:, :, 0], in0=ident[:], scalar1=root, scalar2=None, op0=ALU.mult
-            )
-        for side in ("q", "k"):
+            nc.gpsimd.memset(m_grp[:], 0.0)
+            nc.vector.tensor_scalar(out=m_grp[:, :, 0], in0=ident[:], scalar1=root, scalar2=None, op0=ALU.mult)
             nc.vector.quantize_mx(
                 out=m_code[side][:].bitcast(FP8X4),
                 scales=m_scale[side][:],
-                in_=m_grp[side][:].rearrange("p n t -> p (n t)"),
+                in_=m_grp[:].rearrange("p n t -> p (n t)"),
             )
         neg_top = keep.tile([P, P], F32, name="neg_top")
         nc.vector.memset(neg_top[:], 0.0)
         sums = keep.tile([P, P], F32, name="sums")
         nc.vector.memset(sums[:], 1.0)
-        own_min = keep.tile([P, ROW_TILES], F32, name="own_min")
+        unread_v = []
         unread_s = []
-        unread_w = []
         for r in range(TURNS):
+            unread_v.append(keep.tile([P, N], BF16, name="unread_v_%d" % r))
             unread_s.append(keep.tile([P, N], BF16, name="unread_s_%d" % r))
-            unread_w.append(keep.tile([P, N], BF16, name="unread_w_%d" % r))
         beta_f = keep.tile([P, 1], F32, name="beta_f")
         neg_beta = keep.tile([P, 1], F32, name="neg_beta")
         inv_beta = keep.tile([P, 1], F32, name="inv_beta")
@@ -149,7 +137,6 @@ def tile_multiheadenergyattention_pa_t_kernel(tc, x, wk, wq, betas, out):
         h_code = {}
         h_scale = {}
         banks = {}
-        shifted = {}
 
         def new_bank(key):
             banks[key] = psum.tile([P, BANK], F32, name="bank", tag="bank")
@@ -161,13 +148,15 @@ def tile_multiheadenergyattention_pa_t_kernel(tc, x, wk, wq, betas, out):
             else:
                 nc.scalar.copy(out=dst, in_=src)
 
-        def idle_matmul(bank, width):
-            nc.tensor.matmul(out=bank[:, 0:width], lhsT=zeros[:, 0:P], rhs=zeros[:, 0:width], start=True, stop=True)
+        def idle_matmuls(bank, widths):
+            for width in widths:
+                nc.tensor.matmul(
+                    out=bank[:, 0:width], lhsT=zeros[:, 0:P], rhs=zeros[:, 0:width], start=True, stop=True
+                )
 
-        def flip(key, raw_rows, idle=()):
+        def flip(key, raw_rows, idle):
             bank = new_bank(key)
-            for width in idle:
-                idle_matmul(bank, width)
+            idle_matmuls(bank, idle)
             words = raw_rows.bitcast(F32)
             for c in range(4):
                 nc.tensor.transpose(bank[:, c * P : (c + 1) * P], words[:, c * P : (c + 1) * P], ident[:])
@@ -190,67 +179,58 @@ def tile_multiheadenergyattention_pa_t_kernel(tc, x, wk, wq, betas, out):
                 out=w_code[w][:, t, :].bitcast(FP8X4), scales=w_scale[w][:, t, :], in_=w_grp[w][:, t, :]
             )
 
+        def new_tokens(b, shape):
+            if b not in x_grp:
+                x_grp[b] = pairs.tile([P] + shape, BF16, name="x_grp", tag="x_grp", align_bytes=64)
+                packed = [P, shape[0], shape[1] // 4]
+                x_code[b] = triples.tile(packed, U32, name="x_code", tag="x_code", align_bytes=64)
+                x_scale[b] = triples.tile(packed, U8, name="x_scale", tag="x_scale", align_bytes=64)
+
         def flip_tokens(b, j, *idle):
             flip(("x", b, j), x_raw[b][:, j, :], idle)
 
         def regroup_tokens(b, j, engine):
-            if b not in x_grp:
-                x_grp[b] = pairs.tile([P, NT, D], BF16, name="x_grp", tag="x_grp", align_bytes=64)
-                x_code[b] = triples.tile([P, NT, D // 4], U32, name="x_code", tag="x_code", align_bytes=64)
-                x_scale[b] = triples.tile([P, NT, D // 4], U8, name="x_scale", tag="x_scale", align_bytes=64)
+            new_tokens(b, [NT, D])
             regroup(engine, ("x", b, j), x_grp[b][:, j, :])
 
         def flip_pair(b, h, *idle):
-            bank = new_bank(("p", b, h))
-            for width in idle:
-                idle_matmul(bank, width)
+            bank = new_bank(("pair", b, h))
+            idle_matmuls(bank, idle)
             for r in range(2):
                 words = x_raw[b][:, 2 * h + r, :].bitcast(F32)
                 for u in range(2):
                     at = (2 * r + u) * P
                     nc.tensor.transpose(bank[:, at : at + P], words[:, u * P : (u + 1) * P], ident[:])
 
-        def new_halves(b):
-            if b not in x_grp:
-                x_grp[b] = pairs.tile([P, 2, 4 * N], BF16, name="x_grp", tag="x_grp", align_bytes=64)
-                x_code[b] = triples.tile([P, 2, N], U32, name="x_code", tag="x_code", align_bytes=64)
-                x_scale[b] = triples.tile([P, 2, N], U8, name="x_scale", tag="x_scale", align_bytes=64)
-
         def regroup_pair(b, h, engine):
-            new_halves(b)
+            new_tokens(b, [PASSES, 4 * N])
             copy_out(
                 engine,
                 x_grp[b][:, 0, h * 2 * N : (h + 1) * 2 * N].bitcast(F32).rearrange("p (j r u) -> p j r u", j=2, u=2),
-                banks[("p", b, h)][:].rearrange("p (j u r) -> p j r u", j=2, u=2),
+                banks[("pair", b, h)][:].rearrange("p (j u r) -> p j r u", j=2, u=2),
             )
 
         def turn_blocks(b):
-            new_halves(b)
+            new_tokens(b, [PASSES, 4 * N])
             nc.vector.transpose(
                 out=x_grp[b][:, 1, :].bitcast(F32), in_=x_blocks[b][:].rearrange("p c f -> p (c f)").bitcast(F32)
             )
 
-        def quantise_half(b, g):
+        def quantise_x(b, part):
             nc.vector.quantize_mx(
-                out=x_code[b][:, g, :].bitcast(FP8X4), scales=x_scale[b][:, g, :], in_=x_grp[b][:, g, :]
+                out=x_code[b][:, part, :].bitcast(FP8X4), scales=x_scale[b][:, part, :], in_=x_grp[b][:, part, :]
             )
 
-        def quantise_tokens(b, j):
-            nc.vector.quantize_mx(
-                out=x_code[b][:, j, :].bitcast(FP8X4), scales=x_scale[b][:, j, :], in_=x_grp[b][:, j, :]
-            )
-
-        def moving(tiles, b, j, g):
+        def moving(packed, b, j, g):
             if b < TURNED:
-                return tiles[b][:, j, g * P : (g + 1) * P]
-            return tiles[b][:, g, j * P : (j + 1) * P]
+                return packed[b][:, j, g * P : (g + 1) * P]
+            return packed[b][:, g, j * P : (j + 1) * P]
 
         def project(b, w, j, *idle):
             bank = new_bank(("h", b, w, j))
-            for width in idle:
-                idle_matmul(bank, width)
+            idle_matmuls(bank, idle)
             for t in range(NT):
-                for g in range(2):
+                for g in range(PASSES):
                     cols = slice(g * P, (g + 1) * P)
                     nc.tensor.matmul_mx(
                         out=bank[:, t * P : (t + 1) * P],
@@ -259,7 +239,7 @@ def tile_multiheadenergyattention_pa_t_kernel(tc, x, wk, wq, betas, out):
                         rhs=moving(x_code, b, j, g).bitcast(FP8X4),
                         rhs_scale=moving(x_scale, b, j, g),
                         start=(g == 0),
-                        stop=(g == 1),
+                        stop=(g == PASSES - 1),
                     )
 
         def regroup_heads(b, w, j, engine):
@@ -288,62 +268,7 @@ def tile_multiheadenergyattention_pa_t_kernel(tc, x, wk, wq, betas, out):
                 in_=h_grp[(b, "q")][:, cols, :].rearrange("p n t -> p (n t)"),
             )
 
-        def own_keys(j):
-            return slice(N - P, N) if j % 2 else slice(0, P)
-
-        def other_keys(j):
-            return slice(0, N - P) if j % 2 else slice(P, N)
-
         def scores(b, j):
-            bank = new_bank(("a", b, j))
-            queries = slice(j * P, (j + 1) * P)
-            half = N // 2
-            own = (j // 2) * half
-            for at, first in ((0, half - own if j % 2 else own), (half, own if j % 2 else half - own)):
-                keys = slice(first, first + half)
-                nc.tensor.matmul_mx(
-                    out=bank[:, at : at + half],
-                    lhsT=h_code[(b, "q")][:, queries].bitcast(FP8X4),
-                    lhsT_scale=h_scale[(b, "q")][:, queries],
-                    rhs=h_code[(b, "k")][:, keys].bitcast(FP8X4),
-                    rhs_scale=h_scale[(b, "k")][:, keys],
-                    start=True,
-                    stop=True,
-                )
-
-        def shift_own(b, j):
-            shifted[(b, j)] = rows.tile([P, N], F32, name="shifted", tag="shifted")
-            nc.vector.scalar_tensor_tensor(
-                out=shifted[(b, j)][:, own_keys(j)],
-                in0=banks[("a", b, j)][:, own_keys(j)],
-                scalar=neg_beta[:, 0:1],
-                in1=mask[:],
-                op0=ALU.mult,
-                op1=ALU.max,
-            )
-
-        def least_own(b, j):
-            c = b * NT + j
-            nc.vector.tensor_reduce(
-                out=own_min[:, c : c + 1],
-                in_=shifted[(b, j)][:, own_keys(j)],
-                axis=mybir.AxisListType.X,
-                op=ALU.min,
-            )
-
-        def shift_others(b, j):
-            c = b * NT + j
-            nc.vector.tensor_scalar(
-                out=shifted[(b, j)][:, other_keys(j)],
-                in0=banks[("a", b, j)][:, other_keys(j)],
-                scalar1=neg_beta[:, 0:1],
-                scalar2=own_min[:, c : c + 1],
-                op0=ALU.mult,
-                op1=ALU.min,
-                accum_out=neg_top[:, c : c + 1],
-            )
-
-        def masked_scores(b, j):
             bank = new_bank(("a", b, j))
             own = slice(j * P, (j + 1) * P)
             nc.tensor.matmul_mx(
@@ -365,10 +290,10 @@ def tile_multiheadenergyattention_pa_t_kernel(tc, x, wk, wq, betas, out):
                 stop=True,
             )
 
-        def masked_top(b, j):
+        def row_top(b, j):
             c = b * NT + j
             nc.vector.tensor_scalar(
-                out=unread_w[c % TURNS][:],
+                out=unread_v[c % TURNS][:],
                 in0=banks[("a", b, j)][:],
                 scalar1=neg_beta[:, 0:1],
                 scalar2=None,
@@ -377,7 +302,7 @@ def tile_multiheadenergyattention_pa_t_kernel(tc, x, wk, wq, betas, out):
                 accum_out=neg_top[:, c : c + 1],
             )
 
-        def masked_exp(b, j):
+        def exp_sum(b, j):
             c = b * NT + j
             nc.scalar.activation(
                 out=unread_s[c % TURNS][:],
@@ -385,17 +310,6 @@ def tile_multiheadenergyattention_pa_t_kernel(tc, x, wk, wq, betas, out):
                 func=ACT.Exp,
                 bias=neg_top[:, c : c + 1],
                 scale=beta_f[:, 0:1],
-                accum_out=sums[:, c : c + 1],
-            )
-
-        def exp_sum(b, j):
-            c = b * NT + j
-            nc.scalar.activation(
-                out=unread_s[c % TURNS][:],
-                in_=shifted[(b, j)][:],
-                func=ACT.Exp,
-                bias=neg_top[:, c : c + 1],
-                scale=-1.0,
                 accum_out=sums[:, c : c + 1],
             )
 
@@ -419,94 +333,78 @@ def tile_multiheadenergyattention_pa_t_kernel(tc, x, wk, wq, betas, out):
         run = {
             "flip_w": flip_weights,
             "flip_x": flip_tokens,
+            "flip_p": flip_pair,
             "project": project,
             "scores": scores,
             "lay_w": regroup_weights,
             "lay_x": regroup_tokens,
-            "lay_h": regroup_heads,
-            "quant_w": quantise_weights,
-            "quant_x": quantise_tokens,
-            "flip_p": flip_pair,
             "lay_p": regroup_pair,
+            "lay_h": regroup_heads,
             "turn": turn_blocks,
-            "quant_h": quantise_half,
+            "quant_w": quantise_weights,
+            "quant_x": quantise_x,
             "quant_k": quantise_keys,
             "quant_q": quantise_queries,
-            "own": shift_own,
-            "others": shift_others,
-            "least": least_own,
-            "m_scores": masked_scores,
-            "m_top": masked_top,
-            "m_exp": masked_exp,
-            "beta": beta_columns,
+            "top": row_top,
             "exp": exp_sum,
+            "beta": beta_columns,
         }
 
-        def bank_readers(step):
-            kind = step[0]
-            if kind in ("flip_w", "flip_x", "flip_p"):
-                return [("lay" + kind[4:],) + step[1:3]]
-            if kind == "project":
-                return [("lay_h",) + step[1:]]
-            if kind == "m_scores":
-                return [("m_exp",) + step[1:]]
-            return [("own",) + step[1:], ("others",) + step[1:]]
+        def bare(step):
+            return step[: 4 if step[0] == "project" else 3]
 
         def needs(step):
             kind = step[0]
             if kind in ("lay_w", "lay_x", "lay_p"):
-                return [("flip" + kind[3:],) + step[1:3]]
-            if kind in ("quant_w", "quant_x"):
-                return [("lay" + kind[5:],) + step[1:3]]
+                return [("flip" + kind[3:],) + step[1:]]
+            if kind == "quant_w":
+                return [("lay_w",) + step[1:]]
+            if kind == "quant_x":
+                b, part = step[1:]
+                if b < TURNED:
+                    return [("lay_x", b, part)]
+                return [("turn", b)] if part else [("lay_p", b, 0), ("lay_p", b, 1)]
             if kind == "project":
                 b, w, j = step[1:]
-                return [("quant_w", w, t) for t in range(NT)] + (
-                    [("quant_x", b, j)] if b < TURNED else [("quant_h", b, 0), ("quant_h", b, 1)]
-                )
+                parts = [j] if b < TURNED else range(PASSES)
+                return [("quant_w", w, t) for t in range(NT)] + [("quant_x", b, part) for part in parts]
             if kind == "lay_h":
                 return [("project",) + step[1:]]
-            if kind == "quant_h":
-                return [("turn", step[1])] if step[2] else [("lay_p", step[1], 0), ("lay_p", step[1], 1)]
             if kind == "quant_k":
                 return [("lay_h", step[1], "k", j) for j in range(NT)]
             if kind == "quant_q":
                 return [("lay_h", step[1], "q", step[2])]
-            if kind == "m_top":
-                return [("m_scores",) + step[1:]]
-            if kind == "m_exp":
-                return [("m_top",) + step[1:]]
-            if kind in ("scores", "m_scores"):
+            if kind == "scores":
                 return [("quant_k", step[1]), ("quant_q",) + step[1:]]
-            if kind == "own":
-                c = step[1] * NT + step[2]
-                late = [("exp", (c - ROW_SLOTS) // NT, (c - ROW_SLOTS) % NT)] if c >= ROW_SLOTS else []
-                return [("scores",) + step[1:]] + late
-            if kind == "least":
-                return [("own",) + step[1:]]
-            if kind == "others":
-                return [("least",) + step[1:]]
+            if kind == "top":
+                return [("scores",) + step[1:], ("beta",)]
             if kind == "exp":
-                return [("others",) + step[1:]]
+                return [("top",) + step[1:]]
             return []
 
-        def weave(queues):
-            for engine in queues:
-                queues[engine] = [step for step in queues[engine] if len(step) < 2 or step[1] not in (-1,)]
+        def last_reader(step):
+            if step[0] == "project":
+                return ("lay_h",) + step[1:]
+            if step[0] == "scores":
+                return ("exp",) + step[1:]
+            return ("lay" + step[0][4:],) + step[1:]
+
+        def weave(steps):
             done = set()
             filled = []
-            at = {engine: 0 for engine in queues}
-            for turn in range(sum(len(queues[engine]) for engine in queues)):
-                for engine in queues:
-                    if at[engine] == len(queues[engine]):
+            at = {engine: 0 for engine in steps}
+            for turn in range(sum(len(steps[engine]) for engine in steps)):
+                for engine in steps:
+                    if at[engine] == len(steps[engine]):
                         continue
-                    step = queues[engine][at[engine]]
-                    name = step[:3] if step[0] in ("flip_w", "flip_x", "flip_p") else step[:4] if step[0] == "project" else step
+                    step = steps[engine][at[engine]]
+                    name = bare(step) if engine == TENSOR else step
                     wanted = needs(name)
                     if engine == TENSOR and len(filled) >= BANKS:
-                        wanted = wanted + bank_readers(filled[len(filled) - BANKS])
+                        wanted = wanted + [last_reader(filled[len(filled) - BANKS])]
                     if not all(n in done for n in wanted):
                         continue
-                    if step[0] in ("lay_w", "lay_x", "lay_h", "lay_p"):
+                    if step[0][:3] == "lay":
                         run[step[0]](*step[1:], engine)
                     else:
                         run[step[0]](*step[1:])
@@ -514,100 +412,58 @@ def tile_multiheadenergyattention_pa_t_kernel(tc, x, wk, wq, betas, out):
                         filled.append(name)
                     done.add(name)
                     at[engine] += 1
-            assert all(at[engine] == len(queues[engine]) for engine in queues)
+            assert all(at[engine] == len(steps[engine]) for engine in steps)
 
-        t_list, v_list, s_list = [], [], []
-        last = NB - 1
+        tiles = range(NT)
+        pe = []
+        ve = []
+        se = []
 
-        t_list += [("flip_w", "k", 0) + (BANK,) * WARM_UP] + [("flip_w", "k", t, IDLE) for t in (1, 2, 3)]
-        t_list += [("flip_x", 0, j, IDLE) for j in range(NT)]
-        t_list += [("project", 0, "k", 0, BRIDGE)] + [("project", 0, "k", j) for j in (1, 2, 3)]
-        t_list += [("flip_w", "q", 0, BRIDGE)] + [("flip_w", "q", t) for t in (1, 2, 3)]
-        t_list += [("flip_x", 1, j) for j in range(NT)]
-        t_list += [("project", 0, "q", 0, BRIDGE)] + [("project", 0, "q", j) for j in (1, 2, 3)]
-        s_list += [("lay_w", "k", 0), ("lay_w", "k", 2), ("lay_w", "k", 3), ("lay_x", 0, 0), ("lay_x", 0, 1), ("lay_x", 0, 2)]
-        v_list += [("lay_w", "k", 1), ("quant_w", "k", 0), ("quant_w", "k", 1)]
-        v_list += [("quant_w", "k", 2), ("quant_w", "k", 3), ("quant_x", 0, 0), ("quant_x", 0, 1), ("lay_x", 0, 3)]
-        v_list += [("quant_x", 0, 2), ("quant_x", 0, 3), ("lay_h", 0, "k", 1)]
-        s_list += [("lay_h", 0, "k", 0), ("lay_h", 0, "k", 2), ("lay_h", 0, "k", 3), ("lay_w", "q", 1), ("lay_w", "q", 3)]
-        v_list += [("lay_w", "q", 0), ("lay_w", "q", 2), ("quant_w", "q", 0), ("quant_w", "q", 1), ("quant_w", "q", 2), ("quant_w", "q", 3)]
-        s_list += [("lay_x", 1, 0), ("lay_x", 1, 2)]
-        v_list += [("lay_x", 1, 1), ("lay_x", 1, 3)] + [("quant_x", 1, j) for j in range(NT)] + [("beta",)]
-        s_list += [("lay_h", 0, "q", j) for j in range(NT)]
-        t_list += [("flip_p", 2, 0, BRIDGE), ("flip_p", 2, 1), ("project", 1, "k", 0, BRIDGE), ("project", 1, "k", 1)]
-        t_list += [("project", 1, "k", 2), ("m_scores", 0, 0), ("project", 1, "k", 3), ("m_scores", 0, 1)]
-        t_list += [("project", 1, "q", 0), ("m_scores", 0, 2), ("project", 1, "q", 1), ("m_scores", 0, 3)]
-        t_list += [("project", 1, "q", 2), ("project", 1, "q", 3), ("flip_p", 3, 0, BRIDGE), ("flip_p", 3, 1)]
-        t_list += [("project", 2, "k", 0, BRIDGE), ("project", 2, "k", 1), ("project", 2, "k", 2), ("m_scores", 1, 0)]
-        t_list += [("project", 2, "k", 3), ("m_scores", 1, 1), ("project", 2, "q", 0), ("m_scores", 1, 2)]
-        t_list += [("project", 2, "q", 1), ("m_scores", 1, 3), ("project", 2, "q", 2), ("project", 2, "q", 3)]
-        t_list += [("flip_p", 4, 0, BRIDGE), ("flip_p", 4, 1), ("project", 3, "k", 0, BRIDGE), ("project", 3, "k", 1)]
-        t_list += [("project", 3, "k", 2), ("m_scores", 2, 0), ("project", 3, "k", 3), ("m_scores", 2, 1)]
-        t_list += [("project", 3, "q", 0), ("m_scores", 2, 2), ("project", 3, "q", 1), ("m_scores", 2, 3)]
-        t_list += [("project", 3, "q", 2), ("project", 3, "q", 3), ("flip_p", 5, 0, BRIDGE), ("flip_p", 5, 1)]
-        t_list += [("project", 4, "k", 0, BRIDGE), ("project", 4, "k", 1), ("project", 4, "k", 2), ("m_scores", 3, 0)]
-        t_list += [("project", 4, "k", 3), ("m_scores", 3, 1), ("project", 4, "q", 0), ("m_scores", 3, 2)]
-        t_list += [("project", 4, "q", 1), ("m_scores", 3, 3), ("project", 4, "q", 2), ("project", 4, "q", 3)]
-        t_list += [("flip_p", 6, 0, BRIDGE), ("flip_p", 6, 1), ("project", 5, "k", 0, BRIDGE), ("project", 5, "k", 1)]
-        t_list += [("project", 5, "k", 2), ("m_scores", 4, 0), ("project", 5, "k", 3), ("m_scores", 4, 1)]
-        t_list += [("project", 5, "q", 0), ("m_scores", 4, 2), ("project", 5, "q", 1), ("m_scores", 4, 3)]
-        t_list += [("project", 5, "q", 2), ("project", 5, "q", 3), ("flip_p", 7, 0, BRIDGE), ("flip_p", 7, 1)]
-        t_list += [("project", 6, "k", 0, BRIDGE), ("project", 6, "k", 1), ("project", 6, "k", 2), ("m_scores", 5, 0)]
-        t_list += [("project", 6, "k", 3), ("m_scores", 5, 1), ("project", 6, "q", 0), ("m_scores", 5, 2)]
-        t_list += [("project", 6, "q", 1), ("m_scores", 5, 3), ("project", 6, "q", 2), ("project", 6, "q", 3)]
-        t_list += [("project", 7, "k", 0), ("project", 7, "k", 1), ("m_scores", 6, 0), ("project", 7, "k", 2)]
-        t_list += [("m_scores", 6, 1), ("project", 7, "k", 3), ("m_scores", 6, 2), ("project", 7, "q", 0)]
-        t_list += [("m_scores", 6, 3), ("project", 7, "q", 1), ("project", 7, "q", 2), ("project", 7, "q", 3)]
-        t_list += [("m_scores", 7, 0), ("m_scores", 7, 1), ("m_scores", 7, 2), ("m_scores", 7, 3)]
-        v_list += [("quant_k", 0), ("quant_q", 0, 0), ("quant_q", 0, 1), ("turn", 2)]
-        v_list += [("lay_p", 2, 0), ("lay_p", 2, 1), ("quant_q", 0, 2), ("quant_q", 0, 3)]
-        v_list += [("m_top", 0, 0), ("quant_h", 2, 0), ("m_top", 0, 1), ("m_top", 0, 2)]
-        v_list += [("quant_h", 2, 1), ("m_top", 0, 3), ("quant_k", 1), ("quant_q", 1, 0)]
-        v_list += [("quant_q", 1, 1), ("turn", 3), ("lay_p", 3, 0), ("lay_p", 3, 1)]
-        v_list += [("quant_q", 1, 2), ("quant_q", 1, 3), ("m_top", 1, 0), ("quant_h", 3, 0)]
-        v_list += [("m_top", 1, 1), ("m_top", 1, 2), ("quant_h", 3, 1), ("m_top", 1, 3)]
-        v_list += [("quant_k", 2), ("quant_q", 2, 0), ("quant_q", 2, 1), ("turn", 4)]
-        v_list += [("lay_p", 4, 0), ("lay_p", 4, 1), ("quant_q", 2, 2), ("quant_q", 2, 3)]
-        v_list += [("m_top", 2, 0), ("quant_h", 4, 0), ("m_top", 2, 1), ("m_top", 2, 2)]
-        v_list += [("quant_h", 4, 1), ("m_top", 2, 3), ("quant_k", 3), ("quant_q", 3, 0)]
-        v_list += [("quant_q", 3, 1), ("turn", 5), ("lay_p", 5, 0), ("lay_p", 5, 1)]
-        v_list += [("quant_q", 3, 2), ("quant_q", 3, 3), ("m_top", 3, 0), ("quant_h", 5, 0)]
-        v_list += [("m_top", 3, 1), ("m_top", 3, 2), ("quant_h", 5, 1), ("m_top", 3, 3)]
-        v_list += [("quant_k", 4), ("quant_q", 4, 0), ("quant_q", 4, 1), ("turn", 6)]
-        v_list += [("lay_p", 6, 0), ("lay_p", 6, 1), ("quant_q", 4, 2), ("quant_q", 4, 3)]
-        v_list += [("m_top", 4, 0), ("quant_h", 6, 0), ("m_top", 4, 1), ("m_top", 4, 2)]
-        v_list += [("quant_h", 6, 1), ("m_top", 4, 3), ("quant_k", 5), ("quant_q", 5, 0)]
-        v_list += [("quant_q", 5, 1), ("turn", 7), ("lay_p", 7, 0), ("lay_p", 7, 1)]
-        v_list += [("quant_q", 5, 2), ("quant_q", 5, 3), ("m_top", 5, 0), ("quant_h", 7, 0)]
-        v_list += [("m_top", 5, 1), ("m_top", 5, 2), ("quant_h", 7, 1), ("m_top", 5, 3)]
-        v_list += [("quant_k", 6), ("quant_q", 6, 0), ("lay_h", 6, "q", 1), ("quant_q", 6, 1)]
-        v_list += [("quant_q", 6, 2), ("quant_q", 6, 3), ("m_top", 6, 0), ("m_top", 6, 1)]
-        v_list += [("lay_h", 7, "k", 3), ("m_top", 6, 2), ("quant_k", 7), ("lay_h", 7, "q", 1)]
-        v_list += [("quant_q", 7, 0), ("m_top", 6, 3), ("quant_q", 7, 1), ("quant_q", 7, 2)]
-        v_list += [("m_top", 7, 0), ("quant_q", 7, 3), ("m_top", 7, 1), ("m_top", 7, 2)]
-        v_list += [("m_top", 7, 3)]
-        s_list += [("lay_h", 1, "k", 0), ("lay_h", 1, "k", 1), ("lay_h", 1, "k", 2), ("lay_h", 1, "k", 3)]
-        s_list += [("m_exp", 0, 0), ("lay_h", 1, "q", 0), ("m_exp", 0, 1), ("lay_h", 1, "q", 1)]
-        s_list += [("m_exp", 0, 2), ("lay_h", 1, "q", 2), ("m_exp", 0, 3), ("lay_h", 1, "q", 3)]
-        s_list += [("lay_h", 2, "k", 0), ("lay_h", 2, "k", 1), ("lay_h", 2, "k", 2), ("lay_h", 2, "k", 3)]
-        s_list += [("m_exp", 1, 0), ("lay_h", 2, "q", 0), ("m_exp", 1, 1), ("lay_h", 2, "q", 1)]
-        s_list += [("m_exp", 1, 2), ("lay_h", 2, "q", 2), ("m_exp", 1, 3), ("lay_h", 2, "q", 3)]
-        s_list += [("lay_h", 3, "k", 0), ("lay_h", 3, "k", 1), ("lay_h", 3, "k", 2), ("lay_h", 3, "k", 3)]
-        s_list += [("m_exp", 2, 0), ("lay_h", 3, "q", 0), ("m_exp", 2, 1), ("lay_h", 3, "q", 1)]
-        s_list += [("m_exp", 2, 2), ("lay_h", 3, "q", 2), ("m_exp", 2, 3), ("lay_h", 3, "q", 3)]
-        s_list += [("lay_h", 4, "k", 0), ("lay_h", 4, "k", 1), ("lay_h", 4, "k", 2), ("lay_h", 4, "k", 3)]
-        s_list += [("m_exp", 3, 0), ("lay_h", 4, "q", 0), ("m_exp", 3, 1), ("lay_h", 4, "q", 1)]
-        s_list += [("m_exp", 3, 2), ("lay_h", 4, "q", 2), ("m_exp", 3, 3), ("lay_h", 4, "q", 3)]
-        s_list += [("lay_h", 5, "k", 0), ("lay_h", 5, "k", 1), ("lay_h", 5, "k", 2), ("lay_h", 5, "k", 3)]
-        s_list += [("m_exp", 4, 0), ("lay_h", 5, "q", 0), ("m_exp", 4, 1), ("lay_h", 5, "q", 1)]
-        s_list += [("m_exp", 4, 2), ("lay_h", 5, "q", 2), ("m_exp", 4, 3), ("lay_h", 5, "q", 3)]
-        s_list += [("lay_h", 6, "k", 0), ("lay_h", 6, "k", 1), ("lay_h", 6, "k", 2), ("lay_h", 6, "k", 3)]
-        s_list += [("m_exp", 5, 0), ("lay_h", 6, "q", 0), ("m_exp", 5, 1), ("lay_h", 6, "q", 2)]
-        s_list += [("m_exp", 5, 2), ("lay_h", 6, "q", 3), ("m_exp", 5, 3), ("lay_h", 7, "k", 0)]
-        s_list += [("lay_h", 7, "k", 1), ("lay_h", 7, "k", 2), ("m_exp", 6, 0), ("m_exp", 6, 1)]
-        s_list += [("lay_h", 7, "q", 0), ("m_exp", 6, 2), ("lay_h", 7, "q", 2), ("lay_h", 7, "q", 3)]
-        s_list += [("m_exp", 6, 3), ("m_exp", 7, 0), ("m_exp", 7, 1), ("m_exp", 7, 2)]
-        s_list += [("m_exp", 7, 3)]
+        pe += [("flip_w", "k", 0) + (BANK,) * WARM_UP] + [("flip_w", "k", t, IDLE) for t in (1, 2, 3)]
+        pe += [("flip_x", 0, j, IDLE) for j in tiles]
+        pe += [("project", 0, "k", 0, BRIDGE)] + [("project", 0, "k", j) for j in (1, 2, 3)]
+        pe += [("flip_w", "q", 0, BRIDGE)] + [("flip_w", "q", t) for t in (1, 2, 3)]
+        pe += [("flip_x", 1, j) for j in tiles]
+        pe += [("project", 0, "q", 0, BRIDGE)] + [("project", 0, "q", j) for j in (1, 2, 3)]
+        se += [("lay_w", "k", t) for t in (0, 2, 3)] + [("lay_x", 0, j) for j in (0, 1, 2)]
+        ve += [("lay_w", "k", 1)] + [("quant_w", "k", t) for t in tiles]
+        ve += [("quant_x", 0, 0), ("quant_x", 0, 1), ("lay_x", 0, 3), ("quant_x", 0, 2), ("quant_x", 0, 3)]
+        se += [("lay_h", 0, "k", j) for j in (0, 2, 3)] + [("lay_w", "q", 1), ("lay_w", "q", 3)]
+        ve += [("lay_h", 0, "k", 1), ("lay_w", "q", 0), ("lay_w", "q", 2)] + [("quant_w", "q", t) for t in tiles]
+        se += [("lay_x", 1, 0), ("lay_x", 1, 2)] + [("lay_h", 0, "q", j) for j in tiles]
+        ve += [("lay_x", 1, 1), ("lay_x", 1, 3)] + [("quant_x", 1, j) for j in tiles] + [("beta",)]
 
-        weave({TENSOR: t_list, VECTOR: v_list, SCALAR: s_list})
+        for i in range(1, NB - 1):
+            pe += [("flip_p", i + 1, 0, BRIDGE), ("flip_p", i + 1, 1)]
+            pe += [("project", i, "k", 0, BRIDGE), ("project", i, "k", 1), ("project", i, "k", 2)]
+            pe += [("scores", i - 1, 0), ("project", i, "k", 3), ("scores", i - 1, 1), ("project", i, "q", 0)]
+            pe += [("scores", i - 1, 2), ("project", i, "q", 1), ("scores", i - 1, 3)]
+            pe += [("project", i, "q", 2), ("project", i, "q", 3)]
+        for i in range(NB - 2):
+            ve += [("quant_k", i), ("quant_q", i, 0), ("quant_q", i, 1), ("lay_p", i + 2, 0), ("turn", i + 2)]
+            ve += [("quant_q", i, 2), ("quant_q", i, 3), ("top", i, 0), ("quant_x", i + 2, 0)]
+            ve += [("top", i, 1), ("top", i, 2), ("quant_x", i + 2, 1), ("top", i, 3)]
+        se += [("lay_p", 2, 1)]
+        for i in range(1, NB - 2):
+            se += [("lay_h", i, "k", j) for j in tiles]
+            for j in tiles:
+                se += [("exp", i - 1, j), ("lay_h", i, "q", j)]
+            se += [("lay_p", i + 2, 1)]
+
+        i = NB - 1
+        p = NB - 2
+        pe += [("project", i, "k", 0), ("project", i, "k", 1), ("scores", p, 0), ("project", i, "k", 2)]
+        pe += [("scores", p, 1), ("project", i, "k", 3), ("scores", p, 2), ("project", i, "q", 0), ("scores", p, 3)]
+        pe += [("project", i, "q", j) for j in (1, 2, 3)] + [("scores", i, j) for j in tiles]
+        ve += [("quant_k", p), ("quant_q", p, 0), ("lay_h", p, "q", 1)] + [("quant_q", p, j) for j in (1, 2, 3)]
+        ve += [("top", p, 0), ("top", p, 1), ("lay_h", i, "k", 3), ("top", p, 2), ("quant_k", i), ("lay_h", i, "q", 1)]
+        ve += [("quant_q", i, 0), ("top", p, 3), ("quant_q", i, 1), ("quant_q", i, 2), ("top", i, 0)]
+        ve += [("quant_q", i, 3), ("top", i, 1), ("top", i, 2), ("top", i, 3)]
+        se += [("lay_h", p, "k", j) for j in tiles] + [("exp", p - 1, 0), ("lay_h", p, "q", 0), ("exp", p - 1, 1)]
+        se += [("lay_h", p, "q", 2), ("exp", p - 1, 2), ("lay_h", p, "q", 3), ("exp", p - 1, 3)]
+        se += [("lay_h", i, "k", j) for j in (0, 1, 2)] + [("exp", p, 0), ("exp", p, 1), ("lay_h", i, "q", 0)]
+        se += [("exp", p, 2), ("lay_h", i, "q", 2), ("lay_h", i, "q", 3), ("exp", p, 3)]
+        se += [("exp", i, j) for j in tiles]
+
+        weave({TENSOR: pe, VECTOR: ve, SCALAR: se})
         finish()

@@ -31,6 +31,7 @@ MASK_ROOT = 2.0**50
 TENSOR = "tensor"
 VECTOR = "vector"
 SCALAR = "scalar"
+BOTH = (5,)
 TURNS = 4
 WARM_UP = 4
 IDLE = 320
@@ -179,65 +180,57 @@ def tile_multiheadenergyattention_pa_t_kernel(tc, x, wk, wq, betas, out):
                 out=w_code[w][:, t, :].bitcast(FP8X4), scales=w_scale[w][:, t, :], in_=w_grp[w][:, t, :]
             )
 
-        def new_tokens(b, shape):
-            if b not in x_grp:
-                x_grp[b] = pairs.tile([P] + shape, BF16, name="x_grp", tag="x_grp", align_bytes=64)
-                packed = [P, shape[0], shape[1] // 4]
-                x_code[b] = triples.tile(packed, U32, name="x_code", tag="x_code", align_bytes=64)
-                x_scale[b] = triples.tile(packed, U8, name="x_scale", tag="x_scale", align_bytes=64)
-
-        def flip_tokens(b, j, *idle):
-            flip(("x", b, j), x_raw[b][:, j, :], idle)
-
-        def regroup_tokens(b, j, engine):
-            new_tokens(b, [NT, D])
-            regroup(engine, ("x", b, j), x_grp[b][:, j, :])
-
-        def flip_pair(b, h, *idle):
-            bank = new_bank(("pair", b, h))
+        def flip_tokens(b, g, j, n, *idle):
+            bank = new_bank(("x", b, g, j))
             idle_matmuls(bank, idle)
-            for r in range(2):
-                words = x_raw[b][:, 2 * h + r, :].bitcast(F32)
+            for r in range(n):
+                words = x_raw[b][:, j + r, :].bitcast(F32)
                 for u in range(2):
                     at = (2 * r + u) * P
-                    nc.tensor.transpose(bank[:, at : at + P], words[:, u * P : (u + 1) * P], ident[:])
+                    first = (2 * g + u) * P
+                    nc.tensor.transpose(bank[:, at : at + P], words[:, first : first + P], ident[:])
 
-        def regroup_pair(b, h, engine):
-            new_tokens(b, [PASSES, 4 * N])
+        def new_tokens(b):
+            if b not in x_grp:
+                x_grp[b] = pairs.tile([P, PASSES, 4 * N], BF16, name="x_grp", tag="x_grp", align_bytes=64)
+                x_code[b] = triples.tile([P, PASSES, N], U32, name="x_code", tag="x_code", align_bytes=64)
+                x_scale[b] = triples.tile([P, PASSES, N], U8, name="x_scale", tag="x_scale", align_bytes=64)
+
+        def regroup_tokens(b, g, j, n, engine):
+            new_tokens(b)
             copy_out(
                 engine,
-                x_grp[b][:, 0, h * 2 * N : (h + 1) * 2 * N].bitcast(F32).rearrange("p (j r u) -> p j r u", j=2, u=2),
-                banks[("pair", b, h)][:].rearrange("p (j u r) -> p j r u", j=2, u=2),
+                x_grp[b][:, g, 4 * j * P : 4 * (j + n) * P].bitcast(F32).rearrange("p (j r u) -> p j r u", j=n, u=2),
+                banks[("x", b, g, j)][:, 0 : 2 * n * P].rearrange("p (j u r) -> p j r u", j=n, u=2),
             )
 
         def turn_blocks(b):
-            new_tokens(b, [PASSES, 4 * N])
+            new_tokens(b)
             nc.vector.transpose(
                 out=x_grp[b][:, 1, :].bitcast(F32), in_=x_blocks[b][:].rearrange("p c f -> p (c f)").bitcast(F32)
             )
 
-        def quantise_x(b, part):
+        def quantise_tokens(b, g, j, n):
+            cols = slice(j * P, (j + n) * P)
             nc.vector.quantize_mx(
-                out=x_code[b][:, part, :].bitcast(FP8X4), scales=x_scale[b][:, part, :], in_=x_grp[b][:, part, :]
+                out=x_code[b][:, g, cols].bitcast(FP8X4),
+                scales=x_scale[b][:, g, cols],
+                in_=x_grp[b][:, g, 4 * j * P : 4 * (j + n) * P],
             )
-
-        def moving(packed, b, j, g):
-            if b < TURNED:
-                return packed[b][:, j, g * P : (g + 1) * P]
-            return packed[b][:, g, j * P : (j + 1) * P]
 
         def project(b, w, j, *idle):
             bank = new_bank(("h", b, w, j))
             idle_matmuls(bank, idle)
             for t in range(NT):
                 for g in range(PASSES):
-                    cols = slice(g * P, (g + 1) * P)
+                    rows = slice(g * P, (g + 1) * P)
+                    tokens = slice(j * P, (j + 1) * P)
                     nc.tensor.matmul_mx(
                         out=bank[:, t * P : (t + 1) * P],
-                        lhsT=w_code[w][:, t, cols].bitcast(FP8X4),
-                        lhsT_scale=w_scale[w][:, t, cols],
-                        rhs=moving(x_code, b, j, g).bitcast(FP8X4),
-                        rhs_scale=moving(x_scale, b, j, g),
+                        lhsT=w_code[w][:, t, rows].bitcast(FP8X4),
+                        lhsT_scale=w_scale[w][:, t, rows],
+                        rhs=x_code[b][:, g, tokens].bitcast(FP8X4),
+                        rhs_scale=x_scale[b][:, g, tokens],
                         start=(g == 0),
                         stop=(g == PASSES - 1),
                     )
@@ -330,19 +323,18 @@ def tile_multiheadenergyattention_pa_t_kernel(tc, x, wk, wq, betas, out):
             )
             nc.sync.dma_start(out=out.rearrange("b o (j p) -> (b o j) p", p=P), in_=energy[0:ROW_TILES, :])
 
+        tiles = range(NT)
         run = {
             "flip_w": flip_weights,
             "flip_x": flip_tokens,
-            "flip_p": flip_pair,
             "project": project,
             "scores": scores,
             "lay_w": regroup_weights,
             "lay_x": regroup_tokens,
-            "lay_p": regroup_pair,
             "lay_h": regroup_heads,
             "turn": turn_blocks,
             "quant_w": quantise_weights,
-            "quant_x": quantise_x,
+            "quant_x": quantise_tokens,
             "quant_k": quantise_keys,
             "quant_q": quantise_queries,
             "top": row_top,
@@ -351,23 +343,29 @@ def tile_multiheadenergyattention_pa_t_kernel(tc, x, wk, wq, betas, out):
         }
 
         def bare(step):
-            return step[: 4 if step[0] == "project" else 3]
+            return step[: {"flip_w": 3, "flip_x": 5, "project": 4, "scores": 3}[step[0]]]
+
+        def bank_tiles(b):
+            return 1 if b == 0 else 2
+
+        def quant_tiles(b):
+            return NT if b >= TURNED else bank_tiles(b)
 
         def needs(step):
             kind = step[0]
-            if kind in ("lay_w", "lay_x", "lay_p"):
+            if kind in ("lay_w", "lay_x"):
                 return [("flip" + kind[3:],) + step[1:]]
             if kind == "quant_w":
                 return [("lay_w",) + step[1:]]
             if kind == "quant_x":
-                b, part = step[1:]
-                if b < TURNED:
-                    return [("lay_x", b, part)]
-                return [("turn", b)] if part else [("lay_p", b, 0), ("lay_p", b, 1)]
+                b, g, j, n = step[1:]
+                if g == 1 and b >= TURNED:
+                    return [("turn", b)]
+                return [("lay_x", b, g, r, bank_tiles(b)) for r in range(j, j + n, bank_tiles(b))]
             if kind == "project":
                 b, w, j = step[1:]
-                parts = [j] if b < TURNED else range(PASSES)
-                return [("quant_w", w, t) for t in range(NT)] + [("quant_x", b, part) for part in parts]
+                n = quant_tiles(b)
+                return [("quant_w", w, t) for t in tiles] + [("quant_x", b, g, j // n * n, n) for g in range(PASSES)]
             if kind == "lay_h":
                 return [("project",) + step[1:]]
             if kind == "quant_k":
@@ -414,41 +412,44 @@ def tile_multiheadenergyattention_pa_t_kernel(tc, x, wk, wq, betas, out):
                     at[engine] += 1
             assert all(at[engine] == len(steps[engine]) for engine in steps)
 
-        tiles = range(NT)
         pe = []
         ve = []
         se = []
 
         pe += [("flip_w", "k", 0) + (BANK,) * WARM_UP] + [("flip_w", "k", t, IDLE) for t in (1, 2, 3)]
-        pe += [("flip_x", 0, j, IDLE) for j in tiles]
+        for j in tiles:
+            pe += [("flip_x", 0, 0, j, 1, IDLE), ("flip_x", 0, 1, j, 1)]
         pe += [("project", 0, "k", 0, BRIDGE)] + [("project", 0, "k", j) for j in (1, 2, 3)]
         pe += [("flip_w", "q", 0, BRIDGE)] + [("flip_w", "q", t) for t in (1, 2, 3)]
-        pe += [("flip_x", 1, j) for j in tiles]
+        pe += [("flip_x", 1, g, j, 2) for j in (0, 2) for g in range(PASSES)]
         pe += [("project", 0, "q", 0, BRIDGE)] + [("project", 0, "q", j) for j in (1, 2, 3)]
-        se += [("lay_w", "k", t) for t in (0, 2, 3)] + [("lay_x", 0, j) for j in (0, 1, 2)]
+        se += [("lay_w", "k", t) for t in (0, 2, 3)] + [("lay_x", 0, g, j, 1) for j in tiles for g in range(PASSES)]
         ve += [("lay_w", "k", 1)] + [("quant_w", "k", t) for t in tiles]
-        ve += [("quant_x", 0, 0), ("quant_x", 0, 1), ("lay_x", 0, 3), ("quant_x", 0, 2), ("quant_x", 0, 3)]
-        se += [("lay_h", 0, "k", j) for j in (0, 2, 3)] + [("lay_w", "q", 1), ("lay_w", "q", 3)]
-        ve += [("lay_h", 0, "k", 1), ("lay_w", "q", 0), ("lay_w", "q", 2)] + [("quant_w", "q", t) for t in tiles]
-        se += [("lay_x", 1, 0), ("lay_x", 1, 2)] + [("lay_h", 0, "q", j) for j in tiles]
-        ve += [("lay_x", 1, 1), ("lay_x", 1, 3)] + [("quant_x", 1, j) for j in tiles] + [("beta",)]
+        ve += [("quant_x", 0, g, j, 1) for j in tiles for g in range(PASSES)]
+        se += [("lay_h", 0, "k", j) for j in tiles] + [("lay_w", "q", 1), ("lay_w", "q", 3)]
+        ve += [("lay_w", "q", 0), ("lay_w", "q", 2)] + [("quant_w", "q", t) for t in tiles]
+        se += [("lay_x", 1, 0, 0, 2), ("lay_x", 1, 1, 0, 2), ("lay_x", 1, 1, 2, 2)] + [("lay_h", 0, "q", j) for j in tiles]
+        ve += [("lay_x", 1, 0, 2, 2)]
+        ve += [("quant_x", 1, g, j, 2) for j in (0, 2) for g in range(PASSES)] + [("beta",)]
 
         for i in range(1, NB - 1):
-            pe += [("flip_p", i + 1, 0, BRIDGE), ("flip_p", i + 1, 1)]
+            pe += [("flip_x", i + 1, 0, 0, 2, BRIDGE), ("flip_x", i + 1, 0, 2, 2)]
             pe += [("project", i, "k", 0, BRIDGE), ("project", i, "k", 1), ("project", i, "k", 2)]
             pe += [("scores", i - 1, 0), ("project", i, "k", 3), ("scores", i - 1, 1), ("project", i, "q", 0)]
             pe += [("scores", i - 1, 2), ("project", i, "q", 1), ("scores", i - 1, 3)]
             pe += [("project", i, "q", 2), ("project", i, "q", 3)]
         for i in range(NB - 2):
-            ve += [("quant_k", i), ("quant_q", i, 0), ("quant_q", i, 1), ("lay_p", i + 2, 0), ("turn", i + 2)]
-            ve += [("quant_q", i, 2), ("quant_q", i, 3), ("top", i, 0), ("quant_x", i + 2, 0)]
-            ve += [("top", i, 1), ("top", i, 2), ("quant_x", i + 2, 1), ("top", i, 3)]
-        se += [("lay_p", 2, 1)]
+            ve += [("quant_k", i), ("quant_q", i, 0), ("quant_q", i, 1), ("lay_x", i + 2, 0, 0, 2)]
+            ve += [("lay_x", i + 2, 0, 2, 2)] if i + 2 in BOTH else []
+            ve += [("turn", i + 2)]
+            ve += [("quant_q", i, 2), ("quant_q", i, 3), ("top", i, 0), ("quant_x", i + 2, 0, 0, NT)]
+            ve += [("top", i, 1), ("top", i, 2), ("quant_x", i + 2, 1, 0, NT), ("top", i, 3)]
+        se += [("lay_x", 2, 0, 2, 2)]
         for i in range(1, NB - 2):
             se += [("lay_h", i, "k", j) for j in tiles]
             for j in tiles:
                 se += [("exp", i - 1, j), ("lay_h", i, "q", j)]
-            se += [("lay_p", i + 2, 1)]
+            se += [] if i + 2 in BOTH else [("lay_x", i + 2, 0, 2, 2)]
 
         i = NB - 1
         p = NB - 2

@@ -26,12 +26,14 @@ GROUPS = 2 * N // BLOCK
 ROW_TILES = NB * NT
 FLOPS = 2 * NB * N * D * 2 * Z + 2 * NB * N * N * Z
 
-TURNED = 2
+TURNED = 3
 MASK_ROOT = 2.0**50
 TENSOR = "tensor"
 VECTOR = "vector"
 SCALAR = "scalar"
 BOTH = (5,)
+HEAD = 16
+LAG = 4
 TURNS = 4
 WARM_UP = 4
 IDLE = 320
@@ -44,28 +46,28 @@ def tile_multiheadenergyattention_pa_t_kernel(tc, x, wk, wq, betas, out):
         keep = ctx.enter_context(tc.tile_pool(name="keep", bufs=1))
         pairs = ctx.enter_context(tc.tile_pool(name="pairs", bufs=2))
         triples = ctx.enter_context(tc.tile_pool(name="triples", bufs=3))
-        psum = ctx.enter_context(tc.psum_pool(name="psum", bufs=BANKS))
+        psum = ctx.enter_context(tc.psum_pool(name="psum", bufs=1))
         ctx.enter_context(tc.manual_schedule())
 
         w_dram = {"k": wk, "q": wq}
-        w_raw = {}
-        for w in ("k", "q"):
-            w_raw[w] = keep.tile([P, NT, D], BF16, name="w_raw_" + w)
-        x_raw = []
-        for b in range(NB):
-            x_raw.append(keep.tile([P, NT, D if b < TURNED else D_PASS], BF16, name="x_raw_%d" % b))
+        early = [("k", 0), (0, 0), (0, 1), ("k", 1), (0, 2), ("k", 2), (0, 3), ("k", 3)]
+        early += [("q", t) for t in range(NT)] + [(b, j) for b in range(1, TURNED) for j in range(NT)]
+        raw = {}
+        for tile in early:
+            raw[tile] = keep.tile([P, D], BF16, name="raw_%s_%d" % tile)
+        x_raw = {}
         x_blocks = {}
         for b in range(TURNED, NB):
+            x_raw[b] = keep.tile([P, NT, D_PASS], BF16, name="x_raw_%d" % b)
             x_blocks[b] = keep.tile([P, GROUPS, 2 * BLOCK], BF16, name="x_blocks_%d" % b, align_bytes=64)
 
-        def load_weights(w):
-            tiles = w_dram[w][0, :, :].rearrange("(p t) d -> p t d", t=NT)
-            for t in range(NT):
-                nc.sync.dma_start(out=w_raw[w][:, t, :], in_=tiles[:, t, :])
-
-        def load_tokens(b):
-            for j in range(NT):
-                nc.sync.dma_start(out=x_raw[b][:, j, :], in_=x[b, j * P : (j + 1) * P, :])
+        def load_tile(tile):
+            s, i = tile
+            if s in w_dram:
+                source = w_dram[s][0, :, :].rearrange("(p t) d -> p t d", t=NT)[:, i, :]
+            else:
+                source = x[s, i * P : (i + 1) * P, :]
+            nc.sync.dma_start(out=raw[tile][:], in_=source)
 
         def load_blocks(b):
             for u in range(2):
@@ -76,15 +78,12 @@ def tile_multiheadenergyattention_pa_t_kernel(tc, x, wk, wq, betas, out):
                         in_=x[b, :, first : first + 2 * BLOCK].rearrange("(c n) f -> n c f", c=GROUPS),
                     )
 
-        load_weights("k")
-        load_tokens(0)
-        load_weights("q")
-        load_tokens(1)
+        for tile in early:
+            load_tile(tile)
         beta_bf = keep.tile([P, 1], BF16, name="beta_bf")
+        nc.sync.dma_start(out=beta_bf[:], in_=betas.partition_broadcast(P))
         for b in range(TURNED, NB):
             nc.sync.dma_start(out=x_raw[b][:], in_=x[b, :, 0:D_PASS].rearrange("(j p) d -> p j d", p=P))
-            if b == TURNED:
-                nc.sync.dma_start(out=beta_bf[:], in_=betas.partition_broadcast(P))
             load_blocks(b)
 
         zeros = keep.tile([P, BANK], BF16, name="zeros")
@@ -124,24 +123,32 @@ def tile_multiheadenergyattention_pa_t_kernel(tc, x, wk, wq, betas, out):
             nc.vector.reciprocal(out=inv_beta[:], in_=beta_f[:])
             nc.vector.tensor_scalar(out=neg_inv_beta[:], in0=inv_beta[:], scalar1=-1.0, scalar2=None, op0=ALU.mult)
 
-        w_grp = {}
-        w_code = {}
-        w_scale = {}
+        grp = {}
+        code = {}
+        scale = {}
         for w in ("k", "q"):
-            w_grp[w] = keep.tile([P, NT, D], BF16, name="w_grp_" + w, align_bytes=64)
-            w_code[w] = keep.tile([P, NT, D // 4], U32, name="w_code_" + w, align_bytes=64)
-            w_scale[w] = keep.tile([P, NT, D // 4], U8, name="w_scale_" + w, align_bytes=64)
-        x_grp = {}
-        x_code = {}
-        x_scale = {}
+            grp[w] = keep.tile([P, 4 * D], BF16, name="w_grp_" + w, align_bytes=64)
+            code[w] = keep.tile([P, D], U32, name="w_code_" + w, align_bytes=64)
+            scale[w] = keep.tile([P, D], U8, name="w_scale_" + w, align_bytes=64)
         h_grp = {}
         h_code = {}
         h_scale = {}
         banks = {}
 
-        def new_bank(key):
-            banks[key] = psum.tile([P, BANK], F32, name="bank", tag="bank")
+        def new_bank(key, at):
+            banks[key] = psum.tile([P, BANK], F32, name="bank_%d" % at, tag="bank_%d" % at)
             return banks[key]
+
+        def new_tokens(b):
+            if b not in grp:
+                grp[b] = pairs.tile([P, 4 * D], BF16, name="x_grp", tag="x_grp", align_bytes=64)
+                code[b] = triples.tile([P, D], U32, name="x_code", tag="x_code", align_bytes=64)
+                scale[b] = triples.tile([P, D], U8, name="x_scale", tag="x_scale", align_bytes=64)
+
+        def columns(s, i, g):
+            by_tile = s in w_dram or s < TURNED
+            at = 2 * i + g if by_tile else NT * g + i
+            return slice(at * P, (at + 1) * P)
 
         def copy_out(engine, dst, src):
             if engine == VECTOR:
@@ -149,88 +156,79 @@ def tile_multiheadenergyattention_pa_t_kernel(tc, x, wk, wq, betas, out):
             else:
                 nc.scalar.copy(out=dst, in_=src)
 
+        def quantise(s, cols):
+            nc.vector.quantize_mx(
+                out=code[s][:, cols].bitcast(FP8X4),
+                scales=scale[s][:, cols],
+                in_=grp[s][:, 4 * cols.start : 4 * cols.stop],
+            )
+
         def idle_matmuls(bank, widths):
             for width in widths:
                 nc.tensor.matmul(
                     out=bank[:, 0:width], lhsT=zeros[:, 0:P], rhs=zeros[:, 0:width], start=True, stop=True
                 )
 
-        def flip(key, raw_rows, idle):
-            bank = new_bank(key)
+        def flip(s, i, at, *idle):
+            bank = new_bank(("flip", s, i), at)
             idle_matmuls(bank, idle)
-            words = raw_rows.bitcast(F32)
-            for c in range(4):
-                nc.tensor.transpose(bank[:, c * P : (c + 1) * P], words[:, c * P : (c + 1) * P], ident[:])
+            words = raw[(s, i)][:].bitcast(F32)
+            for q in range(4):
+                nc.tensor.transpose(bank[:, q * P : (q + 1) * P], words[:, q * P : (q + 1) * P], ident[:])
 
-        def regroup(engine, key, grp_rows):
+        def lay(s, i, engine):
+            if s not in w_dram:
+                new_tokens(s)
             copy_out(
                 engine,
-                grp_rows.bitcast(F32).rearrange("p (g r u) -> p g r u", g=2, u=2),
-                banks[key][:].rearrange("p (g u r) -> p g r u", g=2, u=2),
+                grp[s][:, i * D : (i + 1) * D].bitcast(F32).rearrange("p (g r u) -> p g r u", g=2, u=2),
+                banks[("flip", s, i)][:].rearrange("p (g u r) -> p g r u", g=2, u=2),
             )
 
-        def flip_weights(w, t, *idle):
-            flip(("w", w, t), w_raw[w][:, t, :], idle)
+        def quant(s, i):
+            quantise(s, slice(2 * i * P, 2 * (i + 1) * P))
 
-        def regroup_weights(w, t, engine):
-            regroup(engine, ("w", w, t), w_grp[w][:, t, :])
-
-        def quantise_weights(w, t):
-            nc.vector.quantize_mx(
-                out=w_code[w][:, t, :].bitcast(FP8X4), scales=w_scale[w][:, t, :], in_=w_grp[w][:, t, :]
-            )
-
-        def flip_tokens(b, g, j, n, *idle):
-            bank = new_bank(("x", b, g, j))
+        def flip_pair(b, j, at, *idle):
+            bank = new_bank(("flip_pair", b, j), at)
             idle_matmuls(bank, idle)
-            for r in range(n):
+            for r in range(2):
                 words = x_raw[b][:, j + r, :].bitcast(F32)
                 for u in range(2):
-                    at = (2 * r + u) * P
-                    first = (2 * g + u) * P
-                    nc.tensor.transpose(bank[:, at : at + P], words[:, first : first + P], ident[:])
+                    q = 2 * r + u
+                    nc.tensor.transpose(bank[:, q * P : (q + 1) * P], words[:, u * P : (u + 1) * P], ident[:])
 
-        def new_tokens(b):
-            if b not in x_grp:
-                x_grp[b] = pairs.tile([P, PASSES, 4 * N], BF16, name="x_grp", tag="x_grp", align_bytes=64)
-                x_code[b] = triples.tile([P, PASSES, N], U32, name="x_code", tag="x_code", align_bytes=64)
-                x_scale[b] = triples.tile([P, PASSES, N], U8, name="x_scale", tag="x_scale", align_bytes=64)
-
-        def regroup_tokens(b, g, j, n, engine):
+        def lay_pair(b, j, engine):
             new_tokens(b)
             copy_out(
                 engine,
-                x_grp[b][:, g, 4 * j * P : 4 * (j + n) * P].bitcast(F32).rearrange("p (j r u) -> p j r u", j=n, u=2),
-                banks[("x", b, g, j)][:, 0 : 2 * n * P].rearrange("p (j u r) -> p j r u", j=n, u=2),
+                grp[b][:, 4 * j * P : 4 * (j + 2) * P].bitcast(F32).rearrange("p (j r u) -> p j r u", j=2, u=2),
+                banks[("flip_pair", b, j)][:].rearrange("p (j u r) -> p j r u", j=2, u=2),
             )
 
         def turn_blocks(b):
             new_tokens(b)
             nc.vector.transpose(
-                out=x_grp[b][:, 1, :].bitcast(F32), in_=x_blocks[b][:].rearrange("p c f -> p (c f)").bitcast(F32)
+                out=grp[b][:, 4 * N :].bitcast(F32), in_=x_blocks[b][:].rearrange("p c f -> p (c f)").bitcast(F32)
             )
 
-        def quantise_tokens(b, g, j, n):
-            cols = slice(j * P, (j + n) * P)
-            nc.vector.quantize_mx(
-                out=x_code[b][:, g, cols].bitcast(FP8X4),
-                scales=x_scale[b][:, g, cols],
-                in_=x_grp[b][:, g, 4 * j * P : 4 * (j + n) * P],
-            )
+        def quant_pass(b, g):
+            quantise(b, slice(g * N, (g + 1) * N))
 
-        def project(b, w, j, *idle):
-            bank = new_bank(("h", b, w, j))
+        def project(b, w, j, ts, at, *idle):
+            bank = banks.get(("stage_1", b, w, j))
+            if bank is None:
+                bank = new_bank(("stage_1", b, w, j), at)
             idle_matmuls(bank, idle)
-            for t in range(NT):
+            for t in ts:
                 for g in range(PASSES):
-                    rows = slice(g * P, (g + 1) * P)
-                    tokens = slice(j * P, (j + 1) * P)
+                    rows = columns(w, t, g)
+                    tokens = columns(b, j, g)
                     nc.tensor.matmul_mx(
                         out=bank[:, t * P : (t + 1) * P],
-                        lhsT=w_code[w][:, t, rows].bitcast(FP8X4),
-                        lhsT_scale=w_scale[w][:, t, rows],
-                        rhs=x_code[b][:, g, tokens].bitcast(FP8X4),
-                        rhs_scale=x_scale[b][:, g, tokens],
+                        lhsT=code[w][:, rows].bitcast(FP8X4),
+                        lhsT_scale=scale[w][:, rows],
+                        rhs=code[b][:, tokens].bitcast(FP8X4),
+                        rhs_scale=scale[b][:, tokens],
                         start=(g == 0),
                         stop=(g == PASSES - 1),
                     )
@@ -243,7 +241,7 @@ def tile_multiheadenergyattention_pa_t_kernel(tc, x, wk, wq, betas, out):
             copy_out(
                 engine,
                 h_grp[(b, w)][:, j * P : (j + 1) * P, :],
-                banks[("h", b, w, j)][:].rearrange("p (t n) -> p n t", t=NT),
+                banks[("stage_1", b, w, j)][:].rearrange("p (t n) -> p n t", t=NT),
             )
 
         def quantise_keys(b):
@@ -261,8 +259,8 @@ def tile_multiheadenergyattention_pa_t_kernel(tc, x, wk, wq, betas, out):
                 in_=h_grp[(b, "q")][:, cols, :].rearrange("p n t -> p (n t)"),
             )
 
-        def scores(b, j):
-            bank = new_bank(("a", b, j))
+        def scores(b, j, at):
+            bank = new_bank(("scores", b, j), at)
             own = slice(j * P, (j + 1) * P)
             nc.tensor.matmul_mx(
                 out=bank[:],
@@ -287,7 +285,7 @@ def tile_multiheadenergyattention_pa_t_kernel(tc, x, wk, wq, betas, out):
             c = b * NT + j
             nc.vector.tensor_scalar(
                 out=unread_v[c % TURNS][:],
-                in0=banks[("a", b, j)][:],
+                in0=banks[("scores", b, j)][:],
                 scalar1=neg_beta[:, 0:1],
                 scalar2=None,
                 op0=ALU.mult,
@@ -299,7 +297,7 @@ def tile_multiheadenergyattention_pa_t_kernel(tc, x, wk, wq, betas, out):
             c = b * NT + j
             nc.scalar.activation(
                 out=unread_s[c % TURNS][:],
-                in_=banks[("a", b, j)][:],
+                in_=banks[("scores", b, j)][:],
                 func=ACT.Exp,
                 bias=neg_top[:, c : c + 1],
                 scale=beta_f[:, 0:1],
@@ -307,13 +305,13 @@ def tile_multiheadenergyattention_pa_t_kernel(tc, x, wk, wq, betas, out):
             )
 
         def finish():
-            top_bank = new_bank("top")
+            top_bank = new_bank("top", 0)
             nc.tensor.transpose(top_bank[:, 0:P], neg_top[:], ident[:])
             top_t = keep.tile([P, P], F32, name="top_t")
             nc.vector.tensor_scalar(
                 out=top_t[:], in0=top_bank[:, 0:P], scalar1=inv_beta[:, 0:1], scalar2=None, op0=ALU.mult
             )
-            sum_bank = new_bank("sum")
+            sum_bank = new_bank("sum", 1)
             nc.tensor.transpose(sum_bank[:, 0:P], sums[:], ident[:])
             log_t = keep.tile([P, P], F32, name="log_t")
             nc.scalar.activation(out=log_t[:], in_=sum_bank[:, 0:P], func=ACT.Ln)
@@ -325,90 +323,97 @@ def tile_multiheadenergyattention_pa_t_kernel(tc, x, wk, wq, betas, out):
 
         tiles = range(NT)
         run = {
-            "flip_w": flip_weights,
-            "flip_x": flip_tokens,
+            "flip": flip,
+            "flip_pair": flip_pair,
             "project": project,
             "scores": scores,
-            "lay_w": regroup_weights,
-            "lay_x": regroup_tokens,
+            "lay": lay,
+            "lay_pair": lay_pair,
             "lay_h": regroup_heads,
             "turn": turn_blocks,
-            "quant_w": quantise_weights,
-            "quant_x": quantise_tokens,
+            "quant": quant,
+            "quant_pass": quant_pass,
             "quant_k": quantise_keys,
             "quant_q": quantise_queries,
             "top": row_top,
             "exp": exp_sum,
             "beta": beta_columns,
         }
+        widths = {"flip": 3, "flip_pair": 3, "project": 5, "scores": 3}
 
-        def bare(step):
-            return step[: {"flip_w": 3, "flip_x": 5, "project": 4, "scores": 3}[step[0]]]
+        def results(step):
+            if step[0] == "project":
+                b, w, j, ts = step[1:5]
+                return [("project", b, w, j, t) for t in ts]
+            return [step[: widths.get(step[0], len(step))]]
 
-        def bank_tiles(b):
-            return 1 if b == 0 else 2
+        def content(step):
+            return ("stage_1",) + step[1:4] if step[0] == "project" else step[:3]
 
-        def quant_tiles(b):
-            return NT if b >= TURNED else bank_tiles(b)
+        def last_reader(name):
+            return {"stage_1": "lay_h", "scores": "exp", "flip": "lay", "flip_pair": "lay_pair"}[name[0]], name[1:]
 
         def needs(step):
             kind = step[0]
-            if kind in ("lay_w", "lay_x"):
+            if kind in ("lay", "lay_pair"):
                 return [("flip" + kind[3:],) + step[1:]]
-            if kind == "quant_w":
-                return [("lay_w",) + step[1:]]
-            if kind == "quant_x":
-                b, g, j, n = step[1:]
-                if g == 1 and b >= TURNED:
-                    return [("turn", b)]
-                return [("lay_x", b, g, r, bank_tiles(b)) for r in range(j, j + n, bank_tiles(b))]
+            if kind == "quant":
+                return [("lay",) + step[1:]]
+            if kind == "quant_pass":
+                b, g = step[1:]
+                return [("turn", b)] if g == 1 else [("lay_pair", b, j) for j in (0, 2)]
             if kind == "project":
-                b, w, j = step[1:]
-                n = quant_tiles(b)
-                return [("quant_w", w, t) for t in tiles] + [("quant_x", b, g, j // n * n, n) for g in range(PASSES)]
+                b, w, j, ts = step[1:5]
+                tokens = [("quant", b, j)] if b < TURNED else [("quant_pass", b, g) for g in range(PASSES)]
+                return tokens + [("quant", w, t) for t in ts]
             if kind == "lay_h":
-                return [("project",) + step[1:]]
+                return [("project",) + step[1:] + (t,) for t in tiles]
             if kind == "quant_k":
-                return [("lay_h", step[1], "k", j) for j in range(NT)]
+                return [("lay_h", step[1], "k", j) for j in tiles]
             if kind == "quant_q":
                 return [("lay_h", step[1], "q", step[2])]
             if kind == "scores":
-                return [("quant_k", step[1]), ("quant_q",) + step[1:]]
+                return [("quant_k", step[1]), ("quant_q",) + step[1:3]]
             if kind == "top":
                 return [("scores",) + step[1:], ("beta",)]
             if kind == "exp":
                 return [("top",) + step[1:]]
             return []
 
-        def last_reader(step):
-            if step[0] == "project":
-                return ("lay_h",) + step[1:]
-            if step[0] == "scores":
-                return ("exp",) + step[1:]
-            return ("lay" + step[0][4:],) + step[1:]
-
         def weave(steps):
             done = set()
-            filled = []
+            free = list(range(BANKS))
+            held = {}
+            filled = set()
             at = {engine: 0 for engine in steps}
             for turn in range(sum(len(steps[engine]) for engine in steps)):
                 for engine in steps:
                     if at[engine] == len(steps[engine]):
                         continue
                     step = steps[engine][at[engine]]
-                    name = bare(step) if engine == TENSOR else step
-                    wanted = needs(name)
-                    if engine == TENSOR and len(filled) >= BANKS:
-                        wanted = wanted + [last_reader(filled[len(filled) - BANKS])]
-                    if not all(n in done for n in wanted):
+                    if not all(n in done for n in needs(step)):
                         continue
-                    if step[0][:3] == "lay":
+                    if engine == TENSOR:
+                        bank = None
+                        name = content(step)
+                        if name not in filled:
+                            if not free:
+                                continue
+                            bank = free[0]
+                            free.remove(bank)
+                            filled.add(name)
+                            held[last_reader(name)] = bank
+                        n = widths[step[0]]
+                        run[step[0]](*step[1:n], bank, *step[n:])
+                    elif step[0][:3] == "lay":
                         run[step[0]](*step[1:], engine)
                     else:
                         run[step[0]](*step[1:])
-                    if engine == TENSOR:
-                        filled.append(name)
-                    done.add(name)
+                    for result in results(step):
+                        done.add(result)
+                    reader = (step[0], step[1:])
+                    if reader in held:
+                        free.append(held[reader])
                     at[engine] += 1
             assert all(at[engine] == len(steps[engine]) for engine in steps)
 
@@ -416,46 +421,75 @@ def tile_multiheadenergyattention_pa_t_kernel(tc, x, wk, wq, betas, out):
         ve = []
         se = []
 
-        pe += [("flip_w", "k", 0) + (BANK,) * WARM_UP] + [("flip_w", "k", t, IDLE) for t in (1, 2, 3)]
-        for j in tiles:
-            pe += [("flip_x", 0, 0, j, 1, IDLE), ("flip_x", 0, 1, j, 1)]
-        pe += [("project", 0, "k", 0, BRIDGE)] + [("project", 0, "k", j) for j in (1, 2, 3)]
-        pe += [("flip_w", "q", 0, BRIDGE)] + [("flip_w", "q", t) for t in (1, 2, 3)]
-        pe += [("flip_x", 1, g, j, 2) for j in (0, 2) for g in range(PASSES)]
-        pe += [("project", 0, "q", 0, BRIDGE)] + [("project", 0, "q", j) for j in (1, 2, 3)]
-        se += [("lay_w", "k", t) for t in (0, 2, 3)] + [("lay_x", 0, g, j, 1) for j in tiles for g in range(PASSES)]
-        ve += [("lay_w", "k", 1)] + [("quant_w", "k", t) for t in tiles]
-        ve += [("quant_x", 0, g, j, 1) for j in tiles for g in range(PASSES)]
-        se += [("lay_h", 0, "k", j) for j in tiles] + [("lay_w", "q", 1), ("lay_w", "q", 3)]
-        ve += [("lay_w", "q", 0), ("lay_w", "q", 2)] + [("quant_w", "q", t) for t in tiles]
-        se += [("lay_x", 1, 0, 0, 2), ("lay_x", 1, 1, 0, 2), ("lay_x", 1, 1, 2, 2)] + [("lay_h", 0, "q", j) for j in tiles]
-        ve += [("lay_x", 1, 0, 2, 2)]
-        ve += [("quant_x", 1, g, j, 2) for j in (0, 2) for g in range(PASSES)] + [("beta",)]
+        everything = tuple(tiles)
+        for n, tile in enumerate(early[:HEAD]):
+            idle = (BANK,) * WARM_UP if n == 0 else ((IDLE,) if n < 5 else ())
+            pe += [("flip",) + tile + idle]
+            if n % 2 == 1:
+                for m in (n - 1 - LAG, n - LAG):
+                    landed = early[: max(m + 1, 0)]
+                    if not landed:
+                        continue
+                    s, i = landed[-1]
+                    if s == "k":
+                        pe += [("project", 0, "k", j, (i,)) for b, j in landed if b == 0]
+                    if s == 0:
+                        pe += [("project", 0, "k", i, tuple(t for w, t in landed if w == "k"))]
+            if n % 3 == 1:
+                ve += [("lay",) + tile]
+            else:
+                se += [("lay",) + tile]
+            if n > 0:
+                ve += [("quant",) + early[n - 1]]
+            if n == 12:
+                se += [("lay_h", 0, "k", 0)]
+                ve += [("lay_h", 0, "k", 1)]
+            if n == 14:
+                se += [("lay_h", 0, "k", 2)]
+                ve += [("lay_h", 0, "k", 3)]
+        ve += [("quant",) + early[HEAD - 1], ("beta",)]
+        pe += [("project", 0, "q", j, everything) for j in (0, 1, 2, 3)]
+        ve += [("quant_k", 0)]
+        se += [("lay_h", 0, "q", j) for j in tiles]
+        se += [("lay", 2, 0), ("lay", 2, 2)]
 
         for i in range(1, NB - 1):
-            pe += [("flip_x", i + 1, 0, 0, 2, BRIDGE), ("flip_x", i + 1, 0, 2, 2)]
-            pe += [("project", i, "k", 0, BRIDGE), ("project", i, "k", 1), ("project", i, "k", 2)]
-            pe += [("scores", i - 1, 0), ("project", i, "k", 3), ("scores", i - 1, 1), ("project", i, "q", 0)]
-            pe += [("scores", i - 1, 2), ("project", i, "q", 1), ("scores", i - 1, 3)]
-            pe += [("project", i, "q", 2), ("project", i, "q", 3)]
+            if i + 1 < TURNED:
+                pe += [("flip", i + 1, j) for j in tiles]
+            else:
+                pe += [("flip_pair", i + 1, 0, BRIDGE), ("flip_pair", i + 1, 2)]
+            if i > 0:
+                pe += [("project", i, "k", 0, everything, BRIDGE), ("project", i, "k", 1, everything)]
+                pe += [("project", i, "k", 2, everything), ("scores", i - 1, 0), ("project", i, "k", 3, everything)]
+            else:
+                pe += [("scores", i - 1, 0)]
+            pe += [("scores", i - 1, 1), ("project", i, "q", 0, everything)]
+            pe += [("scores", i - 1, 2), ("project", i, "q", 1, everything), ("scores", i - 1, 3)]
+            pe += [("project", i, "q", 2, everything), ("project", i, "q", 3, everything)]
         for i in range(NB - 2):
-            ve += [("quant_k", i), ("quant_q", i, 0), ("quant_q", i, 1), ("lay_x", i + 2, 0, 0, 2)]
-            ve += [("lay_x", i + 2, 0, 2, 2)] if i + 2 in BOTH else []
-            ve += [("turn", i + 2)]
-            ve += [("quant_q", i, 2), ("quant_q", i, 3), ("top", i, 0), ("quant_x", i + 2, 0, 0, NT)]
-            ve += [("top", i, 1), ("top", i, 2), ("quant_x", i + 2, 1, 0, NT), ("top", i, 3)]
-        se += [("lay_x", 2, 0, 2, 2)]
+            more = i + 2 >= TURNED
+            ve += [("quant_k", i)] if i > 0 else []
+            ve += [("quant_q", i, 0), ("quant_q", i, 1)]
+            ve += [("lay_pair", i + 2, 0)] if more else [("lay", i + 2, 1), ("lay", i + 2, 3)]
+            ve += [("lay_pair", i + 2, 2)] if i + 2 in BOTH else []
+            ve += [("turn", i + 2)] if more else []
+            ve += [("quant_q", i, 2), ("quant_q", i, 3), ("top", i, 0)]
+            ve += [("quant_pass", i + 2, 0)] if more else [("quant", i + 2, 0), ("quant", i + 2, 1)]
+            ve += [("top", i, 1), ("top", i, 2)]
+            ve += [("quant_pass", i + 2, 1)] if more else [("quant", i + 2, 2), ("quant", i + 2, 3)]
+            ve += [("top", i, 3)]
         for i in range(1, NB - 2):
             se += [("lay_h", i, "k", j) for j in tiles]
             for j in tiles:
                 se += [("exp", i - 1, j), ("lay_h", i, "q", j)]
-            se += [] if i + 2 in BOTH else [("lay_x", i + 2, 0, 2, 2)]
+            se += [] if i + 2 in BOTH else [("lay_pair", i + 2, 2)]
 
         i = NB - 1
         p = NB - 2
-        pe += [("project", i, "k", 0), ("project", i, "k", 1), ("scores", p, 0), ("project", i, "k", 2)]
-        pe += [("scores", p, 1), ("project", i, "k", 3), ("scores", p, 2), ("project", i, "q", 0), ("scores", p, 3)]
-        pe += [("project", i, "q", j) for j in (1, 2, 3)] + [("scores", i, j) for j in tiles]
+        pe += [("project", i, "k", 0, everything), ("project", i, "k", 1, everything), ("scores", p, 0), ("project", i, "k", 2, everything)]
+        pe += [("scores", p, 1), ("project", i, "k", 3, everything), ("scores", p, 2), ("project", i, "q", 0, everything), ("scores", p, 3)]
+        pe += [("project", i, "q", j, everything) for j in (1, 2, 3)]
+        pe += [("scores", i, j) for j in tiles]
         ve += [("quant_k", p), ("quant_q", p, 0), ("lay_h", p, "q", 1)] + [("quant_q", p, j) for j in (1, 2, 3)]
         ve += [("top", p, 0), ("top", p, 1), ("lay_h", i, "k", 3), ("top", p, 2), ("quant_k", i), ("lay_h", i, "q", 1)]
         ve += [("quant_q", i, 0), ("top", p, 3), ("quant_q", i, 1), ("quant_q", i, 2), ("top", i, 0)]

@@ -10,6 +10,7 @@ U8 = mybir.dt.uint8
 FP8X4 = mybir.dt.float8_e4m3fn_x4
 ALU = mybir.AluOpType
 ACT = mybir.ActivationFunctionType
+AXIS = mybir.AxisListType
 
 NB = 8
 N = 512
@@ -26,12 +27,11 @@ GROUPS = 2 * N // BLOCK
 ROW_TILES = NB * NT
 FLOPS = 2 * NB * N * D * 2 * Z + 2 * NB * N * N * Z
 
-TURNED = 3
+TURNED = 2
 MASK_ROOT = 2.0**50
 TENSOR = "tensor"
 VECTOR = "vector"
 SCALAR = "scalar"
-BOTH = (5,)
 HEAD = 16
 LAG = 4
 TURNS = 4
@@ -103,8 +103,9 @@ def tile_multiheadenergyattention_pa_t_kernel(tc, x, wk, wq, betas, out):
                 scales=m_scale[side][:],
                 in_=m_grp[:].rearrange("p n t -> p (n t)"),
             )
+        tops = keep.tile([P, ROW_TILES], F32, name="tops")
         neg_top = keep.tile([P, P], F32, name="neg_top")
-        nc.vector.memset(neg_top[:], 0.0)
+        nc.gpsimd.memset(neg_top[:], 0.0)
         sums = keep.tile([P, P], F32, name="sums")
         nc.vector.memset(sums[:], 1.0)
         unread_v = []
@@ -283,6 +284,12 @@ def tile_multiheadenergyattention_pa_t_kernel(tc, x, wk, wq, betas, out):
 
         def row_top(b, j):
             c = b * NT + j
+            if b < NB - 2:
+                nc.vector.tensor_reduce(out=tops[:, c : c + 1], in_=banks[("scores", b, j)][:], axis=AXIS.X, op=ALU.max)
+                nc.gpsimd.tensor_scalar(
+                    out=neg_top[:, c : c + 1], in0=tops[:, c : c + 1], scalar1=neg_beta[:, 0:1], scalar2=None, op0=ALU.mult
+                )
+                return
             nc.vector.tensor_scalar(
                 out=unread_v[c % TURNS][:],
                 in0=banks[("scores", b, j)][:],
@@ -451,38 +458,25 @@ def tile_multiheadenergyattention_pa_t_kernel(tc, x, wk, wq, betas, out):
         pe += [("project", 0, "q", j, everything) for j in (0, 1, 2, 3)]
         ve += [("quant_k", 0)]
         se += [("lay_h", 0, "q", j) for j in tiles]
-        se += [("lay", 2, 0), ("lay", 2, 2)]
+        se += [("lay_pair", 2, 2)]
 
         for i in range(1, NB - 1):
-            if i + 1 < TURNED:
-                pe += [("flip", i + 1, j) for j in tiles]
-            else:
-                pe += [("flip_pair", i + 1, 0, BRIDGE), ("flip_pair", i + 1, 2)]
-            if i > 0:
-                pe += [("project", i, "k", 0, everything, BRIDGE), ("project", i, "k", 1, everything)]
-                pe += [("project", i, "k", 2, everything), ("scores", i - 1, 0), ("project", i, "k", 3, everything)]
-            else:
-                pe += [("scores", i - 1, 0)]
-            pe += [("scores", i - 1, 1), ("project", i, "q", 0, everything)]
-            pe += [("scores", i - 1, 2), ("project", i, "q", 1, everything), ("scores", i - 1, 3)]
-            pe += [("project", i, "q", 2, everything), ("project", i, "q", 3, everything)]
+            pe += [("flip_pair", i + 1, 0, BRIDGE), ("flip_pair", i + 1, 2)]
+            pe += [("project", i, "k", 0, everything), ("project", i, "k", 1, everything), ("scores", i - 1, 0)]
+            pe += [("project", i, "k", 2, everything), ("scores", i - 1, 1), ("project", i, "k", 3, everything)]
+            pe += [("project", i, "q", 0, everything), ("scores", i - 1, 2), ("project", i, "q", 1, everything)]
+            pe += [("scores", i - 1, 3), ("project", i, "q", 2, everything), ("project", i, "q", 3, everything)]
         for i in range(NB - 2):
-            more = i + 2 >= TURNED
             ve += [("quant_k", i)] if i > 0 else []
-            ve += [("quant_q", i, 0), ("quant_q", i, 1)]
-            ve += [("lay_pair", i + 2, 0)] if more else [("lay", i + 2, 1), ("lay", i + 2, 3)]
-            ve += [("lay_pair", i + 2, 2)] if i + 2 in BOTH else []
-            ve += [("turn", i + 2)] if more else []
-            ve += [("quant_q", i, 2), ("quant_q", i, 3), ("top", i, 0)]
-            ve += [("quant_pass", i + 2, 0)] if more else [("quant", i + 2, 0), ("quant", i + 2, 1)]
-            ve += [("top", i, 1), ("top", i, 2)]
-            ve += [("quant_pass", i + 2, 1)] if more else [("quant", i + 2, 2), ("quant", i + 2, 3)]
-            ve += [("top", i, 3)]
+            ve += [("quant_q", i, 0), ("quant_q", i, 1), ("lay_pair", i + 2, 0)]
+            ve += [("lay_pair", i + 2, 2), ("turn", i + 2)] if i > 0 else []
+            ve += [("quant_q", i, 2), ("quant_q", i, 3), ("top", i, 0), ("quant_pass", i + 2, 0), ("top", i, 1)]
+            ve += [("turn", i + 2)] if i == 0 else []
+            ve += [("top", i, 2), ("quant_pass", i + 2, 1), ("top", i, 3)]
         for i in range(1, NB - 2):
-            se += [("lay_h", i, "k", j) for j in tiles]
-            for j in tiles:
-                se += [("exp", i - 1, j), ("lay_h", i, "q", j)]
-            se += [] if i + 2 in BOTH else [("lay_pair", i + 2, 2)]
+            se += [("lay_h", i, "k", j) for j in tiles] + [("lay_h", i, "q", 0), ("exp", i - 1, 0)]
+            se += [("lay_h", i, "q", 1), ("exp", i - 1, 1), ("exp", i - 1, 2), ("lay_h", i, "q", 2)]
+            se += [("lay_h", i, "q", 3), ("exp", i - 1, 3)]
 
         i = NB - 1
         p = NB - 2

@@ -35,6 +35,7 @@ SCALAR = "scalar"
 HEAD = 16
 LAG = 4
 TURNS = 4
+SHARED = (3, 6,)
 WARM_UP = 4
 IDLE = 320
 BRIDGE = 32
@@ -252,8 +253,8 @@ def tile_multiheadenergyattention_pa_t_kernel(tc, x, wk, wq, betas, out):
                 in_=h_grp[(b, "k")][:].rearrange("p n t -> p (n t)"),
             )
 
-        def quantise_queries(b, j):
-            cols = slice(j * P, (j + 1) * P)
+        def quantise_queries(b, j, n):
+            cols = slice(j * P, (j + n) * P)
             nc.vector.quantize_mx(
                 out=h_code[(b, "q")][:, cols].bitcast(FP8X4),
                 scales=h_scale[(b, "q")][:, cols],
@@ -360,6 +361,9 @@ def tile_multiheadenergyattention_pa_t_kernel(tc, x, wk, wq, betas, out):
         def last_reader(name):
             return {"stage_1": "lay_h", "scores": "exp", "flip": "lay", "flip_pair": "lay_pair"}[name[0]], name[1:]
 
+        def query_tiles(b):
+            return 2 if b < NB - 2 else 1
+
         def needs(step):
             kind = step[0]
             if kind in ("lay", "lay_pair"):
@@ -378,9 +382,10 @@ def tile_multiheadenergyattention_pa_t_kernel(tc, x, wk, wq, betas, out):
             if kind == "quant_k":
                 return [("lay_h", step[1], "k", j) for j in tiles]
             if kind == "quant_q":
-                return [("lay_h", step[1], "q", step[2])]
+                return [("lay_h", step[1], "q", step[2] + r) for r in range(step[3])]
             if kind == "scores":
-                return [("quant_k", step[1]), ("quant_q",) + step[1:3]]
+                n = query_tiles(step[1])
+                return [("quant_k", step[1]), ("quant_q", step[1], step[2] // n * n, n)]
             if kind == "top":
                 return [("scores",) + step[1:], ("beta",)]
             if kind == "exp":
@@ -468,15 +473,16 @@ def tile_multiheadenergyattention_pa_t_kernel(tc, x, wk, wq, betas, out):
             pe += [("scores", i - 1, 3), ("project", i, "q", 2, everything), ("project", i, "q", 3, everything)]
         for i in range(NB - 2):
             ve += [("quant_k", i)] if i > 0 else []
-            ve += [("quant_q", i, 0), ("quant_q", i, 1), ("lay_pair", i + 2, 0)]
-            ve += [("lay_pair", i + 2, 2), ("turn", i + 2)] if i > 0 else []
-            ve += [("quant_q", i, 2), ("quant_q", i, 3), ("top", i, 0), ("quant_pass", i + 2, 0), ("top", i, 1)]
+            ve += [("quant_q", i, 0, 2), ("lay_pair", i + 2, 0)]
+            ve += [("lay_pair", i + 2, 2)] if i > 0 and i + 2 not in SHARED else []
+            ve += [("turn", i + 2)] if i > 0 else []
+            ve += [("quant_q", i, 2, 2), ("top", i, 0), ("quant_pass", i + 2, 0), ("top", i, 1)]
             ve += [("turn", i + 2)] if i == 0 else []
             ve += [("top", i, 2), ("quant_pass", i + 2, 1), ("top", i, 3)]
         for i in range(1, NB - 2):
             se += [("lay_h", i, "k", j) for j in tiles] + [("lay_h", i, "q", 0), ("exp", i - 1, 0)]
             se += [("lay_h", i, "q", 1), ("exp", i - 1, 1), ("exp", i - 1, 2), ("lay_h", i, "q", 2)]
-            se += [("lay_h", i, "q", 3), ("exp", i - 1, 3)]
+            se += [("lay_h", i, "q", 3), ("exp", i - 1, 3)] + ([("lay_pair", i + 2, 2)] if i + 2 in SHARED else [])
 
         i = NB - 1
         p = NB - 2
@@ -484,10 +490,10 @@ def tile_multiheadenergyattention_pa_t_kernel(tc, x, wk, wq, betas, out):
         pe += [("scores", p, 1), ("project", i, "k", 3, everything), ("scores", p, 2), ("project", i, "q", 0, everything), ("scores", p, 3)]
         pe += [("project", i, "q", j, everything) for j in (1, 2, 3)]
         pe += [("scores", i, j) for j in tiles]
-        ve += [("quant_k", p), ("quant_q", p, 0), ("lay_h", p, "q", 1)] + [("quant_q", p, j) for j in (1, 2, 3)]
+        ve += [("quant_k", p), ("quant_q", p, 0, 1), ("lay_h", p, "q", 1)] + [("quant_q", p, j, 1) for j in (1, 2, 3)]
         ve += [("top", p, 0), ("top", p, 1), ("lay_h", i, "k", 3), ("top", p, 2), ("quant_k", i), ("lay_h", i, "q", 1)]
-        ve += [("quant_q", i, 0), ("top", p, 3), ("quant_q", i, 1), ("quant_q", i, 2), ("top", i, 0)]
-        ve += [("quant_q", i, 3), ("top", i, 1), ("top", i, 2), ("top", i, 3)]
+        ve += [("quant_q", i, 0, 1), ("top", p, 3), ("quant_q", i, 1, 1), ("quant_q", i, 2, 1), ("top", i, 0)]
+        ve += [("quant_q", i, 3, 1), ("top", i, 1), ("top", i, 2), ("top", i, 3)]
         se += [("lay_h", p, "k", j) for j in tiles] + [("exp", p - 1, 0), ("lay_h", p, "q", 0), ("exp", p - 1, 1)]
         se += [("lay_h", p, "q", 2), ("exp", p - 1, 2), ("lay_h", p, "q", 3), ("exp", p - 1, 3)]
         se += [("lay_h", i, "k", j) for j in (0, 1, 2)] + [("exp", p, 0), ("exp", p, 1), ("lay_h", i, "q", 0)]

@@ -35,7 +35,8 @@ SCALAR = "scalar"
 HEAD = 16
 LAG = 4
 TURNS = 4
-SHARED = (3, 6,)
+SHARED = (3, 7,)
+FULL = (5,)
 WARM_UP = 4
 IDLE = 320
 BRIDGE = 32
@@ -59,8 +60,12 @@ def tile_multiheadenergyattention_pa_t_kernel(tc, x, wk, wq, betas, out):
         x_raw = {}
         x_blocks = {}
         for b in range(TURNED, NB):
-            x_raw[b] = keep.tile([P, NT, D_PASS], BF16, name="x_raw_%d" % b)
-            x_blocks[b] = keep.tile([P, GROUPS, 2 * BLOCK], BF16, name="x_blocks_%d" % b, align_bytes=64)
+            if b not in FULL:
+                x_raw[b] = keep.tile([P, NT, D_PASS], BF16, name="x_raw_%d" % b)
+            for g in range(PASSES) if b in FULL else (1,):
+                x_blocks[(b, g)] = keep.tile(
+                    [P, GROUPS, 2 * BLOCK], BF16, name="x_blocks_%d_%d" % (b, g), align_bytes=64
+                )
 
         def load_tile(tile):
             s, i = tile
@@ -70,12 +75,12 @@ def tile_multiheadenergyattention_pa_t_kernel(tc, x, wk, wq, betas, out):
                 source = x[s, i * P : (i + 1) * P, :]
             nc.sync.dma_start(out=raw[tile][:], in_=source)
 
-        def load_blocks(b):
+        def load_blocks(b, g):
             for u in range(2):
                 for q in (0, 2, 1, 3):
-                    first = D_PASS + 256 * u + 2 * BLOCK * q
+                    first = g * D_PASS + 256 * u + 2 * BLOCK * q
                     nc.sync.dma_start(
-                        out=x_blocks[b][BLOCK * q + u : BLOCK * (q + 1) : 2, :, :],
+                        out=x_blocks[(b, g)][BLOCK * q + u : BLOCK * (q + 1) : 2, :, :],
                         in_=x[b, :, first : first + 2 * BLOCK].rearrange("(c n) f -> n c f", c=GROUPS),
                     )
 
@@ -84,8 +89,11 @@ def tile_multiheadenergyattention_pa_t_kernel(tc, x, wk, wq, betas, out):
         beta_bf = keep.tile([P, 1], BF16, name="beta_bf")
         nc.sync.dma_start(out=beta_bf[:], in_=betas.partition_broadcast(P))
         for b in range(TURNED, NB):
-            nc.sync.dma_start(out=x_raw[b][:], in_=x[b, :, 0:D_PASS].rearrange("(j p) d -> p j d", p=P))
-            load_blocks(b)
+            if b in FULL:
+                load_blocks(b, 0)
+            else:
+                nc.sync.dma_start(out=x_raw[b][:], in_=x[b, :, 0:D_PASS].rearrange("(j p) d -> p j d", p=P))
+            load_blocks(b, 1)
 
         zeros = keep.tile([P, BANK], BF16, name="zeros")
         nc.vector.memset(zeros[:], 0.0)
@@ -207,10 +215,11 @@ def tile_multiheadenergyattention_pa_t_kernel(tc, x, wk, wq, betas, out):
                 banks[("flip_pair", b, j)][:].rearrange("p (j u r) -> p j r u", j=2, u=2),
             )
 
-        def turn_blocks(b):
+        def turn_blocks(b, g):
             new_tokens(b)
             nc.vector.transpose(
-                out=grp[b][:, 4 * N :].bitcast(F32), in_=x_blocks[b][:].rearrange("p c f -> p (c f)").bitcast(F32)
+                out=grp[b][:, 4 * g * N : 4 * (g + 1) * N].bitcast(F32),
+                in_=x_blocks[(b, g)][:].rearrange("p c f -> p (c f)").bitcast(F32)
             )
 
         def quant_pass(b, g):
@@ -372,7 +381,9 @@ def tile_multiheadenergyattention_pa_t_kernel(tc, x, wk, wq, betas, out):
                 return [("lay",) + step[1:]]
             if kind == "quant_pass":
                 b, g = step[1:]
-                return [("turn", b)] if g == 1 else [("lay_pair", b, j) for j in (0, 2)]
+                if g == 1 or b in FULL:
+                    return [("turn", b, g)]
+                return [("lay_pair", b, j) for j in (0, 2)]
             if kind == "project":
                 b, w, j, ts = step[1:5]
                 tokens = [("quant", b, j)] if b < TURNED else [("quant_pass", b, g) for g in range(PASSES)]
@@ -466,18 +477,18 @@ def tile_multiheadenergyattention_pa_t_kernel(tc, x, wk, wq, betas, out):
         se += [("lay_pair", 2, 2)]
 
         for i in range(1, NB - 1):
-            pe += [("flip_pair", i + 1, 0, BRIDGE), ("flip_pair", i + 1, 2)]
+            pe += [("flip_pair", i + 1, 0, BRIDGE), ("flip_pair", i + 1, 2)] if i + 1 not in FULL else []
             pe += [("project", i, "k", 0, everything), ("project", i, "k", 1, everything), ("scores", i - 1, 0)]
             pe += [("project", i, "k", 2, everything), ("scores", i - 1, 1), ("project", i, "k", 3, everything)]
             pe += [("project", i, "q", 0, everything), ("scores", i - 1, 2), ("project", i, "q", 1, everything)]
             pe += [("scores", i - 1, 3), ("project", i, "q", 2, everything), ("project", i, "q", 3, everything)]
         for i in range(NB - 2):
             ve += [("quant_k", i)] if i > 0 else []
-            ve += [("quant_q", i, 0, 2), ("lay_pair", i + 2, 0)]
-            ve += [("lay_pair", i + 2, 2)] if i > 0 and i + 2 not in SHARED else []
-            ve += [("turn", i + 2)] if i > 0 else []
+            ve += [("quant_q", i, 0, 2), ("turn", i + 2, 0) if i + 2 in FULL else ("lay_pair", i + 2, 0)]
+            ve += [("lay_pair", i + 2, 2)] if i > 0 and i + 2 not in FULL + SHARED else []
+            ve += [("turn", i + 2, 1)] if i > 0 else []
             ve += [("quant_q", i, 2, 2), ("top", i, 0), ("quant_pass", i + 2, 0), ("top", i, 1)]
-            ve += [("turn", i + 2)] if i == 0 else []
+            ve += [("turn", i + 2, 1)] if i == 0 else []
             ve += [("top", i, 2), ("quant_pass", i + 2, 1), ("top", i, 3)]
         for i in range(1, NB - 2):
             se += [("lay_h", i, "k", j) for j in tiles] + [("lay_h", i, "q", 0), ("exp", i - 1, 0)]

@@ -35,8 +35,9 @@ SCALAR = "scalar"
 HEAD = 16
 LAG = 4
 TURNS = 4
-SHARED = (3, 7,)
-FULL = (5,)
+SHARED = (3, 6)
+ALONE = ()
+FULL = (4, 7,)
 WARM_UP = 4
 IDLE = 320
 BRIDGE = 32
@@ -484,8 +485,8 @@ def tile_multiheadenergyattention_pa_t_kernel(tc, x, wk, wq, betas, out):
             pe += [("scores", i - 1, 3), ("project", i, "q", 2, everything), ("project", i, "q", 3, everything)]
         for i in range(NB - 2):
             ve += [("quant_k", i)] if i > 0 else []
-            ve += [("quant_q", i, 0, 2), ("turn", i + 2, 0) if i + 2 in FULL else ("lay_pair", i + 2, 0)]
-            ve += [("lay_pair", i + 2, 2)] if i > 0 and i + 2 not in FULL + SHARED else []
+            ve += [("quant_q", i, 0, 2), ("turn", i + 2, 0) if i + 2 in FULL else ("lay_pair", i + 2, 0)] if i + 2 not in ALONE else [("quant_q", i, 0, 2)]
+            ve += [("lay_pair", i + 2, 2)] if i > 0 and i + 2 not in FULL + SHARED + ALONE else []
             ve += [("turn", i + 2, 1)] if i > 0 else []
             ve += [("quant_q", i, 2, 2), ("top", i, 0), ("quant_pass", i + 2, 0), ("top", i, 1)]
             ve += [("turn", i + 2, 1)] if i == 0 else []
@@ -493,7 +494,8 @@ def tile_multiheadenergyattention_pa_t_kernel(tc, x, wk, wq, betas, out):
         for i in range(1, NB - 2):
             se += [("lay_h", i, "k", j) for j in tiles] + [("lay_h", i, "q", 0), ("exp", i - 1, 0)]
             se += [("lay_h", i, "q", 1), ("exp", i - 1, 1), ("exp", i - 1, 2), ("lay_h", i, "q", 2)]
-            se += [("lay_h", i, "q", 3), ("exp", i - 1, 3)] + ([("lay_pair", i + 2, 2)] if i + 2 in SHARED else [])
+            se += [("lay_h", i, "q", 3), ("exp", i - 1, 3)] + ([("lay_pair", i + 2, 0)] if i + 2 in ALONE else [])
+            se += [("lay_pair", i + 2, 2)] if i + 2 in SHARED + ALONE else []
 
         i = NB - 1
         p = NB - 2

@@ -500,18 +500,22 @@ def tile_multiheadenergyattention_pa_t_kernel(tc, x, wk, wq, betas, out):
         i = NB - 1
         p = NB - 2
         pe += [("project", i, "k", 0, everything), ("project", i, "k", 1, everything), ("scores", p, 0), ("project", i, "k", 2, everything)]
-        pe += [("scores", p, 1), ("project", i, "k", 3, everything), ("scores", p, 2), ("project", i, "q", 0, everything), ("scores", p, 3)]
-        pe += [("project", i, "q", j, everything) for j in (1, 2, 3)]
-        pe += [("scores", i, j) for j in tiles]
-        ve += [("quant_k", p), ("quant_q", p, 0, 1), ("lay_h", p, "q", 1)] + [("quant_q", p, j, 1) for j in (1, 2, 3)]
-        ve += [("top", p, 0), ("top", p, 1), ("lay_h", i, "k", 3), ("top", p, 2), ("quant_k", i), ("lay_h", i, "q", 1)]
-        ve += [("quant_q", i, 0, 1), ("top", p, 3), ("quant_q", i, 1, 1), ("quant_q", i, 2, 1), ("top", i, 0)]
-        ve += [("quant_q", i, 3, 1), ("top", i, 1), ("top", i, 2), ("top", i, 3)]
-        se += [("lay_h", p, "k", j) for j in tiles] + [("exp", p - 1, 0), ("lay_h", p, "q", 0), ("exp", p - 1, 1)]
-        se += [("lay_h", p, "q", 2), ("exp", p - 1, 2), ("lay_h", p, "q", 3), ("exp", p - 1, 3)]
-        se += [("lay_h", i, "k", j) for j in (0, 1, 2)] + [("exp", p, 0), ("exp", p, 1), ("lay_h", i, "q", 0)]
-        se += [("exp", p, 2), ("lay_h", i, "q", 2), ("lay_h", i, "q", 3), ("exp", p, 3)]
-        se += [("exp", i, j) for j in tiles]
+        pe += [("scores", p, 1), ("project", i, "k", 3, everything), ("scores", p, 2), ("project", i, "q", 0, everything)]
+        pe += [("scores", p, 3), ("project", i, "q", 1, everything), ("project", i, "q", 2, everything), ("project", i, "q", 3, everything)]
+        pe += [("scores", i, 0), ("scores", i, 1), ("scores", i, 2), ("scores", i, 3)]
+        ve += [("quant_k", p), ("quant_q", p, 0, 1), ("lay_h", p, "q", 1), ("quant_q", p, 1, 1)]
+        ve += [("quant_q", p, 2, 1), ("quant_q", p, 3, 1), ("top", p, 0), ("top", p, 1)]
+        ve += [("lay_h", i, "k", 3), ("top", p, 2), ("quant_k", i), ("lay_h", i, "q", 1)]
+        ve += [("quant_q", i, 0, 1), ("quant_q", i, 1, 1), ("top", p, 3), ("quant_q", i, 2, 1)]
+        ve += [("top", i, 0), ("quant_q", i, 3, 1), ("top", i, 1), ("top", i, 2)]
+        ve += [("top", i, 3)]
+        se += [("lay_h", p, "k", 0), ("lay_h", p, "k", 1), ("lay_h", p, "k", 2), ("lay_h", p, "k", 3)]
+        se += [("exp", p - 1, 0), ("lay_h", p, "q", 0), ("exp", p - 1, 1), ("lay_h", p, "q", 2)]
+        se += [("exp", p - 1, 2), ("lay_h", p, "q", 3), ("exp", p - 1, 3), ("lay_h", i, "k", 0)]
+        se += [("lay_h", i, "k", 1), ("lay_h", i, "k", 2), ("exp", p, 0), ("lay_h", i, "q", 0)]
+        se += [("exp", p, 1), ("lay_h", i, "q", 2), ("lay_h", i, "q", 3), ("exp", p, 2)]
+        se += [("exp", p, 3), ("exp", i, 0), ("exp", i, 1), ("exp", i, 2)]
+        se += [("exp", i, 3)]
 
         weave({TENSOR: pe, VECTOR: ve, SCALAR: se})
         finish()

@@ -37,7 +37,7 @@ LAG = 4
 TURNS = 4
 SHARED = (3, 6)
 ALONE = ()
-FULL = (4, 7,)
+FULL = (5, 7,)
 WARM_UP = 4
 IDLE = 320
 BRIDGE = 32

from contextlib import ExitStack

import concourse.mybir as mybir
from concourse.masks import make_identity

F32 = mybir.dt.float32
BF16 = mybir.dt.bfloat16
U32 = mybir.dt.uint32
U8 = mybir.dt.uint8
FP8X4 = mybir.dt.float8_e4m3fn_x4
ALU = mybir.AluOpType
ACT = mybir.ActivationFunctionType
AXIS = mybir.AxisListType

NB = 8
N = 512
D = 1024
Z = 512
P = 128
NT = N // P
PASSES = 2
D_PASS = D // PASSES
BANK = 512
BANKS = 8
BLOCK = 32
GROUPS = 2 * N // BLOCK
ROW_TILES = NB * NT
FLOPS = 2 * NB * N * D * 2 * Z + 2 * NB * N * N * Z

TURNED = 2
MASK_ROOT = 2.0**50
TENSOR = "tensor"
VECTOR = "vector"
SCALAR = "scalar"
HEAD = 16
LAG = 4
TURNS = 4
SHARED = (3, 6)
ALONE = ()
FULL = (5, 7,)
WARM_UP = 4
IDLE = 320
BRIDGE = 32


def tile_multiheadenergyattention_pa_t_kernel(tc, x, wk, wq, betas, out):
    nc = tc.nc
    with ExitStack() as ctx:
        keep = ctx.enter_context(tc.tile_pool(name="keep", bufs=1))
        pairs = ctx.enter_context(tc.tile_pool(name="pairs", bufs=2))
        triples = ctx.enter_context(tc.tile_pool(name="triples", bufs=3))
        psum = ctx.enter_context(tc.psum_pool(name="psum", bufs=1))
        ctx.enter_context(tc.manual_schedule())

        w_dram = {"k": wk, "q": wq}
        early = [("k", 0), (0, 0), (0, 1), ("k", 1), (0, 2), ("k", 2), (0, 3), ("k", 3)]
        early += [("q", t) for t in range(NT)] + [(b, j) for b in range(1, TURNED) for j in range(NT)]
        raw = {}
        for tile in early:
            raw[tile] = keep.tile([P, D], BF16, name="raw_%s_%d" % tile)
        x_raw = {}
        x_blocks = {}
        for b in range(TURNED, NB):
            if b not in FULL:
                x_raw[b] = keep.tile([P, NT, D_PASS], BF16, name="x_raw_%d" % b)
            for g in range(PASSES) if b in FULL else (1,):
                x_blocks[(b, g)] = keep.tile(
                    [P, GROUPS, 2 * BLOCK], BF16, name="x_blocks_%d_%d" % (b, g), align_bytes=64
                )

        def load_tile(tile):
            s, i = tile
            if s in w_dram:
                source = w_dram[s][0, :, :].rearrange("(p t) d -> p t d", t=NT)[:, i, :]
            else:
                source = x[s, i * P : (i + 1) * P, :]
            nc.sync.dma_start(out=raw[tile][:], in_=source)

        def load_blocks(b, g):
            for u in range(2):
                for q in (0, 2, 1, 3):
                    first = g * D_PASS + 256 * u + 2 * BLOCK * q
                    nc.sync.dma_start(
                        out=x_blocks[(b, g)][BLOCK * q + u : BLOCK * (q + 1) : 2, :, :],
                        in_=x[b, :, first : first + 2 * BLOCK].rearrange("(c n) f -> n c f", c=GROUPS),
                    )

        for tile in early:
            load_tile(tile)
        beta_bf = keep.tile([P, 1], BF16, name="beta_bf")
        nc.sync.dma_start(out=beta_bf[:], in_=betas.partition_broadcast(P))
        for b in range(TURNED, NB):
            if b in FULL:
                load_blocks(b, 0)
            else:
                nc.sync.dma_start(out=x_raw[b][:], in_=x[b, :, 0:D_PASS].rearrange("(j p) d -> p j d", p=P))
            load_blocks(b, 1)

        zeros = keep.tile([P, BANK], BF16, name="zeros")
        nc.vector.memset(zeros[:], 0.0)
        ident = keep.tile([P, P], F32, name="ident")
        make_identity(nc, ident[:])
        m_code = {}
        m_scale = {}
        for side, root in (("q", MASK_ROOT), ("k", -MASK_ROOT)):
            m_grp = keep.tile([P, P, 4], BF16, name="m_grp_" + side, align_bytes=64)
            m_code[side] = keep.tile([P, P], U32, name="m_code_" + side, align_bytes=64)
            m_scale[side] = keep.tile([P, P], U8, name="m_scale_" + side, align_bytes=64)
            nc.gpsimd.memset(m_grp[:], 0.0)
            nc.vector.tensor_scalar(out=m_grp[:, :, 0], in0=ident[:], scalar1=root, scalar2=None, op0=ALU.mult)
            nc.vector.quantize_mx(
                out=m_code[side][:].bitcast(FP8X4),
                scales=m_scale[side][:],
                in_=m_grp[:].rearrange("p n t -> p (n t)"),
            )
        tops = keep.tile([P, ROW_TILES], F32, name="tops")
        neg_top = keep.tile([P, P], F32, name="neg_top")
        nc.gpsimd.memset(neg_top[:], 0.0)
        sums = keep.tile([P, P], F32, name="sums")
        nc.vector.memset(sums[:], 1.0)
        unread_v = []
        unread_s = []
        for r in range(TURNS):
            unread_v.append(keep.tile([P, N], BF16, name="unread_v_%d" % r))
            unread_s.append(keep.tile([P, N], BF16, name="unread_s_%d" % r))
        beta_f = keep.tile([P, 1], F32, name="beta_f")
        neg_beta = keep.tile([P, 1], F32, name="neg_beta")
        inv_beta = keep.tile([P, 1], F32, name="inv_beta")
        neg_inv_beta = keep.tile([P, 1], F32, name="neg_inv_beta")

        def beta_columns():
            nc.vector.tensor_copy(out=beta_f[:], in_=beta_bf[:])
            nc.vector.tensor_scalar(out=neg_beta[:], in0=beta_bf[:], scalar1=-1.0, scalar2=None, op0=ALU.mult)
            nc.vector.reciprocal(out=inv_beta[:], in_=beta_f[:])
            nc.vector.tensor_scalar(out=neg_inv_beta[:], in0=inv_beta[:], scalar1=-1.0, scalar2=None, op0=ALU.mult)

        grp = {}
        code = {}
        scale = {}
        for w in ("k", "q"):
            grp[w] = keep.tile([P, 4 * D], BF16, name="w_grp_" + w, align_bytes=64)
            code[w] = keep.tile([P, D], U32, name="w_code_" + w, align_bytes=64)
            scale[w] = keep.tile([P, D], U8, name="w_scale_" + w, align_bytes=64)
        h_grp = {}
        h_code = {}
        h_scale = {}
        banks = {}

        def new_bank(key, at):
            banks[key] = psum.tile([P, BANK], F32, name="bank_%d" % at, tag="bank_%d" % at)
            return banks[key]

        def new_tokens(b):
            if b not in grp:
                grp[b] = pairs.tile([P, 4 * D], BF16, name="x_grp", tag="x_grp", align_bytes=64)
                code[b] = triples.tile([P, D], U32, name="x_code", tag="x_code", align_bytes=64)
                scale[b] = triples.tile([P, D], U8, name="x_scale", tag="x_scale", align_bytes=64)

        def columns(s, i, g):
            by_tile = s in w_dram or s < TURNED
            at = 2 * i + g if by_tile else NT * g + i
            return slice(at * P, (at + 1) * P)

        def copy_out(engine, dst, src):
            if engine == VECTOR:
                nc.vector.tensor_copy(out=dst, in_=src)
            else:
                nc.scalar.copy(out=dst, in_=src)

        def quantise(s, cols):
            nc.vector.quantize_mx(
                out=code[s][:, cols].bitcast(FP8X4),
                scales=scale[s][:, cols],
                in_=grp[s][:, 4 * cols.start : 4 * cols.stop],
            )

        def idle_matmuls(bank, widths):
            for width in widths:
                nc.tensor.matmul(
                    out=bank[:, 0:width], lhsT=zeros[:, 0:P], rhs=zeros[:, 0:width], start=True, stop=True
                )

        def flip(s, i, at, *idle):
            bank = new_bank(("flip", s, i), at)
            idle_matmuls(bank, idle)
            words = raw[(s, i)][:].bitcast(F32)
            for q in range(4):
                nc.tensor.transpose(bank[:, q * P : (q + 1) * P], words[:, q * P : (q + 1) * P], ident[:])

        def lay(s, i, engine):
            if s not in w_dram:
                new_tokens(s)
            copy_out(
                engine,
                grp[s][:, i * D : (i + 1) * D].bitcast(F32).rearrange("p (g r u) -> p g r u", g=2, u=2),
                banks[("flip", s, i)][:].rearrange("p (g u r) -> p g r u", g=2, u=2),
            )

        def quant(s, i):
            quantise(s, slice(2 * i * P, 2 * (i + 1) * P))

        def flip_pair(b, j, at, *idle):
            bank = new_bank(("flip_pair", b, j), at)
            idle_matmuls(bank, idle)
            for r in range(2):
                words = x_raw[b][:, j + r, :].bitcast(F32)
                for u in range(2):
                    q = 2 * r + u
                    nc.tensor.transpose(bank[:, q * P : (q + 1) * P], words[:, u * P : (u + 1) * P], ident[:])

        def lay_pair(b, j, engine):
            new_tokens(b)
            copy_out(
                engine,
                grp[b][:, 4 * j * P : 4 * (j + 2) * P].bitcast(F32).rearrange("p (j r u) -> p j r u", j=2, u=2),
                banks[("flip_pair", b, j)][:].rearrange("p (j u r) -> p j r u", j=2, u=2),
            )

        def turn_blocks(b, g):
            new_tokens(b)
            nc.vector.transpose(
                out=grp[b][:, 4 * g * N : 4 * (g + 1) * N].bitcast(F32),
                in_=x_blocks[(b, g)][:].rearrange("p c f -> p (c f)").bitcast(F32)
            )

        def quant_pass(b, g):
            quantise(b, slice(g * N, (g + 1) * N))

        def project(b, w, j, ts, at, *idle):
            bank = banks.get(("stage_1", b, w, j))
            if bank is None:
                bank = new_bank(("stage_1", b, w, j), at)
            idle_matmuls(bank, idle)
            for t in ts:
                for g in range(PASSES):
                    rows = columns(w, t, g)
                    tokens = columns(b, j, g)
                    nc.tensor.matmul_mx(
                        out=bank[:, t * P : (t + 1) * P],
                        lhsT=code[w][:, rows].bitcast(FP8X4),
                        lhsT_scale=scale[w][:, rows],
                        rhs=code[b][:, tokens].bitcast(FP8X4),
                        rhs_scale=scale[b][:, tokens],
                        start=(g == 0),
                        stop=(g == PASSES - 1),
                    )

        def regroup_heads(b, w, j, engine):
            if (b, w) not in h_grp:
                h_grp[(b, w)] = pairs.tile([P, N, 4], BF16, name="h_grp_" + w, tag="h_grp_" + w, align_bytes=64)
                h_code[(b, w)] = triples.tile([P, N], U32, name="h_code_" + w, tag="h_code_" + w, align_bytes=64)
                h_scale[(b, w)] = triples.tile([P, N], U8, name="h_scale_" + w, tag="h_scale_" + w, align_bytes=64)
            copy_out(
                engine,
                h_grp[(b, w)][:, j * P : (j + 1) * P, :],
                banks[("stage_1", b, w, j)][:].rearrange("p (t n) -> p n t", t=NT),
            )

        def quantise_keys(b):
            nc.vector.quantize_mx(
                out=h_code[(b, "k")][:].bitcast(FP8X4),
                scales=h_scale[(b, "k")][:],
                in_=h_grp[(b, "k")][:].rearrange("p n t -> p (n t)"),
            )

        def quantise_queries(b, j, n):
            cols = slice(j * P, (j + n) * P)
            nc.vector.quantize_mx(
                out=h_code[(b, "q")][:, cols].bitcast(FP8X4),
                scales=h_scale[(b, "q")][:, cols],
                in_=h_grp[(b, "q")][:, cols, :].rearrange("p n t -> p (n t)"),
            )

        def scores(b, j, at):
            bank = new_bank(("scores", b, j), at)
            own = slice(j * P, (j + 1) * P)
            nc.tensor.matmul_mx(
                out=bank[:],
                lhsT=h_code[(b, "q")][:, own].bitcast(FP8X4),
                lhsT_scale=h_scale[(b, "q")][:, own],
                rhs=h_code[(b, "k")][:].bitcast(FP8X4),
                rhs_scale=h_scale[(b, "k")][:],
                start=True,
                stop=False,
            )
            nc.tensor.matmul_mx(
                out=bank[:, own],
                lhsT=m_code["q"][:].bitcast(FP8X4),
                lhsT_scale=m_scale["q"][:],
                rhs=m_code["k"][:].bitcast(FP8X4),
                rhs_scale=m_scale["k"][:],
                start=False,
                stop=True,
            )

        def row_top(b, j):
            c = b * NT + j
            if b < NB - 2:
                nc.vector.tensor_reduce(out=tops[:, c : c + 1], in_=banks[("scores", b, j)][:], axis=AXIS.X, op=ALU.max)
                nc.gpsimd.tensor_scalar(
                    out=neg_top[:, c : c + 1], in0=tops[:, c : c + 1], scalar1=neg_beta[:, 0:1], scalar2=None, op0=ALU.mult
                )
                return
            nc.vector.tensor_scalar(
                out=unread_v[c % TURNS][:],
                in0=banks[("scores", b, j)][:],
                scalar1=neg_beta[:, 0:1],
                scalar2=None,
                op0=ALU.mult,
                op1=ALU.min,
                accum_out=neg_top[:, c : c + 1],
            )

        def exp_sum(b, j):
            c = b * NT + j
            nc.scalar.activation(
                out=unread_s[c % TURNS][:],
                in_=banks[("scores", b, j)][:],
                func=ACT.Exp,
                bias=neg_top[:, c : c + 1],
                scale=beta_f[:, 0:1],
                accum_out=sums[:, c : c + 1],
            )

        def finish():
            top_bank = new_bank("top", 0)
            nc.tensor.transpose(top_bank[:, 0:P], neg_top[:], ident[:])
            top_t = keep.tile([P, P], F32, name="top_t")
            nc.vector.tensor_scalar(
                out=top_t[:], in0=top_bank[:, 0:P], scalar1=inv_beta[:, 0:1], scalar2=None, op0=ALU.mult
            )
            sum_bank = new_bank("sum", 1)
            nc.tensor.transpose(sum_bank[:, 0:P], sums[:], ident[:])
            log_t = keep.tile([P, P], F32, name="log_t")
            nc.scalar.activation(out=log_t[:], in_=sum_bank[:, 0:P], func=ACT.Ln)
            energy = keep.tile([P, P], F32, name="energy")
            nc.vector.scalar_tensor_tensor(
                out=energy[:], in0=log_t[:], scalar=neg_inv_beta[:, 0:1], in1=top_t[:], op0=ALU.mult, op1=ALU.add
            )
            nc.sync.dma_start(out=out.rearrange("b o (j p) -> (b o j) p", p=P), in_=energy[0:ROW_TILES, :])

        tiles = range(NT)
        run = {
            "flip": flip,
            "flip_pair": flip_pair,
            "project": project,
            "scores": scores,
            "lay": lay,
            "lay_pair": lay_pair,
            "lay_h": regroup_heads,
            "turn": turn_blocks,
            "quant": quant,
            "quant_pass": quant_pass,
            "quant_k": quantise_keys,
            "quant_q": quantise_queries,
            "top": row_top,
            "exp": exp_sum,
            "beta": beta_columns,
        }
        widths = {"flip": 3, "flip_pair": 3, "project": 5, "scores": 3}

        def results(step):
            if step[0] == "project":
                b, w, j, ts = step[1:5]
                return [("project", b, w, j, t) for t in ts]
            return [step[: widths.get(step[0], len(step))]]

        def content(step):
            return ("stage_1",) + step[1:4] if step[0] == "project" else step[:3]

        def last_reader(name):
            return {"stage_1": "lay_h", "scores": "exp", "flip": "lay", "flip_pair": "lay_pair"}[name[0]], name[1:]

        def query_tiles(b):
            return 2 if b < NB - 2 else 1

        def needs(step):
            kind = step[0]
            if kind in ("lay", "lay_pair"):
                return [("flip" + kind[3:],) + step[1:]]
            if kind == "quant":
                return [("lay",) + step[1:]]
            if kind == "quant_pass":
                b, g = step[1:]
                if g == 1 or b in FULL:
                    return [("turn", b, g)]
                return [("lay_pair", b, j) for j in (0, 2)]
            if kind == "project":
                b, w, j, ts = step[1:5]
                tokens = [("quant", b, j)] if b < TURNED else [("quant_pass", b, g) for g in range(PASSES)]
                return tokens + [("quant", w, t) for t in ts]
            if kind == "lay_h":
                return [("project",) + step[1:] + (t,) for t in tiles]
            if kind == "quant_k":
                return [("lay_h", step[1], "k", j) for j in tiles]
            if kind == "quant_q":
                return [("lay_h", step[1], "q", step[2] + r) for r in range(step[3])]
            if kind == "scores":
                n = query_tiles(step[1])
                return [("quant_k", step[1]), ("quant_q", step[1], step[2] // n * n, n)]
            if kind == "top":
                return [("scores",) + step[1:], ("beta",)]
            if kind == "exp":
                return [("top",) + step[1:]]
            return []

        def weave(steps):
            done = set()
            free = list(range(BANKS))
            held = {}
            filled = set()
            at = {engine: 0 for engine in steps}
            for turn in range(sum(len(steps[engine]) for engine in steps)):
                for engine in steps:
                    if at[engine] == len(steps[engine]):
                        continue
                    step = steps[engine][at[engine]]
                    if not all(n in done for n in needs(step)):
                        continue
                    if engine == TENSOR:
                        bank = None
                        name = content(step)
                        if name not in filled:
                            if not free:
                                continue
                            bank = free[0]
                            free.remove(bank)
                            filled.add(name)
                            held[last_reader(name)] = bank
                        n = widths[step[0]]
                        run[step[0]](*step[1:n], bank, *step[n:])
                    elif step[0][:3] == "lay":
                        run[step[0]](*step[1:], engine)
                    else:
                        run[step[0]](*step[1:])
                    for result in results(step):
                        done.add(result)
                    reader = (step[0], step[1:])
                    if reader in held:
                        free.append(held[reader])
                    at[engine] += 1
            assert all(at[engine] == len(steps[engine]) for engine in steps)

        pe = []
        ve = []
        se = []

        everything = tuple(tiles)
        for n, tile in enumerate(early[:HEAD]):
            idle = (BANK,) * WARM_UP if n == 0 else ((IDLE,) if n < 5 else ())
            pe += [("flip",) + tile + idle]
            if n % 2 == 1:
                for m in (n - 1 - LAG, n - LAG):
                    landed = early[: max(m + 1, 0)]
                    if not landed:
                        continue
                    s, i = landed[-1]
                    if s == "k":
                        pe += [("project", 0, "k", j, (i,)) for b, j in landed if b == 0]
                    if s == 0:
                        pe += [("project", 0, "k", i, tuple(t for w, t in landed if w == "k"))]
            if n % 3 == 1:
                ve += [("lay",) + tile]
            else:
                se += [("lay",) + tile]
            if n > 0:
                ve += [("quant",) + early[n - 1]]
            if n == 12:
                se += [("lay_h", 0, "k", 0)]
                ve += [("lay_h", 0, "k", 1)]
            if n == 14:
                se += [("lay_h", 0, "k", 2)]
                ve += [("lay_h", 0, "k", 3)]
        ve += [("quant",) + early[HEAD - 1], ("beta",)]
        pe += [("project", 0, "q", j, everything) for j in (0, 1, 2, 3)]
        ve += [("quant_k", 0)]
        se += [("lay_h", 0, "q", j) for j in tiles]
        se += [("lay_pair", 2, 2)]

        for i in range(1, NB - 1):
            pe += [("flip_pair", i + 1, 0, BRIDGE), ("flip_pair", i + 1, 2)] if i + 1 not in FULL else []
            pe += [("project", i, "k", 0, everything), ("project", i, "k", 1, everything), ("scores", i - 1, 0)]
            pe += [("project", i, "k", 2, everything), ("scores", i - 1, 1), ("project", i, "k", 3, everything)]
            pe += [("project", i, "q", 0, everything), ("scores", i - 1, 2), ("project", i, "q", 1, everything)]
            pe += [("scores", i - 1, 3), ("project", i, "q", 2, everything), ("project", i, "q", 3, everything)]
        for i in range(NB - 2):
            ve += [("quant_k", i)] if i > 0 else []
            ve += [("quant_q", i, 0, 2), ("turn", i + 2, 0) if i + 2 in FULL else ("lay_pair", i + 2, 0)] if i + 2 not in ALONE else [("quant_q", i, 0, 2)]
            ve += [("lay_pair", i + 2, 2)] if i > 0 and i + 2 not in FULL + SHARED + ALONE else []
            ve += [("turn", i + 2, 1)] if i > 0 else []
            ve += [("quant_q", i, 2, 2), ("top", i, 0), ("quant_pass", i + 2, 0), ("top", i, 1)]
            ve += [("turn", i + 2, 1)] if i == 0 else []
            ve += [("top", i, 2), ("quant_pass", i + 2, 1), ("top", i, 3)]
        for i in range(1, NB - 2):
            se += [("lay_h", i, "k", j) for j in tiles] + [("lay_h", i, "q", 0), ("exp", i - 1, 0)]
            se += [("lay_h", i, "q", 1), ("exp", i - 1, 1), ("exp", i - 1, 2), ("lay_h", i, "q", 2)]
            se += [("lay_h", i, "q", 3), ("exp", i - 1, 3)] + ([("lay_pair", i + 2, 0)] if i + 2 in ALONE else [])
            se += [("lay_pair", i + 2, 2)] if i + 2 in SHARED + ALONE else []

        i = NB - 1
        p = NB - 2
        pe += [("project", i, "k", 0, everything), ("project", i, "k", 1, everything), ("scores", p, 0), ("project", i, "k", 2, everything)]
        pe += [("scores", p, 1), ("project", i, "k", 3, everything), ("scores", p, 2), ("project", i, "q", 0, everything)]
        pe += [("scores", p, 3), ("project", i, "q", 1, everything), ("project", i, "q", 2, everything), ("project", i, "q", 3, everything)]
        pe += [("scores", i, 0), ("scores", i, 1), ("scores", i, 2), ("scores", i, 3)]
        ve += [("quant_k", p), ("quant_q", p, 0, 1), ("lay_h", p, "q", 1), ("quant_q", p, 1, 1)]
        ve += [("quant_q", p, 2, 1), ("quant_q", p, 3, 1), ("top", p, 0), ("top", p, 1)]
        ve += [("lay_h", i, "k", 3), ("top", p, 2), ("quant_k", i), ("lay_h", i, "q", 1)]
        ve += [("quant_q", i, 0, 1), ("quant_q", i, 1, 1), ("top", p, 3), ("quant_q", i, 2, 1)]
        ve += [("top", i, 0), ("quant_q", i, 3, 1), ("top", i, 1), ("top", i, 2)]
        ve += [("top", i, 3)]
        se += [("lay_h", p, "k", 0), ("lay_h", p, "k", 1), ("lay_h", p, "k", 2), ("lay_h", p, "k", 3)]
        se += [("exp", p - 1, 0), ("lay_h", p, "q", 0), ("exp", p - 1, 1), ("lay_h", p, "q", 2)]
        se += [("exp", p - 1, 2), ("lay_h", p, "q", 3), ("exp", p - 1, 3), ("lay_h", i, "k", 0)]
        se += [("lay_h", i, "k", 1), ("lay_h", i, "k", 2), ("exp", p, 0), ("lay_h", i, "q", 0)]
        se += [("exp", p, 1), ("lay_h", i, "q", 2), ("lay_h", i, "q", 3), ("exp", p, 2)]
        se += [("exp", p, 3), ("exp", i, 0), ("exp", i, 1), ("exp", i, 2)]
        se += [("exp", i, 3)]

        weave({TENSOR: pe, VECTOR: ve, SCALAR: se})
        finish()
